import numpy as np
import ml_dtypes


def mxq(x, axis, fmt="e4m3"):
    dtype, down = {"e4m3": (ml_dtypes.float8_e4m3fn, 7), "e5m2": (ml_dtypes.float8_e5m2, 14)}[fmt]
    v = np.moveaxis(np.asarray(x, np.float32).astype(ml_dtypes.bfloat16).astype(np.float64), axis, -1)
    blocks = v.reshape(v.shape[:-1] + (-1, 32))
    amax = np.abs(blocks).max(-1, keepdims=True)
    byte = np.maximum(np.where(amax > 0, np.frexp(amax)[1] - 1 + 127, 0) - down, 1)
    scale = np.exp2(byte - 127.0)
    codes = (blocks / scale).astype(np.float32).astype(dtype).astype(np.float64)
    return np.moveaxis((codes * scale).reshape(v.shape), -1, axis)


WIDE = False


def mx_kscale(k):
    if not WIDE:
        return np.ones(k)
    levels = np.array([10, -10, 5, -5, 0])
    a = np.random.permutation(np.resize(levels, k // 512 * 4)).reshape(k // 512, 4)
    idx = np.arange(k)
    return np.exp2(a[idx // 512, idx % 128 // 32])


BF16 = ml_dtypes.bfloat16


def bf(x):
    return np.asarray(x, np.float32).astype(BF16)


def f64(x):
    return np.asarray(x).astype(np.float64)


B, N, DIN, DOUT = 8, 1024, 512, 384
EDGE_P = 0.01


def gcn_norm(adj):
    A = (adj != 0).astype(np.float64)
    A = np.maximum(A, np.eye(A.shape[-1]))
    deg = A.sum(axis=-1)
    dinv = np.where(deg > 0, 1.0 / np.sqrt(np.where(deg > 0, deg, 1.0)), 0.0)
    return dinv[..., :, None] * A * dinv[..., None, :]


def setup_inputs():
    s = mx_kscale(DIN)
    x = np.random.standard_normal((B, N, DIN)) * s
    mask = np.random.random((B, N, N)) < EDGE_P
    wgt = (0.5 + np.random.random((B, N, N))) * np.where(np.random.random((B, N, N)) < 0.5, -1.0, 1.0)
    return {"inputs": bf(x), "adj": bf(mask * wgt),
            "W": bf(np.random.standard_normal((DIN, DOUT)) * 2.0 / np.sqrt(DIN) / s[:, None]),
            "b": bf(np.random.standard_normal(DOUT) * 0.1)}


def reference(inputs, adj, W, b):
    norm = gcn_norm(f64(adj))
    h = mxq(f64(inputs), 2, "e4m3") @ mxq(f64(W), 0, "e4m3")
    agg = mxq(norm, 2, "e4m3") @ mxq(h, 1, "e4m3")
    return np.tanh(agg + f64(b))

@@ -1,0 +1,278 @@
+from contextlib import ExitStack
+
+import concourse.mybir as mybir
+from concourse.masks import make_identity
+
+FLOPS = 2 * 8 * 1024 * 512 * 384 + 2 * 8 * 1024 * 1024 * 384
+
+BF16 = mybir.dt.bfloat16
+F32 = mybir.dt.float32
+I32 = mybir.dt.int32
+U32 = mybir.dt.uint32
+U8 = mybir.dt.uint8
+FP8X4 = mybir.dt.float8_e4m3fn_x4
+ALU = mybir.AluOpType
+ACT = mybir.ActivationFunctionType
+AX = mybir.AxisListType
+
+P = 128
+B = 8
+N = 1024
+DIN = 512
+DOUT = 384
+SEG = 2
+RG = P // SEG
+F = N // SEG
+R = N // RG
+RH = R // 2
+NS = 4 // SEG
+GPB = 256 // RG
+PAD = 8 * RG
+V_SHARE = 3
+
+
+def quantise(nc, flat, codes, scales, widths):
+    col = 0
+    for width in widths:
+        nc.vector.quantize_mx(
+            out=codes[:, col // 4 : (col + width) // 4].bitcast(FP8X4),
+            scales=scales[:, col // 4 : (col + width) // 4],
+            in_=flat[:, col : col + width],
+        )
+        col += width
+
+
+def tile_gcnconvmodule_t_kernel(tc, inputs, adj, W, b, out):
+    nc = tc.nc
+    with ExitStack() as ctx:
+        const = ctx.enter_context(tc.tile_pool(name="const", bufs=1))
+        adjp = ctx.enter_context(tc.tile_pool(name="adjp", bufs=3))
+        work = ctx.enter_context(tc.tile_pool(name="work", bufs=2))
+        small = ctx.enter_context(tc.tile_pool(name="small", bufs=3))
+        psum = ctx.enter_context(tc.psum_pool(name="psum", bufs=2))
+
+        ident_bf = const.tile([P, P], BF16, name="ident_bf")
+        make_identity(nc, ident_bf[:])
+        ident_f = const.tile([P, P], F32, name="ident_f")
+        make_identity(nc, ident_f[:])
+        diag_bits = const.tile([P, SEG, RG], BF16, name="diag_bits")
+        nc.vector.tensor_copy(out=diag_bits[:], in_=ident_bf[:].rearrange("p (c s) -> p s c", s=SEG))
+        grp = const.tile([P, RG], F32, name="grp")
+        nc.vector.tensor_reduce(
+            out=grp[:], in_=ident_f[:].rearrange("p (c s) -> p c s", s=SEG), axis=AX.X, op=ALU.add
+        )
+        pair = const.tile([P, RG, SEG], F32, name="pair")
+        nc.vector.tensor_copy(out=pair[:], in_=grp[:].unsqueeze(2).to_broadcast([P, RG, SEG]))
+        mhalf = const.tile([P, R], F32, name="mhalf")
+        nc.vector.memset(mhalf[:], -0.5)
+
+        w_raw = const.tile([P, 4, DOUT], BF16, name="w_raw")
+        nc.sync.dma_start(
+            out=w_raw[:].rearrange("p (u e) d -> p u (e d)", u=2),
+            in_=W.rearrange("(u p e) d -> p u (e d)", u=2, e=2),
+        )
+        b_bf = const.tile([P, DOUT], BF16, name="b_bf")
+        nc.sync.dma_start(out=b_bf[:], in_=b.partition_broadcast(P))
+        bias = const.tile([P, DOUT], F32, name="bias")
+        nc.vector.tensor_copy(out=bias[:], in_=b_bf[:])
+        w_grp = const.tile([P, DOUT, 4], BF16, name="w_grp", align_bytes=64)
+        nc.vector.tensor_copy(out=w_grp[:], in_=w_raw[:].rearrange("p t d -> p d t"))
+        w_codes = const.tile([P, DOUT], U32, name="w_codes", align_bytes=64)
+        w_scales = const.tile([P, DOUT], U8, name="w_scales", align_bytes=64)
+        quantise(nc, w_grp[:].rearrange("p d t -> p (d t)"), w_codes, w_scales, [1024, 512])
+
+        state = {}
+
+        def load(g):
+            ah = adjp.tile([P, R * F + PAD], BF16, name="ah")
+            rows = adj[g].rearrange("n (s f) -> (n s) f", s=SEG).rearrange("(r p) f -> p r f", p=P)
+            data = ah[:, 0 : R * F].rearrange("p (r f) -> p r f", f=F)
+            for half in range(2):
+                nc.sync.dma_start(
+                    out=data[:, half * RH : (half + 1) * RH, :], in_=rows[:, half * RH : (half + 1) * RH, :]
+                )
+            xt = work.tile([P, 8, DIN], BF16, name="xt")
+            nc.sync.dma_start(out=xt[:], in_=inputs[g].rearrange("(q p) k -> p q k", p=P))
+            state[("ah", g)] = ah
+            state[("xt", g)] = xt
+
+        def first_matmul(g):
+            xt = state[("xt", g)]
+            xt32 = xt[:].bitcast(F32)
+            xg = work.tile([P, N * 4], BF16, name="xg", align_bytes=64)
+            xg32 = xg[:].bitcast(F32).rearrange("p (n u) -> p n u", u=2)
+            for i in range(4):
+                xp = psum.tile([P, 2, 256], F32, name="xp", tag="tp")
+                for u in range(2):
+                    for j in range(2):
+                        nc.tensor.transpose(
+                            out=xp[:, u, j * P : (j + 1) * P],
+                            in_=xt32[:, 2 * i + j, u * P : (u + 1) * P],
+                            identity=ident_f[:],
+                        )
+                nc.scalar.copy(out=xg32[:, i * 256 : (i + 1) * 256, :], in_=xp[:].rearrange("p u n -> p n u"))
+            xw = work.tile([P, N], U32, name="xw", align_bytes=64)
+            xs = work.tile([P, N], U8, name="xs", align_bytes=64)
+            quantise(nc, xg, xw, xs, [4096])
+            hq = work.tile([P, 2, DOUT, 4], BF16, name="hq", align_bytes=64)
+            for g2 in range(2):
+                for dblk in range(3):
+                    hp = psum.tile([P, 4, P], F32, name="hp", tag="hp")
+                    for t in range(4):
+                        q = (F // P) * (t % SEG) + g2 * NS + t // SEG
+                        nc.tensor.matmul_mx(
+                            out=hp[:, t, :],
+                            lhsT=xw[:, q * P : (q + 1) * P].bitcast(FP8X4),
+                            lhsT_scale=xs[:, q * P : (q + 1) * P],
+                            rhs=w_codes[:, dblk * P : (dblk + 1) * P].bitcast(FP8X4),
+                            rhs_scale=w_scales[:, dblk * P : (dblk + 1) * P],
+                            start=True,
+                            stop=True,
+                        )
+                    nc.scalar.copy(
+                        out=hq[:, g2, dblk * P : (dblk + 1) * P, :], in_=hp[:].rearrange("p t d -> p d t")
+                    )
+            hw = small.tile([P, 2 * DOUT], U32, name="hw", align_bytes=64)
+            hs = small.tile([P, 2 * DOUT], U8, name="hs", align_bytes=64)
+            quantise(nc, hq[:].rearrange("p g d t -> p (g d t)"), hw, hs, [2048, 1024])
+            state[("hw", g)] = hw
+            state[("hs", g)] = hs
+
+        def degrees(g):
+            ah = state[("ah", g)]
+            ah32 = ah[:].bitcast(I32)
+            d32 = diag_bits[:].bitcast(I32)
+            step = (F + RG) // 2
+            for s in range(SEG):
+                base = 8 * s * (F // 2)
+                view = ah32[:, base : base + 8 * step].rearrange("p (i w) -> p i w", w=step)[:, :, 0 : RG // 2]
+                nc.vector.tensor_tensor(
+                    out=view,
+                    in0=view,
+                    in1=d32[:, s, :].unsqueeze(1).to_broadcast([P, 8, RG // 2]),
+                    op=ALU.bitwise_or,
+                )
+            data = ah[:, 0 : R * F].rearrange("p (r f) -> p r f", f=F)
+            part = small.tile([P, R], F32, name="part")
+            for r in range(R):
+                nc.vector.tensor_scalar(
+                    out=data[:, r, :],
+                    in0=data[:, r, :],
+                    scalar1=0.0,
+                    scalar2=None,
+                    op0=ALU.not_equal,
+                    op1=ALU.add,
+                    accum_out=part[:, r : r + 1],
+                )
+            degp = psum.tile([P, R], F32, name="degp", tag="tp")
+            nc.tensor.matmul(
+                out=degp[:], lhsT=pair[:].rearrange("p c s -> p (c s)"), rhs=part[:], start=True, stop=True
+            )
+            deg = small.tile([P, R], F32, name="deg")
+            nc.scalar.copy(out=deg[:], in_=degp[:])
+            dn = small.tile([P, R], F32, name="dn")
+            nc.gpsimd.tensor_tensor(out=dn[:], in0=deg[:], in1=mhalf[:], op=ALU.pow)
+            rr = work.tile([P, 8, RG, SEG], F32, name="rr")
+            nc.gpsimd.tensor_scalar(
+                out=rr[:],
+                in0=dn[:].rearrange("p (s a) -> p a s", s=SEG).unsqueeze(2).to_broadcast([P, 8, RG, SEG]),
+                scalar1=1.0,
+                scalar2=0.0,
+                op0=ALU.mult,
+                op1=ALU.add,
+            )
+            db = small.tile([P, F], F32, name="db")
+            for h in range(2):
+                dbp = psum.tile([P, 4, P], F32, name="dbp", tag="tp")
+                for a4 in range(4):
+                    nc.tensor.transpose(
+                        out=dbp[:, a4, :],
+                        in_=rr[:, 4 * h + a4, :, :].rearrange("p c s -> p (c s)"),
+                        identity=ident_f[:],
+                    )
+                nc.scalar.copy(
+                    out=db[:, 4 * h * RG : (4 * h + 4) * RG].rearrange("p (a c) -> p a c", c=RG),
+                    in_=dbp[:].rearrange("p a (c s) -> p a c s", s=SEG)[:, :, :, 0],
+                )
+            state[("dn", g)] = dn
+            state[("db", g)] = db
+
+        def aggregate(g, half):
+            ah = state[("ah", g)]
+            dn = state[("dn", g)]
+            db = state[("db", g)]
+            hw = state[("hw", g)]
+            hs = state[("hs", g)]
+            data = ah[:, 0 : R * F].rearrange("p (r f) -> p r f", f=F)
+            r0 = half * RH
+            gt = work.tile([P, RH, F], BF16, name="gt")
+            for k in range(RH):
+                if k < V_SHARE:
+                    nc.vector.tensor_scalar(
+                        out=gt[:, k, :],
+                        in0=db[:],
+                        scalar1=dn[:, r0 + k : r0 + k + 1],
+                        scalar2=None,
+                        op0=ALU.mult,
+                    )
+                else:
+                    nc.scalar.activation(
+                        out=gt[:, k, :], in_=db[:], func=ACT.Copy, scale=dn[:, r0 + k : r0 + k + 1]
+                    )
+            nc.vector.tensor_tensor(
+                out=data[:, r0 : r0 + RH, :], in0=data[:, r0 : r0 + RH, :], in1=gt[:], op=ALU.mult
+            )
+            codes = []
+            for g2 in range(2):
+                nt = work.tile([P, 2048], BF16, name="nt", align_bytes=64)
+                for bk in range(2):
+                    npt = psum.tile([P, 1024], BF16, name="npt", tag="np")
+                    for k in range(GPB):
+                        r = r0 + bk * GPB + k
+                        for sg in range(NS):
+                            col = P * (g2 * NS + sg)
+                            nc.tensor.transpose(
+                                out=npt[:, k * RG * 4 : (k + 1) * RG * 4].rearrange(
+                                    "p (c s t) -> p c s t", s=NS, t=SEG
+                                )[:, :, sg, :],
+                                in_=data[:, r, col : col + P],
+                                identity=ident_bf[:],
+                            )
+                    nc.scalar.copy(out=nt[:, bk * 1024 : (bk + 1) * 1024], in_=npt[:])
+                ntw = work.tile([P, 512], U32, name="ntw", align_bytes=64, bufs=4)
+                nts = work.tile([P, 512], U8, name="nts", align_bytes=64, bufs=4)
+                quantise(nc, nt, ntw, nts, [2048])
+                codes.append((ntw, nts))
+            ot = work.tile([P, 4, DOUT], F32, name="ot", bufs=3)
+            for c in range(4):
+                acc = psum.tile([P, DOUT], F32, name="acc", tag="ap")
+                for lo, hi in ((0, 256), (256, 384)):
+                    for g2 in range(2):
+                        ntw, nts = codes[g2]
+                        nc.tensor.matmul_mx(
+                            out=acc[:, lo:hi],
+                            lhsT=ntw[:, c * P : (c + 1) * P].bitcast(FP8X4),
+                            lhsT_scale=nts[:, c * P : (c + 1) * P],
+                            rhs=hw[:, g2 * DOUT + lo : g2 * DOUT + hi].bitcast(FP8X4),
+                            rhs_scale=hs[:, g2 * DOUT + lo : g2 * DOUT + hi],
+                            start=(g2 == 0),
+                            stop=(g2 == 1),
+                        )
+                nc.vector.tensor_tensor(out=ot[:, c, :], in0=acc[:], in1=bias[:], op=ALU.add)
+            nc.scalar.activation(out=ot[:], in_=ot[:], func=ACT.Tanh)
+            nc.sync.dma_start(
+                out=out[g, half * 512 : (half + 1) * 512, :].rearrange("(c p) d -> p c d", p=P), in_=ot[:]
+            )
+
+        load(0)
+        load(1)
+        first_matmul(0)
+        degrees(0)
+        for g in range(B):
+            if g + 2 < B:
+                load(g + 2)
+            if g + 1 < B:
+                first_matmul(g + 1)
+                degrees(g + 1)
+            aggregate(g, 0)
+            aggregate(g, 1)

@@ -28,7 +28,7 @@ RH = R // 2
 NS = 4 // SEG
 GPB = 256 // RG
 PAD = 8 * RG
-V_SHARE = 3
+V_SHARE = 4
 
 
 def quantise(nc, flat, codes, scales, widths):
@@ -46,11 +46,12 @@ def tile_gcnconvmodule_t_kernel(tc, inputs, adj, W, b, out):
     nc = tc.nc
     with ExitStack() as ctx:
         const = ctx.enter_context(tc.tile_pool(name="const", bufs=1))
-        adjp = ctx.enter_context(tc.tile_pool(name="adjp", bufs=3))
+        adjp = ctx.enter_context(tc.tile_pool(name="adjp", bufs=4))
         work = ctx.enter_context(tc.tile_pool(name="work", bufs=2))
         small = ctx.enter_context(tc.tile_pool(name="small", bufs=3))
         psum = ctx.enter_context(tc.psum_pool(name="psum", bufs=2))
 
+        ctx.enter_context(tc.manual_schedule())
         ident_bf = const.tile([P, P], BF16, name="ident_bf")
         make_identity(nc, ident_bf[:])
         ident_f = const.tile([P, P], F32, name="ident_f")
@@ -81,92 +82,110 @@ def tile_gcnconvmodule_t_kernel(tc, inputs, adj, W, b, out):
         w_scales = const.tile([P, DOUT], U8, name="w_scales", align_bytes=64)
         quantise(nc, w_grp[:].rearrange("p d t -> p (d t)"), w_codes, w_scales, [1024, 512])
 
-        state = {}
+        st = {}
 
-        def load(g):
-            ah = adjp.tile([P, R * F + PAD], BF16, name="ah")
+        def adj_view(g):
+            return st[("ah", g)][:, 0 : R * F].rearrange("p (r f) -> p r f", f=F)
+
+        def load_adj(g):
+            st[("ah", g)] = adjp.tile([P, R * F + PAD], BF16, name="ah")
             rows = adj[g].rearrange("n (s f) -> (n s) f", s=SEG).rearrange("(r p) f -> p r f", p=P)
-            data = ah[:, 0 : R * F].rearrange("p (r f) -> p r f", f=F)
+            data = adj_view(g)
             for half in range(2):
                 nc.sync.dma_start(
                     out=data[:, half * RH : (half + 1) * RH, :], in_=rows[:, half * RH : (half + 1) * RH, :]
                 )
-            xt = work.tile([P, 8, DIN], BF16, name="xt")
-            nc.sync.dma_start(out=xt[:], in_=inputs[g].rearrange("(q p) k -> p q k", p=P))
-            state[("ah", g)] = ah
-            state[("xt", g)] = xt
 
-        def first_matmul(g):
-            xt = state[("xt", g)]
-            xt32 = xt[:].bitcast(F32)
-            xg = work.tile([P, N * 4], BF16, name="xg", align_bytes=64)
-            xg32 = xg[:].bitcast(F32).rearrange("p (n u) -> p n u", u=2)
-            for i in range(4):
-                xp = psum.tile([P, 2, 256], F32, name="xp", tag="tp")
-                for u in range(2):
-                    for j in range(2):
-                        nc.tensor.transpose(
-                            out=xp[:, u, j * P : (j + 1) * P],
-                            in_=xt32[:, 2 * i + j, u * P : (u + 1) * P],
-                            identity=ident_f[:],
-                        )
-                nc.scalar.copy(out=xg32[:, i * 256 : (i + 1) * 256, :], in_=xp[:].rearrange("p u n -> p n u"))
+        def load_x(g):
+            xt = work.tile([P, 8, DIN], BF16, name="xt")
+            st[("xt", g)] = xt
+            nc.sync.dma_start(out=xt[:], in_=inputs[g].rearrange("(q p) k -> p q k", p=P))
+
+        def x_transpose(g, i):
+            if i == 0:
+                st[("xg", g)] = work.tile([P, N * 4], BF16, name="xg", align_bytes=64)
+            xt32 = st[("xt", g)][:].bitcast(F32)
+            xg32 = st[("xg", g)][:].bitcast(F32).rearrange("p (n u) -> p n u", u=2)
+            xp = psum.tile([P, 2, 256], F32, name="xp", tag="tp")
+            for u in range(2):
+                for j in range(2):
+                    nc.tensor.transpose(
+                        out=xp[:, u, j * P : (j + 1) * P],
+                        in_=xt32[:, 2 * i + j, u * P : (u + 1) * P],
+                        identity=ident_f[:],
+                    )
+            nc.scalar.copy(out=xg32[:, i * 256 : (i + 1) * 256, :], in_=xp[:].rearrange("p u n -> p n u"))
+
+        def x_quantise(g):
             xw = work.tile([P, N], U32, name="xw", align_bytes=64)
             xs = work.tile([P, N], U8, name="xs", align_bytes=64)
-            quantise(nc, xg, xw, xs, [4096])
-            hq = work.tile([P, 2, DOUT, 4], BF16, name="hq", align_bytes=64)
-            for g2 in range(2):
-                for dblk in range(3):
-                    hp = psum.tile([P, 4, P], F32, name="hp", tag="hp")
-                    for t in range(4):
-                        q = (F // P) * (t % SEG) + g2 * NS + t // SEG
-                        nc.tensor.matmul_mx(
-                            out=hp[:, t, :],
-                            lhsT=xw[:, q * P : (q + 1) * P].bitcast(FP8X4),
-                            lhsT_scale=xs[:, q * P : (q + 1) * P],
-                            rhs=w_codes[:, dblk * P : (dblk + 1) * P].bitcast(FP8X4),
-                            rhs_scale=w_scales[:, dblk * P : (dblk + 1) * P],
-                            start=True,
-                            stop=True,
-                        )
-                    nc.scalar.copy(
-                        out=hq[:, g2, dblk * P : (dblk + 1) * P, :], in_=hp[:].rearrange("p t d -> p d t")
-                    )
+            quantise(nc, st[("xg", g)], xw, xs, [2048, 2048])
+            st[("xw", g)] = xw
+            st[("xs", g)] = xs
+
+        def h_matmul(g, g2, dblk):
+            if g2 == 0 and dblk == 0:
+                st[("hq", g)] = work.tile([P, 2, DOUT, 4], BF16, name="hq", align_bytes=64)
+            xw = st[("xw", g)]
+            xs = st[("xs", g)]
+            hp = psum.tile([P, 4, P], F32, name="hp", tag="hp")
+            for t in range(4):
+                q = (F // P) * (t % SEG) + g2 * NS + t // SEG
+                nc.tensor.matmul_mx(
+                    out=hp[:, t, :],
+                    lhsT=xw[:, q * P : (q + 1) * P].bitcast(FP8X4),
+                    lhsT_scale=xs[:, q * P : (q + 1) * P],
+                    rhs=w_codes[:, dblk * P : (dblk + 1) * P].bitcast(FP8X4),
+                    rhs_scale=w_scales[:, dblk * P : (dblk + 1) * P],
+                    start=True,
+                    stop=True,
+                )
+            nc.scalar.copy(
+                out=st[("hq", g)][:, g2, dblk * P : (dblk + 1) * P, :], in_=hp[:].rearrange("p t d -> p d t")
+            )
+
+        def h_quantise(g):
             hw = small.tile([P, 2 * DOUT], U32, name="hw", align_bytes=64)
             hs = small.tile([P, 2 * DOUT], U8, name="hs", align_bytes=64)
-            quantise(nc, hq[:].rearrange("p g d t -> p (g d t)"), hw, hs, [2048, 1024])
-            state[("hw", g)] = hw
-            state[("hs", g)] = hs
+            quantise(nc, st[("hq", g)][:].rearrange("p g d t -> p (g d t)"), hw, hs, [2048, 1024])
+            st[("hw", g)] = hw
+            st[("hs", g)] = hs
 
-        def degrees(g):
-            ah = state[("ah", g)]
-            ah32 = ah[:].bitcast(I32)
+        def diag_or(g, s):
+            ah32 = st[("ah", g)][:].bitcast(I32)
             d32 = diag_bits[:].bitcast(I32)
             step = (F + RG) // 2
-            for s in range(SEG):
-                base = 8 * s * (F // 2)
-                view = ah32[:, base : base + 8 * step].rearrange("p (i w) -> p i w", w=step)[:, :, 0 : RG // 2]
-                nc.vector.tensor_tensor(
-                    out=view,
-                    in0=view,
-                    in1=d32[:, s, :].unsqueeze(1).to_broadcast([P, 8, RG // 2]),
-                    op=ALU.bitwise_or,
-                )
-            data = ah[:, 0 : R * F].rearrange("p (r f) -> p r f", f=F)
-            part = small.tile([P, R], F32, name="part")
-            for r in range(R):
-                nc.vector.tensor_scalar(
-                    out=data[:, r, :],
-                    in0=data[:, r, :],
-                    scalar1=0.0,
-                    scalar2=None,
-                    op0=ALU.not_equal,
-                    op1=ALU.add,
-                    accum_out=part[:, r : r + 1],
-                )
+            base = 8 * s * (F // 2)
+            view = ah32[:, base : base + 8 * step].rearrange("p (i w) -> p i w", w=step)[:, :, 0 : RG // 2]
+            nc.vector.tensor_tensor(
+                out=view,
+                in0=view,
+                in1=d32[:, s, :].unsqueeze(1).to_broadcast([P, 8, RG // 2]),
+                op=ALU.bitwise_or,
+            )
+
+        def count(g, r):
+            if r == 0:
+                st[("part", g)] = small.tile([P, R], F32, name="part")
+            data = adj_view(g)
+            nc.vector.tensor_scalar(
+                out=data[:, r, :],
+                in0=data[:, r, :],
+                scalar1=0.0,
+                scalar2=None,
+                op0=ALU.not_equal,
+                op1=ALU.add,
+                accum_out=st[("part", g)][:, r : r + 1],
+            )
+
+        def deg_a(g):
             degp = psum.tile([P, R], F32, name="degp", tag="tp")
             nc.tensor.matmul(
-                out=degp[:], lhsT=pair[:].rearrange("p c s -> p (c s)"), rhs=part[:], start=True, stop=True
+                out=degp[:],
+                lhsT=pair[:].rearrange("p c s -> p (c s)"),
+                rhs=st[("part", g)][:],
+                start=True,
+                stop=True,
             )
             deg = small.tile([P, R], F32, name="deg")
             nc.scalar.copy(out=deg[:], in_=degp[:])
@@ -181,6 +200,11 @@ def tile_gcnconvmodule_t_kernel(tc, inputs, adj, W, b, out):
                 op0=ALU.mult,
                 op1=ALU.add,
             )
+            st[("dn", g)] = dn
+            st[("rr", g)] = rr
+
+        def deg_b(g):
+            rr = st[("rr", g)]
             db = small.tile([P, F], F32, name="db")
             for h in range(2):
                 dbp = psum.tile([P, 4, P], F32, name="dbp", tag="tp")
@@ -194,18 +218,15 @@ def tile_gcnconvmodule_t_kernel(tc, inputs, adj, W, b, out):
                     out=db[:, 4 * h * RG : (4 * h + 4) * RG].rearrange("p (a c) -> p a c", c=RG),
                     in_=dbp[:].rearrange("p a (c s) -> p a c s", s=SEG)[:, :, :, 0],
                 )
-            state[("dn", g)] = dn
-            state[("db", g)] = db
+            st[("db", g)] = db
 
-        def aggregate(g, half):
-            ah = state[("ah", g)]
-            dn = state[("dn", g)]
-            db = state[("db", g)]
-            hw = state[("hw", g)]
-            hs = state[("hs", g)]
-            data = ah[:, 0 : R * F].rearrange("p (r f) -> p r f", f=F)
-            r0 = half * RH
+        def outer(u):
+            g = u // 2
+            r0 = (u % 2) * RH
+            dn = st[("dn", g)]
+            db = st[("db", g)]
             gt = work.tile([P, RH, F], BF16, name="gt")
+            st[("gt", u)] = gt
             for k in range(RH):
                 if k < V_SHARE:
                     nc.vector.tensor_scalar(
@@ -219,60 +240,120 @@ def tile_gcnconvmodule_t_kernel(tc, inputs, adj, W, b, out):
                     nc.scalar.activation(
                         out=gt[:, k, :], in_=db[:], func=ACT.Copy, scale=dn[:, r0 + k : r0 + k + 1]
                     )
+
+        def mask(u, bk):
+            data = adj_view(u // 2)
+            r0 = (u % 2) * RH + bk * GPB
             nc.vector.tensor_tensor(
-                out=data[:, r0 : r0 + RH, :], in0=data[:, r0 : r0 + RH, :], in1=gt[:], op=ALU.mult
-            )
-            codes = []
-            for g2 in range(2):
-                nt = work.tile([P, 2048], BF16, name="nt", align_bytes=64)
-                for bk in range(2):
-                    npt = psum.tile([P, 1024], BF16, name="npt", tag="np")
-                    for k in range(GPB):
-                        r = r0 + bk * GPB + k
-                        for sg in range(NS):
-                            col = P * (g2 * NS + sg)
-                            nc.tensor.transpose(
-                                out=npt[:, k * RG * 4 : (k + 1) * RG * 4].rearrange(
-                                    "p (c s t) -> p c s t", s=NS, t=SEG
-                                )[:, :, sg, :],
-                                in_=data[:, r, col : col + P],
-                                identity=ident_bf[:],
-                            )
-                    nc.scalar.copy(out=nt[:, bk * 1024 : (bk + 1) * 1024], in_=npt[:])
-                ntw = work.tile([P, 512], U32, name="ntw", align_bytes=64, bufs=4)
-                nts = work.tile([P, 512], U8, name="nts", align_bytes=64, bufs=4)
-                quantise(nc, nt, ntw, nts, [2048])
-                codes.append((ntw, nts))
-            ot = work.tile([P, 4, DOUT], F32, name="ot", bufs=3)
-            for c in range(4):
-                acc = psum.tile([P, DOUT], F32, name="acc", tag="ap")
-                for lo, hi in ((0, 256), (256, 384)):
-                    for g2 in range(2):
-                        ntw, nts = codes[g2]
-                        nc.tensor.matmul_mx(
-                            out=acc[:, lo:hi],
-                            lhsT=ntw[:, c * P : (c + 1) * P].bitcast(FP8X4),
-                            lhsT_scale=nts[:, c * P : (c + 1) * P],
-                            rhs=hw[:, g2 * DOUT + lo : g2 * DOUT + hi].bitcast(FP8X4),
-                            rhs_scale=hs[:, g2 * DOUT + lo : g2 * DOUT + hi],
-                            start=(g2 == 0),
-                            stop=(g2 == 1),
-                        )
-                nc.vector.tensor_tensor(out=ot[:, c, :], in0=acc[:], in1=bias[:], op=ALU.add)
-            nc.scalar.activation(out=ot[:], in_=ot[:], func=ACT.Tanh)
-            nc.sync.dma_start(
-                out=out[g, half * 512 : (half + 1) * 512, :].rearrange("(c p) d -> p c d", p=P), in_=ot[:]
+                out=data[:, r0 : r0 + GPB, :],
+                in0=data[:, r0 : r0 + GPB, :],
+                in1=st[("gt", u)][:, bk * GPB : (bk + 1) * GPB, :],
+                op=ALU.mult,
             )
 
-        load(0)
-        load(1)
-        first_matmul(0)
-        degrees(0)
-        for g in range(B):
-            if g + 2 < B:
-                load(g + 2)
-            if g + 1 < B:
-                first_matmul(g + 1)
-                degrees(g + 1)
-            aggregate(g, 0)
-            aggregate(g, 1)
+        def n_transpose(u, g2, bk):
+            if bk == 0:
+                st[("nt", u, g2)] = work.tile([P, 2048], BF16, name="nt", align_bytes=64, bufs=4)
+            data = adj_view(u // 2)
+            npt = psum.tile([P, 1024], BF16, name="npt", tag="np")
+            for k in range(GPB):
+                r = (u % 2) * RH + bk * GPB + k
+                for sg in range(NS):
+                    col = P * (g2 * NS + sg)
+                    nc.tensor.transpose(
+                        out=npt[:, k * RG * 4 : (k + 1) * RG * 4].rearrange("p (c s t) -> p c s t", s=NS, t=SEG)[
+                            :, :, sg, :
+                        ],
+                        in_=data[:, r, col : col + P],
+                        identity=ident_bf[:],
+                    )
+            nc.scalar.copy(out=st[("nt", u, g2)][:, bk * 1024 : (bk + 1) * 1024], in_=npt[:])
+
+        def n_quantise(u, g2):
+            ntw = work.tile([P, 512], U32, name="ntw", align_bytes=64, bufs=4)
+            nts = work.tile([P, 512], U8, name="nts", align_bytes=64, bufs=4)
+            quantise(nc, st[("nt", u, g2)], ntw, nts, [2048])
+            st[("ntw", u, g2)] = ntw
+            st[("nts", u, g2)] = nts
+
+        def agg(u, c):
+            if c == 0:
+                st[("ot", u)] = work.tile([P, 4, DOUT], F32, name="ot", bufs=3)
+            hw = st[("hw", u // 2)]
+            hs = st[("hs", u // 2)]
+            acc = psum.tile([P, DOUT], F32, name="acc", tag="ap")
+            for lo, hi in ((0, 256), (256, 384)):
+                for g2 in range(2):
+                    nc.tensor.matmul_mx(
+                        out=acc[:, lo:hi],
+                        lhsT=st[("ntw", u, g2)][:, c * P : (c + 1) * P].bitcast(FP8X4),
+                        lhsT_scale=st[("nts", u, g2)][:, c * P : (c + 1) * P],
+                        rhs=hw[:, g2 * DOUT + lo : g2 * DOUT + hi].bitcast(FP8X4),
+                        rhs_scale=hs[:, g2 * DOUT + lo : g2 * DOUT + hi],
+                        start=(g2 == 0),
+                        stop=(g2 == 1),
+                    )
+            nc.vector.tensor_tensor(out=st[("ot", u)][:, c, :], in0=acc[:], in1=bias[:], op=ALU.add)
+
+        def finish(u):
+            ot = st[("ot", u)]
+            nc.scalar.activation(out=ot[:], in_=ot[:], func=ACT.Tanh)
+            nc.sync.dma_start(
+                out=out[u // 2, (u % 2) * 512 : (u % 2 + 1) * 512, :].rearrange("(c p) d -> p c d", p=P),
+                in_=ot[:],
+            )
+
+        U = 2 * B
+
+        def okg(g):
+            return 0 <= g < B
+
+        def oku(u):
+            return 0 <= u < U
+
+        for k in range(-7, U + 2):
+            if oku(k - 2):
+                finish(k - 2)
+            for bk in range(2):
+                if oku(k):
+                    mask(k, bk)
+                if oku(k - 1):
+                    agg(k - 1, 2 * bk)
+                    agg(k - 1, 2 * bk + 1)
+                if oku(k):
+                    n_transpose(k, 0, bk)
+                    n_transpose(k, 1, bk)
+            if k % 2 == 0:
+                ga = (k + 2) // 2
+                if okg(ga):
+                    for g2 in range(2):
+                        for dblk in range(3):
+                            h_matmul(ga, g2, dblk)
+                    diag_or(ga, 1)
+                    for r in range(RH, R):
+                        count(ga, r)
+                    deg_a(ga)
+                if okg((k + 4) // 2):
+                    x_quantise((k + 4) // 2)
+            else:
+                if okg((k + 1) // 2):
+                    deg_b((k + 1) // 2)
+                gb = (k + 3) // 2
+                if okg(gb):
+                    diag_or(gb, 0)
+                    for r in range(RH):
+                        count(gb, r)
+                if okg((k + 1) // 2):
+                    h_quantise((k + 1) // 2)
+                if okg((k + 5) // 2):
+                    for i in range(4):
+                        x_transpose((k + 5) // 2, i)
+                if okg((k + 5) // 2):
+                    load_adj((k + 5) // 2)
+                if okg((k + 7) // 2):
+                    load_x((k + 7) // 2)
+            if oku(k):
+                n_quantise(k, 0)
+                n_quantise(k, 1)
+            if oku(k + 1):
+                outer(k + 1)

@@ -28,7 +28,7 @@ RH = R // 2
 NS = 4 // SEG
 GPB = 256 // RG
 PAD = 8 * RG
-V_SHARE = 4
+V_SHARE = 8
 
 
 def quantise(nc, flat, codes, scales, widths):

@@ -29,6 +29,8 @@ NS = 4 // SEG
 GPB = 256 // RG
 PAD = 8 * RG
 V_SHARE = 8
+FE_ON_V = ()
+LEVELS = 4
 
 
 def quantise(nc, flat, codes, scales, widths):
@@ -50,37 +52,7 @@ def tile_gcnconvmodule_t_kernel(tc, inputs, adj, W, b, out):
         work = ctx.enter_context(tc.tile_pool(name="work", bufs=2))
         small = ctx.enter_context(tc.tile_pool(name="small", bufs=3))
         psum = ctx.enter_context(tc.psum_pool(name="psum", bufs=2))
-
         ctx.enter_context(tc.manual_schedule())
-        ident_bf = const.tile([P, P], BF16, name="ident_bf")
-        make_identity(nc, ident_bf[:])
-        ident_f = const.tile([P, P], F32, name="ident_f")
-        make_identity(nc, ident_f[:])
-        diag_bits = const.tile([P, SEG, RG], BF16, name="diag_bits")
-        nc.vector.tensor_copy(out=diag_bits[:], in_=ident_bf[:].rearrange("p (c s) -> p s c", s=SEG))
-        grp = const.tile([P, RG], F32, name="grp")
-        nc.vector.tensor_reduce(
-            out=grp[:], in_=ident_f[:].rearrange("p (c s) -> p c s", s=SEG), axis=AX.X, op=ALU.add
-        )
-        pair = const.tile([P, RG, SEG], F32, name="pair")
-        nc.vector.tensor_copy(out=pair[:], in_=grp[:].unsqueeze(2).to_broadcast([P, RG, SEG]))
-        mhalf = const.tile([P, R], F32, name="mhalf")
-        nc.vector.memset(mhalf[:], -0.5)
-
-        w_raw = const.tile([P, 4, DOUT], BF16, name="w_raw")
-        nc.sync.dma_start(
-            out=w_raw[:].rearrange("p (u e) d -> p u (e d)", u=2),
-            in_=W.rearrange("(u p e) d -> p u (e d)", u=2, e=2),
-        )
-        b_bf = const.tile([P, DOUT], BF16, name="b_bf")
-        nc.sync.dma_start(out=b_bf[:], in_=b.partition_broadcast(P))
-        bias = const.tile([P, DOUT], F32, name="bias")
-        nc.vector.tensor_copy(out=bias[:], in_=b_bf[:])
-        w_grp = const.tile([P, DOUT, 4], BF16, name="w_grp", align_bytes=64)
-        nc.vector.tensor_copy(out=w_grp[:], in_=w_raw[:].rearrange("p t d -> p d t"))
-        w_codes = const.tile([P, DOUT], U32, name="w_codes", align_bytes=64)
-        w_scales = const.tile([P, DOUT], U8, name="w_scales", align_bytes=64)
-        quantise(nc, w_grp[:].rearrange("p d t -> p (d t)"), w_codes, w_scales, [1024, 512])
 
         st = {}
 
@@ -101,6 +73,42 @@ def tile_gcnconvmodule_t_kernel(tc, inputs, adj, W, b, out):
             st[("xt", g)] = xt
             nc.sync.dma_start(out=xt[:], in_=inputs[g].rearrange("(q p) k -> p q k", p=P))
 
+        load_x(0)
+        load_adj(0)
+
+        ident_bf = const.tile([P, P], BF16, name="ident_bf")
+        make_identity(nc, ident_bf[:])
+        ident_f = const.tile([P, P], F32, name="ident_f")
+        make_identity(nc, ident_f[:])
+        diag_bits = const.tile([P, SEG, RG], BF16, name="diag_bits")
+        nc.vector.tensor_copy(out=diag_bits[:], in_=ident_bf[:].rearrange("p (c s) -> p s c", s=SEG))
+        grp = const.tile([P, RG], F32, name="grp")
+        nc.vector.tensor_reduce(
+            out=grp[:], in_=ident_f[:].rearrange("p (c s) -> p c s", s=SEG), axis=AX.X, op=ALU.add
+        )
+        pair = const.tile([P, RG, SEG], F32, name="pair")
+        nc.vector.tensor_copy(out=pair[:], in_=grp[:].unsqueeze(2).to_broadcast([P, RG, SEG]))
+        mhalf = const.tile([P, R], F32, name="mhalf")
+        nc.vector.memset(mhalf[:], -0.5)
+
+        w_raw = work.tile([P, 4, DOUT], BF16, name="w_raw", tag="ot")
+        nc.sync.dma_start(
+            out=w_raw[:].rearrange("p (u e) d -> p u (e d)", u=2),
+            in_=W.rearrange("(u p e) d -> p u (e d)", u=2, e=2),
+        )
+        b_rows = const.tile([P, P], BF16, name="b_rows")
+        nc.vector.memset(b_rows[:], 0.0)
+        nc.sync.dma_start(out=b_rows[0:3, :], in_=b.rearrange("(r c) -> r c", c=P))
+        bp = psum.tile([P, P], BF16, name="bp", tag="tp")
+        nc.tensor.transpose(out=bp[:], in_=b_rows[:], identity=ident_bf[:])
+        bcol = const.tile([P, 3], F32, name="bcol")
+        nc.vector.tensor_copy(out=bcol[:], in_=bp[:, 0:3])
+        w_grp = work.tile([P, DOUT, 4], BF16, name="w_grp", tag="tt", align_bytes=64)
+        nc.vector.tensor_copy(out=w_grp[:], in_=w_raw[:].rearrange("p t d -> p d t"))
+        w_codes = const.tile([P, DOUT], U32, name="w_codes", align_bytes=64)
+        w_scales = const.tile([P, DOUT], U8, name="w_scales", align_bytes=64)
+        quantise(nc, w_grp[:].rearrange("p d t -> p (d t)"), w_codes, w_scales, [1024, 512])
+
         def x_transpose(g, i):
             if i == 0:
                 st[("xg", g)] = work.tile([P, N * 4], BF16, name="xg", align_bytes=64)
@@ -119,7 +127,7 @@ def tile_gcnconvmodule_t_kernel(tc, inputs, adj, W, b, out):
         def x_quantise(g):
             xw = work.tile([P, N], U32, name="xw", align_bytes=64)
             xs = work.tile([P, N], U8, name="xs", align_bytes=64)
-            quantise(nc, st[("xg", g)], xw, xs, [2048, 2048])
+            quantise(nc, st[("xg", g)], xw, xs, [4096])
             st[("xw", g)] = xw
             st[("xs", g)] = xs
 
@@ -128,7 +136,7 @@ def tile_gcnconvmodule_t_kernel(tc, inputs, adj, W, b, out):
                 st[("hq", g)] = work.tile([P, 2, DOUT, 4], BF16, name="hq", align_bytes=64)
             xw = st[("xw", g)]
             xs = st[("xs", g)]
-            hp = psum.tile([P, 4, P], F32, name="hp", tag="hp")
+            hp = psum.tile([P, 4, P], F32, name="hp", tag="tp")
             for t in range(4):
                 q = (F // P) * (t % SEG) + g2 * NS + t // SEG
                 nc.tensor.matmul_mx(
@@ -151,7 +159,7 @@ def tile_gcnconvmodule_t_kernel(tc, inputs, adj, W, b, out):
             st[("hw", g)] = hw
             st[("hs", g)] = hs
 
-        def diag_or(g, s):
+        def diag_one(g, s):
             ah32 = st[("ah", g)][:].bitcast(I32)
             d32 = diag_bits[:].bitcast(I32)
             step = (F + RG) // 2
@@ -164,19 +172,30 @@ def tile_gcnconvmodule_t_kernel(tc, inputs, adj, W, b, out):
                 op=ALU.bitwise_or,
             )
 
-        def count(g, r):
-            if r == 0:
-                st[("part", g)] = small.tile([P, R], F32, name="part")
+        def to_mask(g):
             data = adj_view(g)
-            nc.vector.tensor_scalar(
-                out=data[:, r, :],
-                in0=data[:, r, :],
-                scalar1=0.0,
-                scalar2=None,
-                op0=ALU.not_equal,
-                op1=ALU.add,
-                accum_out=st[("part", g)][:, r : r + 1],
+            nc.vector.tensor_scalar(out=data, in0=data, scalar1=0.0, scalar2=None, op0=ALU.not_equal)
+
+        def fold(g, lv):
+            data = adj_view(g)
+            width = F >> (lv + 1)
+            if lv == 0:
+                st[("tree", g)] = work.tile([P, R, F // 2], BF16, name="tree", bufs=1)
+                nc.vector.tensor_tensor(
+                    out=st[("tree", g)][:], in0=data[:, :, 0:width], in1=data[:, :, width : 2 * width], op=ALU.add
+                )
+            else:
+                tree = st[("tree", g)]
+                nc.vector.tensor_tensor(
+                    out=tree[:, :, 0:width], in0=tree[:, :, 0:width], in1=tree[:, :, width : 2 * width], op=ALU.add
+                )
+
+        def fold_end(g):
+            part = small.tile([P, R], F32, name="part")
+            nc.vector.tensor_reduce(
+                out=part[:], in_=st[("tree", g)][:, :, 0 : F >> LEVELS], axis=AX.X, op=ALU.add
             )
+            st[("part", g)] = part
 
         def deg_a(g):
             degp = psum.tile([P, R], F32, name="degp", tag="tp")
@@ -191,7 +210,7 @@ def tile_gcnconvmodule_t_kernel(tc, inputs, adj, W, b, out):
             nc.scalar.copy(out=deg[:], in_=degp[:])
             dn = small.tile([P, R], F32, name="dn")
             nc.gpsimd.tensor_tensor(out=dn[:], in0=deg[:], in1=mhalf[:], op=ALU.pow)
-            rr = work.tile([P, 8, RG, SEG], F32, name="rr")
+            rr = work.tile([P, 8, RG, SEG], F32, name="rr", bufs=1)
             nc.gpsimd.tensor_scalar(
                 out=rr[:],
                 in0=dn[:].rearrange("p (s a) -> p a s", s=SEG).unsqueeze(2).to_broadcast([P, 8, RG, SEG]),
@@ -220,40 +239,35 @@ def tile_gcnconvmodule_t_kernel(tc, inputs, adj, W, b, out):
                 )
             st[("db", g)] = db
 
-        def outer(u):
+        def outer_row(u, k):
             g = u // 2
-            r0 = (u % 2) * RH
-            dn = st[("dn", g)]
-            db = st[("db", g)]
-            gt = work.tile([P, RH, F], BF16, name="gt")
-            st[("gt", u)] = gt
-            for k in range(RH):
-                if k < V_SHARE:
-                    nc.vector.tensor_scalar(
-                        out=gt[:, k, :],
-                        in0=db[:],
-                        scalar1=dn[:, r0 + k : r0 + k + 1],
-                        scalar2=None,
-                        op0=ALU.mult,
-                    )
-                else:
-                    nc.scalar.activation(
-                        out=gt[:, k, :], in_=db[:], func=ACT.Copy, scale=dn[:, r0 + k : r0 + k + 1]
-                    )
+            r = (u % 2) * RH + k
+            if k == 0:
+                st[("gt", u)] = work.tile([P, RH, F], BF16, name="gt")
+            gt = st[("gt", u)]
+            if k < V_SHARE:
+                nc.vector.tensor_scalar(
+                    out=gt[:, k, :],
+                    in0=st[("db", g)][:],
+                    scalar1=st[("dn", g)][:, r : r + 1],
+                    scalar2=None,
+                    op0=ALU.mult,
+                )
+            else:
+                nc.scalar.activation(
+                    out=gt[:, k, :], in_=st[("db", g)][:], func=ACT.Copy, scale=st[("dn", g)][:, r : r + 1]
+                )
 
-        def mask(u, bk):
+        def mask(u):
             data = adj_view(u // 2)
-            r0 = (u % 2) * RH + bk * GPB
+            r0 = (u % 2) * RH
             nc.vector.tensor_tensor(
-                out=data[:, r0 : r0 + GPB, :],
-                in0=data[:, r0 : r0 + GPB, :],
-                in1=st[("gt", u)][:, bk * GPB : (bk + 1) * GPB, :],
-                op=ALU.mult,
+                out=data[:, r0 : r0 + RH, :], in0=data[:, r0 : r0 + RH, :], in1=st[("gt", u)][:], op=ALU.mult
             )
 
         def n_transpose(u, g2, bk):
-            if bk == 0:
-                st[("nt", u, g2)] = work.tile([P, 2048], BF16, name="nt", align_bytes=64, bufs=4)
+            if g2 == 0 and bk == 0:
+                st[("nt", u)] = work.tile([P, 2, 2048], BF16, name="nt", align_bytes=64)
             data = adj_view(u // 2)
             npt = psum.tile([P, 1024], BF16, name="npt", tag="np")
             for k in range(GPB):
@@ -267,40 +281,54 @@ def tile_gcnconvmodule_t_kernel(tc, inputs, adj, W, b, out):
                         in_=data[:, r, col : col + P],
                         identity=ident_bf[:],
                     )
-            nc.scalar.copy(out=st[("nt", u, g2)][:, bk * 1024 : (bk + 1) * 1024], in_=npt[:])
+            nc.scalar.copy(out=st[("nt", u)][:, g2, bk * 1024 : (bk + 1) * 1024], in_=npt[:])
 
-        def n_quantise(u, g2):
-            ntw = work.tile([P, 512], U32, name="ntw", align_bytes=64, bufs=4)
-            nts = work.tile([P, 512], U8, name="nts", align_bytes=64, bufs=4)
-            quantise(nc, st[("nt", u, g2)], ntw, nts, [2048])
-            st[("ntw", u, g2)] = ntw
-            st[("nts", u, g2)] = nts
+        def n_quantise(u):
+            ntw = work.tile([P, 2 * 512], U32, name="ntw", align_bytes=64)
+            nts = work.tile([P, 2 * 512], U8, name="nts", align_bytes=64)
+            quantise(nc, st[("nt", u)][:].rearrange("p g c -> p (g c)"), ntw, nts, [4096])
+            st[("ntw", u)] = ntw
+            st[("nts", u)] = nts
 
-        def agg(u, c):
-            if c == 0:
-                st[("ot", u)] = work.tile([P, 4, DOUT], F32, name="ot", bufs=3)
+        def agg_mm(u, dblk):
+            if dblk == 0:
+                st[("tt", u)] = work.tile([P, 3, 512], F32, name="tt", align_bytes=64)
             hw = st[("hw", u // 2)]
             hs = st[("hs", u // 2)]
-            acc = psum.tile([P, DOUT], F32, name="acc", tag="ap")
-            for lo, hi in ((0, 256), (256, 384)):
-                for g2 in range(2):
-                    nc.tensor.matmul_mx(
-                        out=acc[:, lo:hi],
-                        lhsT=st[("ntw", u, g2)][:, c * P : (c + 1) * P].bitcast(FP8X4),
-                        lhsT_scale=st[("nts", u, g2)][:, c * P : (c + 1) * P],
-                        rhs=hw[:, g2 * DOUT + lo : g2 * DOUT + hi].bitcast(FP8X4),
-                        rhs_scale=hs[:, g2 * DOUT + lo : g2 * DOUT + hi],
-                        start=(g2 == 0),
-                        stop=(g2 == 1),
-                    )
-            nc.vector.tensor_tensor(out=st[("ot", u)][:, c, :], in0=acc[:], in1=bias[:], op=ALU.add)
+            acc = psum.tile([P, 512], F32, name="acc", tag="ag")
+            for g2 in range(2):
+                lo = g2 * DOUT + dblk * P
+                nc.tensor.matmul_mx(
+                    out=acc[:],
+                    lhsT=hw[:, lo : lo + P].bitcast(FP8X4),
+                    lhsT_scale=hs[:, lo : lo + P],
+                    rhs=st[("ntw", u)][:, g2 * 512 : (g2 + 1) * 512].bitcast(FP8X4),
+                    rhs_scale=st[("nts", u)][:, g2 * 512 : (g2 + 1) * 512],
+                    start=(g2 == 0),
+                    stop=(g2 == 1),
+                )
+            nc.scalar.activation(
+                out=st[("tt", u)][:, dblk, :], in_=acc[:], func=ACT.Tanh, bias=bcol[:, dblk : dblk + 1], scale=1.0
+            )
 
-        def finish(u):
-            ot = st[("ot", u)]
-            nc.scalar.activation(out=ot[:], in_=ot[:], func=ACT.Tanh)
+        def fin(u, c):
+            if c == 0:
+                st[("ot", u)] = work.tile([P, 4, DOUT], F32, name="ot")
+            tt = st[("tt", u)]
+            fo = psum.tile([P, DOUT], F32, name="fo", tag="fo")
+            for dblk in range(3):
+                nc.tensor.transpose(
+                    out=fo[:, dblk * P : (dblk + 1) * P], in_=tt[:, dblk, c * P : (c + 1) * P], identity=ident_f[:]
+                )
+            if c in FE_ON_V:
+                nc.vector.tensor_copy(out=st[("ot", u)][:, c, :], in_=fo[:])
+            else:
+                nc.scalar.copy(out=st[("ot", u)][:, c, :], in_=fo[:])
+
+        def store(u):
             nc.sync.dma_start(
                 out=out[u // 2, (u % 2) * 512 : (u % 2 + 1) * 512, :].rearrange("(c p) d -> p c d", p=P),
-                in_=ot[:],
+                in_=st[("ot", u)][:],
             )
 
         U = 2 * B
@@ -312,48 +340,70 @@ def tile_gcnconvmodule_t_kernel(tc, inputs, adj, W, b, out):
             return 0 <= u < U
 
         for k in range(-7, U + 2):
+            if oku(k - 1):
+                n_quantise(k - 1)
             if oku(k - 2):
-                finish(k - 2)
-            for bk in range(2):
-                if oku(k):
-                    mask(k, bk)
-                if oku(k - 1):
-                    agg(k - 1, 2 * bk)
-                    agg(k - 1, 2 * bk + 1)
-                if oku(k):
-                    n_transpose(k, 0, bk)
-                    n_transpose(k, 1, bk)
+                fin(k - 2, 0)
+                fin(k - 2, 1)
+            if oku(k):
+                mask(k)
+            if oku(k - 1):
+                agg_mm(k - 1, 0)
+                agg_mm(k - 1, 1)
+            if oku(k):
+                n_transpose(k, 0, 0)
+                n_transpose(k, 1, 0)
+            if oku(k - 1):
+                agg_mm(k - 1, 2)
+            if oku(k):
+                n_transpose(k, 0, 1)
+                n_transpose(k, 1, 1)
+            if oku(k - 2):
+                fin(k - 2, 2)
+                fin(k - 2, 3)
+                store(k - 2)
+            rows = list(range(RH)) if oku(k + 1) else []
             if k % 2 == 0:
                 ga = (k + 2) // 2
                 if okg(ga):
+                    deg_b(ga)
                     for g2 in range(2):
                         for dblk in range(3):
                             h_matmul(ga, g2, dblk)
-                    diag_or(ga, 1)
-                    for r in range(RH, R):
-                        count(ga, r)
-                    deg_a(ga)
-                if okg((k + 4) // 2):
-                    x_quantise((k + 4) // 2)
+                gc = (k + 4) // 2
+                if okg(gc):
+                    diag_one(gc, 0)
+                    diag_one(gc, 1)
+                for j in rows[0:2]:
+                    outer_row(k + 1, j)
+                if okg(gc):
+                    to_mask(gc)
+                for j in rows[2:4]:
+                    outer_row(k + 1, j)
+                if okg(gc):
+                    fold(gc, 0)
+                for j in rows[4:]:
+                    outer_row(k + 1, j)
             else:
-                if okg((k + 1) // 2):
-                    deg_b((k + 1) // 2)
-                gb = (k + 3) // 2
-                if okg(gb):
-                    diag_or(gb, 0)
-                    for r in range(RH):
-                        count(gb, r)
-                if okg((k + 1) // 2):
-                    h_quantise((k + 1) // 2)
                 if okg((k + 5) // 2):
                     for i in range(4):
                         x_transpose((k + 5) // 2, i)
-                if okg((k + 5) // 2):
-                    load_adj((k + 5) // 2)
-                if okg((k + 7) // 2):
+                gb = (k + 3) // 2
+                if okg(gb):
+                    fold(gb, 1)
+                    x_quantise(gb)
+                    fold(gb, 2)
+                if okg((k + 1) // 2):
+                    h_quantise((k + 1) // 2)
+                if okg(gb):
+                    fold(gb, 3)
+                for j in rows[0:2]:
+                    outer_row(k + 1, j)
+                if okg(gb):
+                    fold_end(gb)
+                    deg_a(gb)
+                for j in rows[2:]:
+                    outer_row(k + 1, j)
+                if okg((k + 7) // 2) and k + 7 > 0:
+                    load_adj((k + 7) // 2)
                     load_x((k + 7) // 2)
-            if oku(k):
-                n_quantise(k, 0)
-                n_quantise(k, 1)
-            if oku(k + 1):
-                outer(k + 1)

@@ -28,7 +28,7 @@ RH = R // 2
 NS = 4 // SEG
 GPB = 256 // RG
 PAD = 8 * RG
-V_SHARE = 8
+V_SHARE = 4
 FE_ON_V = ()
 LEVELS = 4
 
@@ -74,7 +74,6 @@ def tile_gcnconvmodule_t_kernel(tc, inputs, adj, W, b, out):
             nc.sync.dma_start(out=xt[:], in_=inputs[g].rearrange("(q p) k -> p q k", p=P))
 
         load_x(0)
-        load_adj(0)
 
         ident_bf = const.tile([P, P], BF16, name="ident_bf")
         make_identity(nc, ident_bf[:])
@@ -91,19 +90,16 @@ def tile_gcnconvmodule_t_kernel(tc, inputs, adj, W, b, out):
         mhalf = const.tile([P, R], F32, name="mhalf")
         nc.vector.memset(mhalf[:], -0.5)
 
-        w_raw = work.tile([P, 4, DOUT], BF16, name="w_raw", tag="ot")
+        w_raw = work.tile([P, 4, DOUT], BF16, name="w_raw", tag="ot", bufs=3)
         nc.sync.dma_start(
             out=w_raw[:].rearrange("p (u e) d -> p u (e d)", u=2),
             in_=W.rearrange("(u p e) d -> p u (e d)", u=2, e=2),
         )
-        b_rows = const.tile([P, P], BF16, name="b_rows")
-        nc.vector.memset(b_rows[:], 0.0)
-        nc.sync.dma_start(out=b_rows[0:3, :], in_=b.rearrange("(r c) -> r c", c=P))
-        bp = psum.tile([P, P], BF16, name="bp", tag="tp")
-        nc.tensor.transpose(out=bp[:], in_=b_rows[:], identity=ident_bf[:])
-        bcol = const.tile([P, 3], F32, name="bcol")
-        nc.vector.tensor_copy(out=bcol[:], in_=bp[:, 0:3])
-        w_grp = work.tile([P, DOUT, 4], BF16, name="w_grp", tag="tt", align_bytes=64)
+        load_adj(0)
+        b_bf = const.tile([P, DOUT], BF16, name="b_bf")
+        nc.sync.dma_start(out=b_bf[:], in_=b.partition_broadcast(P))
+        bias = const.tile([P, DOUT], F32, name="bias")
+        w_grp = work.tile([P, DOUT, 4], BF16, name="w_grp", tag="nt", align_bytes=64)
         nc.vector.tensor_copy(out=w_grp[:], in_=w_raw[:].rearrange("p t d -> p d t"))
         w_codes = const.tile([P, DOUT], U32, name="w_codes", align_bytes=64)
         w_scales = const.tile([P, DOUT], U8, name="w_scales", align_bytes=64)
@@ -172,30 +168,19 @@ def tile_gcnconvmodule_t_kernel(tc, inputs, adj, W, b, out):
                 op=ALU.bitwise_or,
             )
 
-        def to_mask(g):
+        def count(g, r):
+            if r == 0:
+                st[("part", g)] = small.tile([P, R], F32, name="part")
             data = adj_view(g)
-            nc.vector.tensor_scalar(out=data, in0=data, scalar1=0.0, scalar2=None, op0=ALU.not_equal)
-
-        def fold(g, lv):
-            data = adj_view(g)
-            width = F >> (lv + 1)
-            if lv == 0:
-                st[("tree", g)] = work.tile([P, R, F // 2], BF16, name="tree", bufs=1)
-                nc.vector.tensor_tensor(
-                    out=st[("tree", g)][:], in0=data[:, :, 0:width], in1=data[:, :, width : 2 * width], op=ALU.add
-                )
-            else:
-                tree = st[("tree", g)]
-                nc.vector.tensor_tensor(
-                    out=tree[:, :, 0:width], in0=tree[:, :, 0:width], in1=tree[:, :, width : 2 * width], op=ALU.add
-                )
-
-        def fold_end(g):
-            part = small.tile([P, R], F32, name="part")
-            nc.vector.tensor_reduce(
-                out=part[:], in_=st[("tree", g)][:, :, 0 : F >> LEVELS], axis=AX.X, op=ALU.add
+            nc.vector.tensor_scalar(
+                out=data[:, r, :],
+                in0=data[:, r, :],
+                scalar1=0.0,
+                scalar2=None,
+                op0=ALU.not_equal,
+                op1=ALU.add,
+                accum_out=st[("part", g)][:, r : r + 1],
             )
-            st[("part", g)] = part
 
         def deg_a(g):
             degp = psum.tile([P, R], F32, name="degp", tag="tp")
@@ -259,11 +244,18 @@ def tile_gcnconvmodule_t_kernel(tc, inputs, adj, W, b, out):
                 )
 
         def mask(u):
-            data = adj_view(u // 2)
-            r0 = (u % 2) * RH
-            nc.vector.tensor_tensor(
-                out=data[:, r0 : r0 + RH, :], in0=data[:, r0 : r0 + RH, :], in1=st[("gt", u)][:], op=ALU.mult
-            )
+            g = u // 2
+            data = adj_view(g)
+            for k in range(RH):
+                r = (u % 2) * RH + k
+                nc.vector.scalar_tensor_tensor(
+                    out=data[:, r, :],
+                    in0=st[("db", g)][:],
+                    scalar=st[("dn", g)][:, r : r + 1],
+                    in1=data[:, r, :],
+                    op0=ALU.mult,
+                    op1=ALU.mult,
+                )
 
         def n_transpose(u, g2, bk):
             if g2 == 0 and bk == 0:
@@ -290,45 +282,36 @@ def tile_gcnconvmodule_t_kernel(tc, inputs, adj, W, b, out):
             st[("ntw", u)] = ntw
             st[("nts", u)] = nts
 
-        def agg_mm(u, dblk):
-            if dblk == 0:
-                st[("tt", u)] = work.tile([P, 3, 512], F32, name="tt", align_bytes=64)
+        def agg_mm(u, c):
             hw = st[("hw", u // 2)]
             hs = st[("hs", u // 2)]
-            acc = psum.tile([P, 512], F32, name="acc", tag="ag")
-            for g2 in range(2):
-                lo = g2 * DOUT + dblk * P
-                nc.tensor.matmul_mx(
-                    out=acc[:],
-                    lhsT=hw[:, lo : lo + P].bitcast(FP8X4),
-                    lhsT_scale=hs[:, lo : lo + P],
-                    rhs=st[("ntw", u)][:, g2 * 512 : (g2 + 1) * 512].bitcast(FP8X4),
-                    rhs_scale=st[("nts", u)][:, g2 * 512 : (g2 + 1) * 512],
-                    start=(g2 == 0),
-                    stop=(g2 == 1),
-                )
-            nc.scalar.activation(
-                out=st[("tt", u)][:, dblk, :], in_=acc[:], func=ACT.Tanh, bias=bcol[:, dblk : dblk + 1], scale=1.0
-            )
+            acc = psum.tile([P, DOUT], F32, name="acc", tag="ap", bufs=4)
+            st[("acc", u, c)] = acc
+            for lo, hi in ((0, 256), (256, 384)):
+                for g2 in range(2):
+                    nc.tensor.matmul_mx(
+                        out=acc[:, lo:hi],
+                        lhsT=st[("ntw", u)][:, g2 * 512 + c * P : g2 * 512 + (c + 1) * P].bitcast(FP8X4),
+                        lhsT_scale=st[("nts", u)][:, g2 * 512 + c * P : g2 * 512 + (c + 1) * P],
+                        rhs=hw[:, g2 * DOUT + lo : g2 * DOUT + hi].bitcast(FP8X4),
+                        rhs_scale=hs[:, g2 * DOUT + lo : g2 * DOUT + hi],
+                        start=(g2 == 0),
+                        stop=(g2 == 1),
+                    )
 
-        def fin(u, c):
+        def agg_bias(u, c):
             if c == 0:
-                st[("ot", u)] = work.tile([P, 4, DOUT], F32, name="ot")
-            tt = st[("tt", u)]
-            fo = psum.tile([P, DOUT], F32, name="fo", tag="fo")
-            for dblk in range(3):
-                nc.tensor.transpose(
-                    out=fo[:, dblk * P : (dblk + 1) * P], in_=tt[:, dblk, c * P : (c + 1) * P], identity=ident_f[:]
-                )
-            if c in FE_ON_V:
-                nc.vector.tensor_copy(out=st[("ot", u)][:, c, :], in_=fo[:])
-            else:
-                nc.scalar.copy(out=st[("ot", u)][:, c, :], in_=fo[:])
+                st[("ot", u)] = work.tile([P, 4, DOUT], F32, name="ot", bufs=3)
+            nc.vector.tensor_tensor(out=st[("ot", u)][:, c, :], in0=st[("acc", u, c)][:], in1=bias[:], op=ALU.add)
 
-        def store(u):
+        def finish(u, c0, c1):
+            ot = st[("ot", u)]
+            nc.scalar.activation(out=ot[:, c0:c1, :], in_=ot[:, c0:c1, :], func=ACT.Tanh)
             nc.sync.dma_start(
-                out=out[u // 2, (u % 2) * 512 : (u % 2 + 1) * 512, :].rearrange("(c p) d -> p c d", p=P),
-                in_=st[("ot", u)][:],
+                out=out[u // 2, (u % 2) * 512 + c0 * P : (u % 2) * 512 + c1 * P, :].rearrange(
+                    "(c p) d -> p c d", p=P
+                ),
+                in_=ot[:, c0:c1, :],
             )
 
         U = 2 * B
@@ -339,71 +322,55 @@ def tile_gcnconvmodule_t_kernel(tc, inputs, adj, W, b, out):
         def oku(u):
             return 0 <= u < U
 
-        for k in range(-7, U + 2):
+        for k in range(-7, U + 3):
             if oku(k - 1):
                 n_quantise(k - 1)
-            if oku(k - 2):
-                fin(k - 2, 0)
-                fin(k - 2, 1)
             if oku(k):
                 mask(k)
-            if oku(k - 1):
-                agg_mm(k - 1, 0)
-                agg_mm(k - 1, 1)
-            if oku(k):
                 n_transpose(k, 0, 0)
                 n_transpose(k, 1, 0)
-            if oku(k - 1):
-                agg_mm(k - 1, 2)
-            if oku(k):
                 n_transpose(k, 0, 1)
                 n_transpose(k, 1, 1)
-            if oku(k - 2):
-                fin(k - 2, 2)
-                fin(k - 2, 3)
-                store(k - 2)
-            rows = list(range(RH)) if oku(k + 1) else []
+            if k == 2:
+                nc.vector.tensor_copy(out=bias[:], in_=b_bf[:])
+            for c in range(4):
+                if oku(k - 2):
+                    agg_bias(k - 2, c)
+                    if k - 2 == U - 1:
+                        finish(k - 2, c, c + 1)
+                if oku(k - 1):
+                    agg_mm(k - 1, c)
+            if oku(k - 2) and k - 2 < U - 1:
+                finish(k - 2, 0, 4)
+            rows = list(range(RH)) if oku(k + 1) and not True else []
             if k % 2 == 0:
                 ga = (k + 2) // 2
                 if okg(ga):
-                    deg_b(ga)
                     for g2 in range(2):
                         for dblk in range(3):
                             h_matmul(ga, g2, dblk)
+                    deg_b(ga)
+            if k % 2 == 0:
                 gc = (k + 4) // 2
                 if okg(gc):
                     diag_one(gc, 0)
-                    diag_one(gc, 1)
-                for j in rows[0:2]:
-                    outer_row(k + 1, j)
-                if okg(gc):
-                    to_mask(gc)
-                for j in rows[2:4]:
-                    outer_row(k + 1, j)
-                if okg(gc):
-                    fold(gc, 0)
-                for j in rows[4:]:
-                    outer_row(k + 1, j)
+                    for r in range(RH):
+                        count(gc, r)
             else:
+                gb = (k + 3) // 2
+                if okg(gb):
+                    diag_one(gb, 1)
+                    for r in range(RH, R):
+                        count(gb, r)
+                    deg_a(gb)
+                    x_quantise(gb)
                 if okg((k + 5) // 2):
                     for i in range(4):
                         x_transpose((k + 5) // 2, i)
-                gb = (k + 3) // 2
-                if okg(gb):
-                    fold(gb, 1)
-                    x_quantise(gb)
-                    fold(gb, 2)
                 if okg((k + 1) // 2):
                     h_quantise((k + 1) // 2)
-                if okg(gb):
-                    fold(gb, 3)
-                for j in rows[0:2]:
-                    outer_row(k + 1, j)
-                if okg(gb):
-                    fold_end(gb)
-                    deg_a(gb)
-                for j in rows[2:]:
-                    outer_row(k + 1, j)
                 if okg((k + 7) // 2) and k + 7 > 0:
                     load_adj((k + 7) // 2)
                     load_x((k + 7) // 2)
+            for j in rows:
+                outer_row(k + 1, j)

@@ -51,7 +51,7 @@ def tile_gcnconvmodule_t_kernel(tc, inputs, adj, W, b, out):
         adjp = ctx.enter_context(tc.tile_pool(name="adjp", bufs=4))
         work = ctx.enter_context(tc.tile_pool(name="work", bufs=2))
         small = ctx.enter_context(tc.tile_pool(name="small", bufs=3))
-        psum = ctx.enter_context(tc.psum_pool(name="psum", bufs=2))
+        psum = ctx.enter_context(tc.psum_pool(name="psum", bufs=4))
         ctx.enter_context(tc.manual_schedule())
 
         st = {}
@@ -257,13 +257,13 @@ def tile_gcnconvmodule_t_kernel(tc, inputs, adj, W, b, out):
                     op1=ALU.mult,
                 )
 
-        def n_transpose(u, g2, bk):
-            if g2 == 0 and bk == 0:
+        def n_transpose(u, g2, qd):
+            if g2 == 0 and qd == 0:
                 st[("nt", u)] = work.tile([P, 2, 2048], BF16, name="nt", align_bytes=64)
             data = adj_view(u // 2)
-            npt = psum.tile([P, 1024], BF16, name="npt", tag="np")
-            for k in range(GPB):
-                r = (u % 2) * RH + bk * GPB + k
+            npt = psum.tile([P, 512], BF16, name="npt", tag="tp")
+            for k in range(2):
+                r = (u % 2) * RH + qd * 2 + k
                 for sg in range(NS):
                     col = P * (g2 * NS + sg)
                     nc.tensor.transpose(
@@ -273,7 +273,7 @@ def tile_gcnconvmodule_t_kernel(tc, inputs, adj, W, b, out):
                         in_=data[:, r, col : col + P],
                         identity=ident_bf[:],
                     )
-            nc.scalar.copy(out=st[("nt", u)][:, g2, bk * 1024 : (bk + 1) * 1024], in_=npt[:])
+            nc.scalar.copy(out=st[("nt", u)][:, g2, qd * 512 : (qd + 1) * 512], in_=npt[:])
 
         def n_quantise(u):
             ntw = work.tile([P, 2 * 512], U32, name="ntw", align_bytes=64)
@@ -327,10 +327,9 @@ def tile_gcnconvmodule_t_kernel(tc, inputs, adj, W, b, out):
                 n_quantise(k - 1)
             if oku(k):
                 mask(k)
-                n_transpose(k, 0, 0)
-                n_transpose(k, 1, 0)
-                n_transpose(k, 0, 1)
-                n_transpose(k, 1, 1)
+                for qd in range(4):
+                    n_transpose(k, 0, qd)
+                    n_transpose(k, 1, qd)
             if k == 2:
                 nc.vector.tensor_copy(out=bias[:], in_=b_bf[:])
             for c in range(4):

@@ -20,17 +20,13 @@ B = 8
 N = 1024
 DIN = 512
 DOUT = 384
-SEG = 2
-RG = P // SEG
-F = N // SEG
-R = N // RG
-RH = R // 2
-NS = 4 // SEG
-GPB = 256 // RG
-PAD = 8 * RG
-V_SHARE = 4
-FE_ON_V = ()
-LEVELS = 4
+PIECES = 2
+ROWS = P // PIECES
+PIECE = N // PIECES
+GROUPS = N // ROWS
+UNIT_GROUPS = GROUPS // 2
+UNITS = 2 * B
+PAD = 8 * ROWS
 
 
 def quantise(nc, flat, codes, scales, widths):
@@ -57,16 +53,15 @@ def tile_gcnconvmodule_t_kernel(tc, inputs, adj, W, b, out):
         st = {}
 
         def adj_view(g):
-            return st[("ah", g)][:, 0 : R * F].rearrange("p (r f) -> p r f", f=F)
+            return st[("ah", g)][:, 0 : GROUPS * PIECE].rearrange("p (r f) -> p r f", f=PIECE)
 
         def load_adj(g):
-            st[("ah", g)] = adjp.tile([P, R * F + PAD], BF16, name="ah")
-            rows = adj[g].rearrange("n (s f) -> (n s) f", s=SEG).rearrange("(r p) f -> p r f", p=P)
+            st[("ah", g)] = adjp.tile([P, GROUPS * PIECE + PAD], BF16, name="ah")
+            rows = adj[g].rearrange("n (s f) -> (n s) f", s=PIECES).rearrange("(r p) f -> p r f", p=P)
             data = adj_view(g)
             for half in range(2):
-                nc.sync.dma_start(
-                    out=data[:, half * RH : (half + 1) * RH, :], in_=rows[:, half * RH : (half + 1) * RH, :]
-                )
+                lo = half * UNIT_GROUPS
+                nc.sync.dma_start(out=data[:, lo : lo + UNIT_GROUPS, :], in_=rows[:, lo : lo + UNIT_GROUPS, :])
 
         def load_x(g):
             xt = work.tile([P, 8, DIN], BF16, name="xt")
@@ -74,21 +69,26 @@ def tile_gcnconvmodule_t_kernel(tc, inputs, adj, W, b, out):
             nc.sync.dma_start(out=xt[:], in_=inputs[g].rearrange("(q p) k -> p q k", p=P))
 
         load_x(0)
+        load_x(1)
 
         ident_bf = const.tile([P, P], BF16, name="ident_bf")
         make_identity(nc, ident_bf[:])
         ident_f = const.tile([P, P], F32, name="ident_f")
         make_identity(nc, ident_f[:])
-        diag_bits = const.tile([P, SEG, RG], BF16, name="diag_bits")
-        nc.vector.tensor_copy(out=diag_bits[:], in_=ident_bf[:].rearrange("p (c s) -> p s c", s=SEG))
-        grp = const.tile([P, RG], F32, name="grp")
+        diag_bits = const.tile([P, PIECES, ROWS], BF16, name="diag_bits")
+        nc.vector.tensor_copy(out=diag_bits[:], in_=ident_bf[:].rearrange("p (c s) -> p s c", s=PIECES))
+        same_row = const.tile([P, ROWS], F32, name="same_row")
         nc.vector.tensor_reduce(
-            out=grp[:], in_=ident_f[:].rearrange("p (c s) -> p c s", s=SEG), axis=AX.X, op=ALU.add
+            out=same_row[:], in_=ident_f[:].rearrange("p (c s) -> p c s", s=PIECES), axis=AX.X, op=ALU.add
         )
-        pair = const.tile([P, RG, SEG], F32, name="pair")
-        nc.vector.tensor_copy(out=pair[:], in_=grp[:].unsqueeze(2).to_broadcast([P, RG, SEG]))
-        mhalf = const.tile([P, R], F32, name="mhalf")
-        nc.vector.memset(mhalf[:], -0.5)
+        pair = const.tile([P, ROWS, PIECES], F32, name="pair")
+        nc.vector.tensor_copy(out=pair[:], in_=same_row[:].unsqueeze(2).to_broadcast([P, ROWS, PIECES]))
+        parity = const.tile([P, PIECES], F32, name="parity")
+        nc.vector.tensor_reduce(
+            out=parity[:], in_=ident_f[:].rearrange("p (c s) -> p s c", s=PIECES), axis=AX.X, op=ALU.add
+        )
+        minus_half = const.tile([P, GROUPS], F32, name="minus_half")
+        nc.vector.memset(minus_half[:], -0.5)
 
         w_raw = work.tile([P, 4, DOUT], BF16, name="w_raw", tag="ot", bufs=3)
         nc.sync.dma_start(
@@ -134,7 +134,7 @@ def tile_gcnconvmodule_t_kernel(tc, inputs, adj, W, b, out):
             xs = st[("xs", g)]
             hp = psum.tile([P, 4, P], F32, name="hp", tag="tp")
             for t in range(4):
-                q = (F // P) * (t % SEG) + g2 * NS + t // SEG
+                q = 4 * (t % 2) + 2 * g2 + t // 2
                 nc.tensor.matmul_mx(
                     out=hp[:, t, :],
                     lhsT=xw[:, q * P : (q + 1) * P].bitcast(FP8X4),
@@ -149,8 +149,8 @@ def tile_gcnconvmodule_t_kernel(tc, inputs, adj, W, b, out):
             )
 
         def h_quantise(g):
-            hw = small.tile([P, 2 * DOUT], U32, name="hw", align_bytes=64)
-            hs = small.tile([P, 2 * DOUT], U8, name="hs", align_bytes=64)
+            hw = small.tile([P, 2 * DOUT], U32, name="hw", align_bytes=64, bufs=4)
+            hs = small.tile([P, 2 * DOUT], U8, name="hs", align_bytes=64, bufs=4)
             quantise(nc, st[("hq", g)][:].rearrange("p g d t -> p (g d t)"), hw, hs, [2048, 1024])
             st[("hw", g)] = hw
             st[("hs", g)] = hs
@@ -158,19 +158,19 @@ def tile_gcnconvmodule_t_kernel(tc, inputs, adj, W, b, out):
         def diag_one(g, s):
             ah32 = st[("ah", g)][:].bitcast(I32)
             d32 = diag_bits[:].bitcast(I32)
-            step = (F + RG) // 2
-            base = 8 * s * (F // 2)
-            view = ah32[:, base : base + 8 * step].rearrange("p (i w) -> p i w", w=step)[:, :, 0 : RG // 2]
+            step = (PIECE + ROWS) // 2
+            base = 8 * s * (PIECE // 2)
+            view = ah32[:, base : base + 8 * step].rearrange("p (i w) -> p i w", w=step)[:, :, 0 : ROWS // 2]
             nc.vector.tensor_tensor(
                 out=view,
                 in0=view,
-                in1=d32[:, s, :].unsqueeze(1).to_broadcast([P, 8, RG // 2]),
+                in1=d32[:, s, :].unsqueeze(1).to_broadcast([P, 8, ROWS // 2]),
                 op=ALU.bitwise_or,
             )
 
         def count(g, r):
             if r == 0:
-                st[("part", g)] = small.tile([P, R], F32, name="part")
+                st[("part", g)] = small.tile([P, GROUPS], F32, name="part")
             data = adj_view(g)
             nc.vector.tensor_scalar(
                 out=data[:, r, :],
@@ -182,8 +182,8 @@ def tile_gcnconvmodule_t_kernel(tc, inputs, adj, W, b, out):
                 accum_out=st[("part", g)][:, r : r + 1],
             )
 
-        def deg_a(g):
-            degp = psum.tile([P, R], F32, name="degp", tag="tp")
+        def dinv_rows(g):
+            degp = psum.tile([P, GROUPS], F32, name="degp", tag="tp")
             nc.tensor.matmul(
                 out=degp[:],
                 lhsT=pair[:].rearrange("p c s -> p (c s)"),
@@ -191,63 +191,53 @@ def tile_gcnconvmodule_t_kernel(tc, inputs, adj, W, b, out):
                 start=True,
                 stop=True,
             )
-            deg = small.tile([P, R], F32, name="deg")
+            deg = small.tile([P, GROUPS], F32, name="deg")
             nc.scalar.copy(out=deg[:], in_=degp[:])
-            dn = small.tile([P, R], F32, name="dn")
-            nc.gpsimd.tensor_tensor(out=dn[:], in0=deg[:], in1=mhalf[:], op=ALU.pow)
-            rr = work.tile([P, 8, RG, SEG], F32, name="rr", bufs=1)
+            dn = small.tile([P, GROUPS], F32, name="dn")
+            nc.gpsimd.tensor_tensor(out=dn[:], in0=deg[:], in1=minus_half[:], op=ALU.pow)
+            halves = dn[:].rearrange("p (s h a) -> p h s a", s=PIECES, h=2)
+            pick = small.tile([P, 3, PIECES, 4], F32, name="pick")
+            for h in range(2):
+                nc.gpsimd.tensor_scalar(
+                    out=pick[:, h, :, :],
+                    in0=halves[:, h, :, :],
+                    scalar1=parity[:, h : h + 1],
+                    scalar2=0.0,
+                    op0=ALU.mult,
+                    op1=ALU.add,
+                )
+            nc.gpsimd.tensor_tensor(out=pick[:, 2, :, :], in0=pick[:, 0, :, :], in1=pick[:, 1, :, :], op=ALU.add)
+            rep = work.tile([P, 4, ROWS, PIECES], F32, name="rep", bufs=1)
             nc.gpsimd.tensor_scalar(
-                out=rr[:],
-                in0=dn[:].rearrange("p (s a) -> p a s", s=SEG).unsqueeze(2).to_broadcast([P, 8, RG, SEG]),
+                out=rep[:],
+                in0=pick[:, 2, :, :].rearrange("p s a -> p a s").unsqueeze(2).to_broadcast([P, 4, ROWS, PIECES]),
                 scalar1=1.0,
                 scalar2=0.0,
                 op0=ALU.mult,
                 op1=ALU.add,
             )
             st[("dn", g)] = dn
-            st[("rr", g)] = rr
+            st[("rep", g)] = rep
 
-        def deg_b(g):
-            rr = st[("rr", g)]
-            db = small.tile([P, F], F32, name="db")
-            for h in range(2):
-                dbp = psum.tile([P, 4, P], F32, name="dbp", tag="tp")
-                for a4 in range(4):
-                    nc.tensor.transpose(
-                        out=dbp[:, a4, :],
-                        in_=rr[:, 4 * h + a4, :, :].rearrange("p c s -> p (c s)"),
-                        identity=ident_f[:],
-                    )
-                nc.scalar.copy(
-                    out=db[:, 4 * h * RG : (4 * h + 4) * RG].rearrange("p (a c) -> p a c", c=RG),
-                    in_=dbp[:].rearrange("p a (c s) -> p a c s", s=SEG)[:, :, :, 0],
+        def dinv_columns(g):
+            rep = st[("rep", g)]
+            db = small.tile([P, PIECE], F32, name="db")
+            dbp = psum.tile([P, 4, P], F32, name="dbp", tag="tp")
+            for a in range(4):
+                nc.tensor.transpose(
+                    out=dbp[:, a, :], in_=rep[:, a, :, :].rearrange("p c s -> p (c s)"), identity=ident_f[:]
                 )
+            nc.scalar.copy(
+                out=db[:].rearrange("p (h a c) -> p h a c", h=2, a=4),
+                in_=dbp[:].rearrange("p a (c h) -> p h a c", h=2),
+            )
             st[("db", g)] = db
 
-        def outer_row(u, k):
-            g = u // 2
-            r = (u % 2) * RH + k
-            if k == 0:
-                st[("gt", u)] = work.tile([P, RH, F], BF16, name="gt")
-            gt = st[("gt", u)]
-            if k < V_SHARE:
-                nc.vector.tensor_scalar(
-                    out=gt[:, k, :],
-                    in0=st[("db", g)][:],
-                    scalar1=st[("dn", g)][:, r : r + 1],
-                    scalar2=None,
-                    op0=ALU.mult,
-                )
-            else:
-                nc.scalar.activation(
-                    out=gt[:, k, :], in_=st[("db", g)][:], func=ACT.Copy, scale=st[("dn", g)][:, r : r + 1]
-                )
-
-        def mask(u):
+        def norm_rows(u):
             g = u // 2
             data = adj_view(g)
-            for k in range(RH):
-                r = (u % 2) * RH + k
+            for k in range(UNIT_GROUPS):
+                r = (u % 2) * UNIT_GROUPS + k
                 nc.vector.scalar_tensor_tensor(
                     out=data[:, r, :],
                     in0=st[("db", g)][:],
@@ -257,32 +247,32 @@ def tile_gcnconvmodule_t_kernel(tc, inputs, adj, W, b, out):
                     op1=ALU.mult,
                 )
 
-        def n_transpose(u, g2, qd):
+        def norm_transpose(u, g2, qd):
             if g2 == 0 and qd == 0:
                 st[("nt", u)] = work.tile([P, 2, 2048], BF16, name="nt", align_bytes=64)
             data = adj_view(u // 2)
             npt = psum.tile([P, 512], BF16, name="npt", tag="tp")
             for k in range(2):
-                r = (u % 2) * RH + qd * 2 + k
-                for sg in range(NS):
-                    col = P * (g2 * NS + sg)
+                r = (u % 2) * UNIT_GROUPS + qd * 2 + k
+                for v in range(2):
+                    col = P * (g2 * 2 + v)
                     nc.tensor.transpose(
-                        out=npt[:, k * RG * 4 : (k + 1) * RG * 4].rearrange("p (c s t) -> p c s t", s=NS, t=SEG)[
-                            :, :, sg, :
-                        ],
+                        out=npt[:, k * ROWS * 4 : (k + 1) * ROWS * 4].rearrange(
+                            "p (c v s) -> p c v s", v=2, s=PIECES
+                        )[:, :, v, :],
                         in_=data[:, r, col : col + P],
                         identity=ident_bf[:],
                     )
             nc.scalar.copy(out=st[("nt", u)][:, g2, qd * 512 : (qd + 1) * 512], in_=npt[:])
 
-        def n_quantise(u):
+        def norm_quantise(u):
             ntw = work.tile([P, 2 * 512], U32, name="ntw", align_bytes=64)
             nts = work.tile([P, 2 * 512], U8, name="nts", align_bytes=64)
             quantise(nc, st[("nt", u)][:].rearrange("p g c -> p (g c)"), ntw, nts, [4096])
             st[("ntw", u)] = ntw
             st[("nts", u)] = nts
 
-        def agg_mm(u, c):
+        def agg_matmul(u, c):
             hw = st[("hw", u // 2)]
             hs = st[("hs", u // 2)]
             acc = psum.tile([P, DOUT], F32, name="acc", tag="ap", bufs=4)
@@ -307,69 +297,62 @@ def tile_gcnconvmodule_t_kernel(tc, inputs, adj, W, b, out):
         def finish(u, c0, c1):
             ot = st[("ot", u)]
             nc.scalar.activation(out=ot[:, c0:c1, :], in_=ot[:, c0:c1, :], func=ACT.Tanh)
+            row = (u % 2) * 512
             nc.sync.dma_start(
-                out=out[u // 2, (u % 2) * 512 + c0 * P : (u % 2) * 512 + c1 * P, :].rearrange(
-                    "(c p) d -> p c d", p=P
-                ),
+                out=out[u // 2, row + c0 * P : row + c1 * P, :].rearrange("(c p) d -> p c d", p=P),
                 in_=ot[:, c0:c1, :],
             )
 
-        U = 2 * B
+        def graph(g, first=0):
+            return first <= g < B
 
-        def okg(g):
-            return 0 <= g < B
+        def unit(u):
+            return 0 <= u < UNITS
 
-        def oku(u):
-            return 0 <= u < U
-
-        for k in range(-7, U + 3):
-            if oku(k - 1):
-                n_quantise(k - 1)
-            if oku(k):
-                mask(k)
+        for k in range(-9, UNITS + 2):
+            if unit(k - 1):
+                norm_quantise(k - 1)
+            if unit(k):
+                norm_rows(k)
                 for qd in range(4):
-                    n_transpose(k, 0, qd)
-                    n_transpose(k, 1, qd)
+                    norm_transpose(k, 0, qd)
+                    norm_transpose(k, 1, qd)
             if k == 2:
                 nc.vector.tensor_copy(out=bias[:], in_=b_bf[:])
             for c in range(4):
-                if oku(k - 2):
+                if unit(k - 2):
                     agg_bias(k - 2, c)
-                    if k - 2 == U - 1:
+                    if k - 2 == UNITS - 1:
                         finish(k - 2, c, c + 1)
-                if oku(k - 1):
-                    agg_mm(k - 1, c)
-            if oku(k - 2) and k - 2 < U - 1:
+                if unit(k - 1):
+                    agg_matmul(k - 1, c)
+            if unit(k - 2) and k - 2 < UNITS - 1:
                 finish(k - 2, 0, 4)
-            rows = list(range(RH)) if oku(k + 1) and not True else []
             if k % 2 == 0:
-                ga = (k + 2) // 2
-                if okg(ga):
+                if graph((k + 4) // 2):
                     for g2 in range(2):
                         for dblk in range(3):
-                            h_matmul(ga, g2, dblk)
-                    deg_b(ga)
-            if k % 2 == 0:
-                gc = (k + 4) // 2
-                if okg(gc):
-                    diag_one(gc, 0)
-                    for r in range(RH):
-                        count(gc, r)
+                            h_matmul((k + 4) // 2, g2, dblk)
+                if graph((k + 2) // 2):
+                    dinv_columns((k + 2) // 2)
+                if graph((k + 4) // 2):
+                    diag_one((k + 4) // 2, 0)
+                    for r in range(UNIT_GROUPS):
+                        count((k + 4) // 2, r)
             else:
-                gb = (k + 3) // 2
-                if okg(gb):
-                    diag_one(gb, 1)
-                    for r in range(RH, R):
-                        count(gb, r)
-                    deg_a(gb)
-                    x_quantise(gb)
-                if okg((k + 5) // 2):
+                if graph((k + 3) // 2):
+                    diag_one((k + 3) // 2, 1)
+                    for r in range(UNIT_GROUPS, GROUPS):
+                        count((k + 3) // 2, r)
+                    dinv_rows((k + 3) // 2)
+                if graph((k + 5) // 2):
+                    x_quantise((k + 5) // 2)
+                if graph((k + 7) // 2):
                     for i in range(4):
-                        x_transpose((k + 5) // 2, i)
-                if okg((k + 1) // 2):
-                    h_quantise((k + 1) // 2)
-                if okg((k + 7) // 2) and k + 7 > 0:
+                        x_transpose((k + 7) // 2, i)
+                if graph((k + 3) // 2):
+                    h_quantise((k + 3) // 2)
+                if graph((k + 7) // 2, first=1):
                     load_adj((k + 7) // 2)
-                    load_x((k + 7) // 2)
-            for j in rows:
-                outer_row(k + 1, j)
+                if graph((k + 9) // 2, first=2):
+                    load_x((k + 9) // 2)

@@ -27,6 +27,9 @@ GROUPS = N // ROWS
 UNIT_GROUPS = GROUPS // 2
 UNITS = 2 * B
 PAD = 8 * ROWS
+G_ROWS = (2, 1)
+G_FIRST = 2
+G_END = UNITS - 3
 
 
 def quantise(nc, flat, codes, scales, widths):
@@ -55,21 +58,26 @@ def tile_gcnconvmodule_t_kernel(tc, inputs, adj, W, b, out):
         def adj_view(g):
             return st[("ah", g)][:, 0 : GROUPS * PIECE].rearrange("p (r f) -> p r f", f=PIECE)
 
-        def load_adj(g):
-            st[("ah", g)] = adjp.tile([P, GROUPS * PIECE + PAD], BF16, name="ah")
+        def load_adj(g, half):
+            if half == 0:
+                st[("ah", g)] = adjp.tile([P, GROUPS * PIECE + PAD], BF16, name="ah")
             rows = adj[g].rearrange("n (s f) -> (n s) f", s=PIECES).rearrange("(r p) f -> p r f", p=P)
-            data = adj_view(g)
-            for half in range(2):
-                lo = half * UNIT_GROUPS
-                nc.sync.dma_start(out=data[:, lo : lo + UNIT_GROUPS, :], in_=rows[:, lo : lo + UNIT_GROUPS, :])
+            lo = half * UNIT_GROUPS
+            nc.sync.dma_start(out=adj_view(g)[:, lo : lo + UNIT_GROUPS, :], in_=rows[:, lo : lo + UNIT_GROUPS, :])
 
         def load_x(g):
             xt = work.tile([P, 8, DIN], BF16, name="xt")
             st[("xt", g)] = xt
             nc.sync.dma_start(out=xt[:], in_=inputs[g].rearrange("(q p) k -> p q k", p=P))
 
+        def load(g):
+            load_adj(g, 0)
+            load_x(g)
+            load_adj(g, 1)
+
+        load_adj(0, 0)
+        load_adj(0, 1)
         load_x(0)
-        load_x(1)
 
         ident_bf = const.tile([P, P], BF16, name="ident_bf")
         make_identity(nc, ident_bf[:])
@@ -77,33 +85,30 @@ def tile_gcnconvmodule_t_kernel(tc, inputs, adj, W, b, out):
         make_identity(nc, ident_f[:])
         diag_bits = const.tile([P, PIECES, ROWS], BF16, name="diag_bits")
         nc.vector.tensor_copy(out=diag_bits[:], in_=ident_bf[:].rearrange("p (c s) -> p s c", s=PIECES))
-        same_row = const.tile([P, ROWS], F32, name="same_row")
+        grp = const.tile([P, ROWS], F32, name="grp")
         nc.vector.tensor_reduce(
-            out=same_row[:], in_=ident_f[:].rearrange("p (c s) -> p c s", s=PIECES), axis=AX.X, op=ALU.add
+            out=grp[:], in_=ident_f[:].rearrange("p (c s) -> p c s", s=PIECES), axis=AX.X, op=ALU.add
         )
         pair = const.tile([P, ROWS, PIECES], F32, name="pair")
-        nc.vector.tensor_copy(out=pair[:], in_=same_row[:].unsqueeze(2).to_broadcast([P, ROWS, PIECES]))
-        parity = const.tile([P, PIECES], F32, name="parity")
-        nc.vector.tensor_reduce(
-            out=parity[:], in_=ident_f[:].rearrange("p (c s) -> p s c", s=PIECES), axis=AX.X, op=ALU.add
-        )
-        minus_half = const.tile([P, GROUPS], F32, name="minus_half")
-        nc.vector.memset(minus_half[:], -0.5)
+        nc.vector.tensor_copy(out=pair[:], in_=grp[:].unsqueeze(2).to_broadcast([P, ROWS, PIECES]))
+        mhalf = const.tile([P, GROUPS], F32, name="mhalf")
+        nc.vector.memset(mhalf[:], -0.5)
 
         w_raw = work.tile([P, 4, DOUT], BF16, name="w_raw", tag="ot", bufs=3)
         nc.sync.dma_start(
             out=w_raw[:].rearrange("p (u e) d -> p u (e d)", u=2),
             in_=W.rearrange("(u p e) d -> p u (e d)", u=2, e=2),
         )
-        load_adj(0)
         b_bf = const.tile([P, DOUT], BF16, name="b_bf")
         nc.sync.dma_start(out=b_bf[:], in_=b.partition_broadcast(P))
         bias = const.tile([P, DOUT], F32, name="bias")
-        w_grp = work.tile([P, DOUT, 4], BF16, name="w_grp", tag="nt", align_bytes=64)
-        nc.vector.tensor_copy(out=w_grp[:], in_=w_raw[:].rearrange("p t d -> p d t"))
         w_codes = const.tile([P, DOUT], U32, name="w_codes", align_bytes=64)
         w_scales = const.tile([P, DOUT], U8, name="w_scales", align_bytes=64)
-        quantise(nc, w_grp[:].rearrange("p d t -> p (d t)"), w_codes, w_scales, [1024, 512])
+
+        def w_quantise():
+            w_grp = work.tile([P, DOUT, 4], BF16, name="w_grp", tag="nt", align_bytes=64)
+            nc.vector.tensor_copy(out=w_grp[:], in_=w_raw[:].rearrange("p t d -> p d t"))
+            quantise(nc, w_grp[:].rearrange("p d t -> p (d t)"), w_codes, w_scales, [1024, 512])
 
         def x_transpose(g, i):
             if i == 0:
@@ -149,8 +154,8 @@ def tile_gcnconvmodule_t_kernel(tc, inputs, adj, W, b, out):
             )
 
         def h_quantise(g):
-            hw = small.tile([P, 2 * DOUT], U32, name="hw", align_bytes=64, bufs=4)
-            hs = small.tile([P, 2 * DOUT], U8, name="hs", align_bytes=64, bufs=4)
+            hw = small.tile([P, 2 * DOUT], U32, name="hw", align_bytes=64)
+            hs = small.tile([P, 2 * DOUT], U8, name="hs", align_bytes=64)
             quantise(nc, st[("hq", g)][:].rearrange("p g d t -> p (g d t)"), hw, hs, [2048, 1024])
             st[("hw", g)] = hw
             st[("hs", g)] = hs
@@ -194,49 +199,65 @@ def tile_gcnconvmodule_t_kernel(tc, inputs, adj, W, b, out):
             deg = small.tile([P, GROUPS], F32, name="deg")
             nc.scalar.copy(out=deg[:], in_=degp[:])
             dn = small.tile([P, GROUPS], F32, name="dn")
-            nc.gpsimd.tensor_tensor(out=dn[:], in0=deg[:], in1=minus_half[:], op=ALU.pow)
-            halves = dn[:].rearrange("p (s h a) -> p h s a", s=PIECES, h=2)
-            pick = small.tile([P, 3, PIECES, 4], F32, name="pick")
+            nc.gpsimd.tensor_tensor(out=dn[:], in0=deg[:], in1=mhalf[:], op=ALU.pow)
+            st[("dn", g)] = dn
+
+        def dinv_repeat(g):
+            rr = work.tile([P, 8, ROWS, PIECES], F32, name="rr", bufs=1)
+            nc.scalar.copy(
+                out=rr[:],
+                in_=st[("dn", g)][:]
+                .rearrange("p (s a) -> p a s", s=PIECES)
+                .unsqueeze(2)
+                .to_broadcast([P, 8, ROWS, PIECES]),
+            )
+            st[("rr", g)] = rr
+
+        def dinv_columns(g):
+            rr = st[("rr", g)]
+            db = small.tile([P, PIECE], F32, name="db")
             for h in range(2):
+                dbp = psum.tile([P, 4, P], F32, name="dbp", tag="tp")
+                for a in range(4):
+                    nc.tensor.transpose(
+                        out=dbp[:, a, :],
+                        in_=rr[:, 4 * h + a, :, :].rearrange("p c s -> p (c s)"),
+                        identity=ident_f[:],
+                    )
+                nc.scalar.copy(
+                    out=db[:, 4 * h * ROWS : (4 * h + 4) * ROWS].rearrange("p (a c) -> p a c", c=ROWS),
+                    in_=dbp[:].rearrange("p a (c s) -> p a c s", s=PIECES)[:, :, :, 0],
+                )
+            st[("db", g)] = db
+
+        def vector_rows(u):
+            return UNIT_GROUPS - G_ROWS[u % 2] if G_FIRST <= u < G_END else UNIT_GROUPS
+
+        def release_gpsimd(u):
+            if vector_rows(u) < UNIT_GROUPS:
+                st[("go", u)] = small.tile([P, 1], F32, name="go")
+                nc.vector.memset(st[("go", u)][:], 0.0)
+
+        def norm_rows_gpsimd(u):
+            g = u // 2
+            data = adj_view(g)
+            for k in range(vector_rows(u), UNIT_GROUPS):
+                r = (u % 2) * UNIT_GROUPS + k
+                og = small.tile([P, PIECE], BF16, name="og")
                 nc.gpsimd.tensor_scalar(
-                    out=pick[:, h, :, :],
-                    in0=halves[:, h, :, :],
-                    scalar1=parity[:, h : h + 1],
-                    scalar2=0.0,
+                    out=og[:],
+                    in0=st[("db", g)][:],
+                    scalar1=st[("dn", g)][:, r : r + 1],
+                    scalar2=st[("go", u)][:, 0:1],
                     op0=ALU.mult,
                     op1=ALU.add,
                 )
-            nc.gpsimd.tensor_tensor(out=pick[:, 2, :, :], in0=pick[:, 0, :, :], in1=pick[:, 1, :, :], op=ALU.add)
-            rep = work.tile([P, 4, ROWS, PIECES], F32, name="rep", bufs=1)
-            nc.gpsimd.tensor_scalar(
-                out=rep[:],
-                in0=pick[:, 2, :, :].rearrange("p s a -> p a s").unsqueeze(2).to_broadcast([P, 4, ROWS, PIECES]),
-                scalar1=1.0,
-                scalar2=0.0,
-                op0=ALU.mult,
-                op1=ALU.add,
-            )
-            st[("dn", g)] = dn
-            st[("rep", g)] = rep
-
-        def dinv_columns(g):
-            rep = st[("rep", g)]
-            db = small.tile([P, PIECE], F32, name="db")
-            dbp = psum.tile([P, 4, P], F32, name="dbp", tag="tp")
-            for a in range(4):
-                nc.tensor.transpose(
-                    out=dbp[:, a, :], in_=rep[:, a, :, :].rearrange("p c s -> p (c s)"), identity=ident_f[:]
-                )
-            nc.scalar.copy(
-                out=db[:].rearrange("p (h a c) -> p h a c", h=2, a=4),
-                in_=dbp[:].rearrange("p a (c h) -> p h a c", h=2),
-            )
-            st[("db", g)] = db
+                nc.gpsimd.tensor_tensor(out=data[:, r, :], in0=data[:, r, :], in1=og[:], op=ALU.mult)
 
         def norm_rows(u):
             g = u // 2
             data = adj_view(g)
-            for k in range(UNIT_GROUPS):
+            for k in range(vector_rows(u)):
                 r = (u % 2) * UNIT_GROUPS + k
                 nc.vector.scalar_tensor_tensor(
                     out=data[:, r, :],
@@ -309,7 +330,7 @@ def tile_gcnconvmodule_t_kernel(tc, inputs, adj, W, b, out):
         def unit(u):
             return 0 <= u < UNITS
 
-        for k in range(-9, UNITS + 2):
+        for k in range(-7, UNITS + 2):
             if unit(k - 1):
                 norm_quantise(k - 1)
             if unit(k):
@@ -319,6 +340,18 @@ def tile_gcnconvmodule_t_kernel(tc, inputs, adj, W, b, out):
                     norm_transpose(k, 1, qd)
             if k == 2:
                 nc.vector.tensor_copy(out=bias[:], in_=b_bf[:])
+            if unit(k + 1):
+                release_gpsimd(k + 1)
+            if k % 2 == 0 and graph((k + 4) // 2):
+                diag_one((k + 4) // 2, 0)
+            if k % 2 == 1 and graph((k + 3) // 2):
+                diag_one((k + 3) // 2, 1)
+            if unit(k + 1):
+                norm_rows_gpsimd(k + 1)
+            if k % 2 == 1 and graph((k + 3) // 2):
+                for r in range(UNIT_GROUPS, GROUPS):
+                    count((k + 3) // 2, r)
+                dinv_rows((k + 3) // 2)
             for c in range(4):
                 if unit(k - 2):
                     agg_bias(k - 2, c)
@@ -329,30 +362,24 @@ def tile_gcnconvmodule_t_kernel(tc, inputs, adj, W, b, out):
             if unit(k - 2) and k - 2 < UNITS - 1:
                 finish(k - 2, 0, 4)
             if k % 2 == 0:
-                if graph((k + 4) // 2):
+                if graph((k + 2) // 2):
+                    dinv_repeat((k + 2) // 2)
                     for g2 in range(2):
                         for dblk in range(3):
-                            h_matmul((k + 4) // 2, g2, dblk)
-                if graph((k + 2) // 2):
+                            h_matmul((k + 2) // 2, g2, dblk)
                     dinv_columns((k + 2) // 2)
                 if graph((k + 4) // 2):
-                    diag_one((k + 4) // 2, 0)
                     for r in range(UNIT_GROUPS):
                         count((k + 4) // 2, r)
             else:
                 if graph((k + 3) // 2):
-                    diag_one((k + 3) // 2, 1)
-                    for r in range(UNIT_GROUPS, GROUPS):
-                        count((k + 3) // 2, r)
-                    dinv_rows((k + 3) // 2)
+                    if k == -3:
+                        w_quantise()
+                    x_quantise((k + 3) // 2)
                 if graph((k + 5) // 2):
-                    x_quantise((k + 5) // 2)
-                if graph((k + 7) // 2):
                     for i in range(4):
-                        x_transpose((k + 7) // 2, i)
-                if graph((k + 3) // 2):
-                    h_quantise((k + 3) // 2)
+                        x_transpose((k + 5) // 2, i)
+                if graph((k + 1) // 2):
+                    h_quantise((k + 1) // 2)
                 if graph((k + 7) // 2, first=1):
-                    load_adj((k + 7) // 2)
-                if graph((k + 9) // 2, first=2):
-                    load_x((k + 9) // 2)
+                    load((k + 7) // 2)

@@ -13,23 +13,15 @@ U8 = mybir.dt.uint8
 FP8X4 = mybir.dt.float8_e4m3fn_x4
 ALU = mybir.AluOpType
 ACT = mybir.ActivationFunctionType
-AX = mybir.AxisListType
 
 P = 128
 B = 8
 N = 1024
 DIN = 512
 DOUT = 384
-PIECES = 2
-ROWS = P // PIECES
-PIECE = N // PIECES
-GROUPS = N // ROWS
-UNIT_GROUPS = GROUPS // 2
+Q = N // P
+UQ = Q // 2
 UNITS = 2 * B
-PAD = 8 * ROWS
-G_ROWS = (2, 1)
-G_FIRST = 2
-G_END = UNITS - 3
 
 
 def quantise(nc, flat, codes, scales, widths):
@@ -47,33 +39,34 @@ def tile_gcnconvmodule_t_kernel(tc, inputs, adj, W, b, out):
     nc = tc.nc
     with ExitStack() as ctx:
         const = ctx.enter_context(tc.tile_pool(name="const", bufs=1))
-        adjp = ctx.enter_context(tc.tile_pool(name="adjp", bufs=4))
+        adjp = ctx.enter_context(tc.tile_pool(name="adjp", bufs=3))
         work = ctx.enter_context(tc.tile_pool(name="work", bufs=2))
         small = ctx.enter_context(tc.tile_pool(name="small", bufs=3))
-        psum = ctx.enter_context(tc.psum_pool(name="psum", bufs=4))
+        psum = ctx.enter_context(tc.psum_pool(name="psum", bufs=2))
         ctx.enter_context(tc.manual_schedule())
 
         st = {}
 
         def adj_view(g):
-            return st[("ah", g)][:, 0 : GROUPS * PIECE].rearrange("p (r f) -> p r f", f=PIECE)
+            return st[("ah", g)][:, 0 : Q * N].rearrange("p (q m) -> p q m", m=N)
+
+        def adj_words(g):
+            return st[("ah", g)][:].bitcast(F32)[:, 0 : Q * N // 2].rearrange("p (q w) -> p q w", w=N // 2)
 
         def load_adj(g, half):
             if half == 0:
-                st[("ah", g)] = adjp.tile([P, GROUPS * PIECE + PAD], BF16, name="ah")
-            rows = adj[g].rearrange("n (s f) -> (n s) f", s=PIECES).rearrange("(r p) f -> p r f", p=P)
-            lo = half * UNIT_GROUPS
-            nc.sync.dma_start(out=adj_view(g)[:, lo : lo + UNIT_GROUPS, :], in_=rows[:, lo : lo + UNIT_GROUPS, :])
+                st[("ah", g)] = adjp.tile([P, Q * (N + P)], BF16, name="ah")
+            rows = adj[g].rearrange("(q p) m -> p q m", p=P)
+            lo = half * UQ
+            nc.sync.dma_start(out=adj_view(g)[:, lo : lo + UQ, :], in_=rows[:, lo : lo + UQ, :])
 
         def load_x(g):
             xt = work.tile([P, 8, DIN], BF16, name="xt")
             st[("xt", g)] = xt
-            nc.sync.dma_start(out=xt[:], in_=inputs[g].rearrange("(q p) k -> p q k", p=P))
-
-        def load(g):
-            load_adj(g, 0)
-            load_x(g)
-            load_adj(g, 1)
+            nc.sync.dma_start(
+                out=xt[:].rearrange("p (a e) k -> p a (e k)", e=2),
+                in_=inputs[g].rearrange("(a p e) k -> p a (e k)", p=P, e=2),
+            )
 
         load_adj(0, 0)
         load_adj(0, 1)
@@ -83,15 +76,9 @@ def tile_gcnconvmodule_t_kernel(tc, inputs, adj, W, b, out):
         make_identity(nc, ident_bf[:])
         ident_f = const.tile([P, P], F32, name="ident_f")
         make_identity(nc, ident_f[:])
-        diag_bits = const.tile([P, PIECES, ROWS], BF16, name="diag_bits")
-        nc.vector.tensor_copy(out=diag_bits[:], in_=ident_bf[:].rearrange("p (c s) -> p s c", s=PIECES))
-        grp = const.tile([P, ROWS], F32, name="grp")
-        nc.vector.tensor_reduce(
-            out=grp[:], in_=ident_f[:].rearrange("p (c s) -> p c s", s=PIECES), axis=AX.X, op=ALU.add
-        )
-        pair = const.tile([P, ROWS, PIECES], F32, name="pair")
-        nc.vector.tensor_copy(out=pair[:], in_=grp[:].unsqueeze(2).to_broadcast([P, ROWS, PIECES]))
-        mhalf = const.tile([P, GROUPS], F32, name="mhalf")
+        ones = const.tile([P, 1], BF16, name="ones")
+        nc.vector.memset(ones[:], 1.0)
+        mhalf = const.tile([P, UQ], F32, name="mhalf")
         nc.vector.memset(mhalf[:], -0.5)
 
         w_raw = work.tile([P, 4, DOUT], BF16, name="w_raw", tag="ot", bufs=3)
@@ -100,13 +87,18 @@ def tile_gcnconvmodule_t_kernel(tc, inputs, adj, W, b, out):
             in_=W.rearrange("(u p e) d -> p u (e d)", u=2, e=2),
         )
         b_bf = const.tile([P, DOUT], BF16, name="b_bf")
+        load_adj(1, 0)
+        load_adj(1, 1)
+        load_x(1)
         nc.sync.dma_start(out=b_bf[:], in_=b.partition_broadcast(P))
+        load_adj(2, 0)
+        load_adj(2, 1)
         bias = const.tile([P, DOUT], F32, name="bias")
         w_codes = const.tile([P, DOUT], U32, name="w_codes", align_bytes=64)
         w_scales = const.tile([P, DOUT], U8, name="w_scales", align_bytes=64)
 
         def w_quantise():
-            w_grp = work.tile([P, DOUT, 4], BF16, name="w_grp", tag="nt", align_bytes=64)
+            w_grp = work.tile([P, DOUT, 4], BF16, name="w_grp", align_bytes=64, bufs=1)
             nc.vector.tensor_copy(out=w_grp[:], in_=w_raw[:].rearrange("p t d -> p d t"))
             quantise(nc, w_grp[:].rearrange("p d t -> p (d t)"), w_codes, w_scales, [1024, 512])
 
@@ -132,14 +124,15 @@ def tile_gcnconvmodule_t_kernel(tc, inputs, adj, W, b, out):
             st[("xw", g)] = xw
             st[("xs", g)] = xs
 
-        def h_matmul(g, g2, dblk):
-            if g2 == 0 and dblk == 0:
+        def h_matmul(g, i):
+            g2, dblk = divmod(i, 3)
+            if i == 0:
                 st[("hq", g)] = work.tile([P, 2, DOUT, 4], BF16, name="hq", align_bytes=64)
             xw = st[("xw", g)]
             xs = st[("xs", g)]
             hp = psum.tile([P, 4, P], F32, name="hp", tag="tp")
             for t in range(4):
-                q = 4 * (t % 2) + 2 * g2 + t // 2
+                q = 4 * g2 + t
                 nc.tensor.matmul_mx(
                     out=hp[:, t, :],
                     lhsT=xw[:, q * P : (q + 1) * P].bitcast(FP8X4),
@@ -160,143 +153,129 @@ def tile_gcnconvmodule_t_kernel(tc, inputs, adj, W, b, out):
             st[("hw", g)] = hw
             st[("hs", g)] = hs
 
-        def diag_one(g, s):
+        def diagonal(g, h):
             ah32 = st[("ah", g)][:].bitcast(I32)
-            d32 = diag_bits[:].bitcast(I32)
-            step = (PIECE + ROWS) // 2
-            base = 8 * s * (PIECE // 2)
-            view = ah32[:, base : base + 8 * step].rearrange("p (i w) -> p i w", w=step)[:, :, 0 : ROWS // 2]
+            step = (N + P) // 2
+            base = h * UQ * step
+            diag = ah32[:, base : base + UQ * step].rearrange("p (i w) -> p i w", w=step)[:, :, 0 : P // 2]
             nc.vector.tensor_tensor(
-                out=view,
-                in0=view,
-                in1=d32[:, s, :].unsqueeze(1).to_broadcast([P, 8, ROWS // 2]),
+                out=diag,
+                in0=diag,
+                in1=ident_bf[:].bitcast(I32).unsqueeze(1).to_broadcast([P, UQ, P // 2]),
                 op=ALU.bitwise_or,
             )
 
-        def count(g, r):
-            if r == 0:
-                st[("part", g)] = small.tile([P, GROUPS], F32, name="part")
-            data = adj_view(g)
+        def pair_transpose(words0, words1, g2):
+            vt = psum.tile([P, 2, 256], F32, name="vt", tag="vp", bufs=3)
+            for u in range(2):
+                for j, words in enumerate((words0, words1)):
+                    lo = g2 * 256 + u * P
+                    nc.tensor.transpose(
+                        out=vt[:, u, j * P : (j + 1) * P], in_=words[:, lo : lo + P], identity=ident_f[:]
+                    )
+            return vt[:].rearrange("p u n -> p (u n)").bitcast(BF16).rearrange("p (u n e) -> p n u e", u=2, e=2)
+
+        def at_view(g, h, i):
+            pair, g2 = divmod(i, 2)
+            n0 = h * 512 + pair * 256
+            return st[("at", g)][:, g2, n0 : n0 + 256, :].rearrange("p n (u e) -> p n u e", e=2)
+
+        def mask_fill(g, h, i):
+            pair, g2 = divmod(i, 2)
+            words = adj_words(g)
+            q = h * UQ + 2 * pair
+            st[("mv", g, h, i)] = pair_transpose(words[:, q, :], words[:, q + 1, :], g2)
+
+        def mask(g, h, i):
+            if h == 0 and i == 0:
+                st[("at", g)] = work.tile([P, 2, N, 4], BF16, name="at", align_bytes=64, bufs=3)
             nc.vector.tensor_scalar(
-                out=data[:, r, :],
-                in0=data[:, r, :],
+                out=at_view(g, h, i),
+                in0=st[("mv", g, h, i)],
                 scalar1=0.0,
                 scalar2=None,
                 op0=ALU.not_equal,
-                op1=ALU.add,
-                accum_out=st[("part", g)][:, r : r + 1],
             )
 
-        def dinv_rows(g):
-            degp = psum.tile([P, GROUPS], F32, name="degp", tag="tp")
-            nc.tensor.matmul(
-                out=degp[:],
-                lhsT=pair[:].rearrange("p c s -> p (c s)"),
-                rhs=st[("part", g)][:],
-                start=True,
-                stop=True,
-            )
-            deg = small.tile([P, GROUPS], F32, name="deg")
-            nc.scalar.copy(out=deg[:], in_=degp[:])
-            dn = small.tile([P, GROUPS], F32, name="dn")
-            nc.gpsimd.tensor_tensor(out=dn[:], in0=deg[:], in1=mhalf[:], op=ALU.pow)
-            st[("dn", g)] = dn
-
-        def dinv_repeat(g):
-            rr = work.tile([P, 8, ROWS, PIECES], F32, name="rr", bufs=1)
-            nc.scalar.copy(
-                out=rr[:],
-                in_=st[("dn", g)][:]
-                .rearrange("p (s a) -> p a s", s=PIECES)
-                .unsqueeze(2)
-                .to_broadcast([P, 8, ROWS, PIECES]),
-            )
-            st[("rr", g)] = rr
-
-        def dinv_columns(g):
-            rr = st[("rr", g)]
-            db = small.tile([P, PIECE], F32, name="db")
-            for h in range(2):
-                dbp = psum.tile([P, 4, P], F32, name="dbp", tag="tp")
-                for a in range(4):
-                    nc.tensor.transpose(
-                        out=dbp[:, a, :],
-                        in_=rr[:, 4 * h + a, :, :].rearrange("p c s -> p (c s)"),
-                        identity=ident_f[:],
+        def dinv_rows(g, h):
+            at = st[("at", g)]
+            degp = psum.tile([P, UQ], F32, name="degp", tag="tp")
+            for j in range(UQ):
+                q = h * UQ + j
+                for i in range(8):
+                    nc.tensor.matmul(
+                        out=degp[:, j : j + 1],
+                        lhsT=at[:, i // 4, q * P : (q + 1) * P, i % 4],
+                        rhs=ones[:],
+                        start=(i == 0),
+                        stop=(i == 7),
                     )
-                nc.scalar.copy(
-                    out=db[:, 4 * h * ROWS : (4 * h + 4) * ROWS].rearrange("p (a c) -> p a c", c=ROWS),
-                    in_=dbp[:].rearrange("p a (c s) -> p a c s", s=PIECES)[:, :, :, 0],
-                )
-            st[("db", g)] = db
+            deg = small.tile([P, UQ], F32, name="deg")
+            nc.scalar.copy(out=deg[:], in_=degp[:])
+            if h == 0:
+                st[("dn", g)] = small.tile([P, Q], F32, name="dn", bufs=4)
+            nc.gpsimd.tensor_tensor(
+                out=st[("dn", g)][:, h * UQ : (h + 1) * UQ], in0=deg[:], in1=mhalf[:], op=ALU.pow
+            )
 
-        def vector_rows(u):
-            return UNIT_GROUPS - G_ROWS[u % 2] if G_FIRST <= u < G_END else UNIT_GROUPS
+        def dinv_columns(g, h):
+            if h == 0:
+                st[("db", g)] = work.tile([P, N], F32, name="db")
+            dn = st[("dn", g)]
+            dbp = psum.tile([P, 512], F32, name="dbp", tag="tp")
+            for i in range(4):
+                q = 4 * h + i
+                nc.tensor.transpose(
+                    out=dbp[:, i * P : (i + 1) * P],
+                    in_=dn[:, q : q + 1].to_broadcast([P, P]),
+                    identity=ident_f[:],
+                )
+            nc.scalar.copy(out=st[("db", g)][:, h * 512 : (h + 1) * 512], in_=dbp[:])
 
         def release_gpsimd(u):
-            if vector_rows(u) < UNIT_GROUPS:
-                st[("go", u)] = small.tile([P, 1], F32, name="go")
-                nc.vector.memset(st[("go", u)][:], 0.0)
+            st[("go", u)] = small.tile([P, 1], F32, name="go")
+            nc.vector.memset(st[("go", u)][:], 0.0)
 
-        def norm_rows_gpsimd(u):
+        def on_scalar(j):
+            return j % 2 == 0
+
+        def outer_row(u, j):
             g = u // 2
-            data = adj_view(g)
-            for k in range(vector_rows(u), UNIT_GROUPS):
-                r = (u % 2) * UNIT_GROUPS + k
-                og = small.tile([P, PIECE], BF16, name="og")
+            q = (u % 2) * UQ + j
+            dt = small.tile([P, N], BF16, name="dt", bufs=2 * UQ)
+            db = st[("db", g)]
+            dn = st[("dn", g)][:, q : q + 1]
+            if on_scalar(j):
+                nc.scalar.activation(out=dt[:], in_=db[:], func=ACT.Copy, scale=dn)
+            else:
                 nc.gpsimd.tensor_scalar(
-                    out=og[:],
-                    in0=st[("db", g)][:],
-                    scalar1=st[("dn", g)][:, r : r + 1],
-                    scalar2=st[("go", u)][:, 0:1],
-                    op0=ALU.mult,
-                    op1=ALU.add,
+                    out=dt[:], in0=db[:], scalar1=dn, scalar2=st[("go", u)][:, 0:1], op0=ALU.mult, op1=ALU.add
                 )
-                nc.gpsimd.tensor_tensor(out=data[:, r, :], in0=data[:, r, :], in1=og[:], op=ALU.mult)
+            st[("dt", u, j)] = dt
 
-        def norm_rows(u):
-            g = u // 2
-            data = adj_view(g)
-            for k in range(vector_rows(u)):
-                r = (u % 2) * UNIT_GROUPS + k
-                nc.vector.scalar_tensor_tensor(
-                    out=data[:, r, :],
-                    in0=st[("db", g)][:],
-                    scalar=st[("dn", g)][:, r : r + 1],
-                    in1=data[:, r, :],
-                    op0=ALU.mult,
-                    op1=ALU.mult,
-                )
+        def norm_fill(u, i):
+            pair, g2 = divmod(i, 2)
+            words = [st[("dt", u, 2 * pair + j)][:].bitcast(F32) for j in range(2)]
+            st[("nv", u, i)] = pair_transpose(words[0], words[1], g2)
 
-        def norm_transpose(u, g2, qd):
-            if g2 == 0 and qd == 0:
-                st[("nt", u)] = work.tile([P, 2, 2048], BF16, name="nt", align_bytes=64)
-            data = adj_view(u // 2)
-            npt = psum.tile([P, 512], BF16, name="npt", tag="tp")
-            for k in range(2):
-                r = (u % 2) * UNIT_GROUPS + qd * 2 + k
-                for v in range(2):
-                    col = P * (g2 * 2 + v)
-                    nc.tensor.transpose(
-                        out=npt[:, k * ROWS * 4 : (k + 1) * ROWS * 4].rearrange(
-                            "p (c v s) -> p c v s", v=2, s=PIECES
-                        )[:, :, v, :],
-                        in_=data[:, r, col : col + P],
-                        identity=ident_bf[:],
-                    )
-            nc.scalar.copy(out=st[("nt", u)][:, g2, qd * 512 : (qd + 1) * 512], in_=npt[:])
+        def norm(u, i):
+            at = at_view(u // 2, u % 2, i)
+            nc.vector.tensor_tensor(out=at, in0=st[("nv", u, i)], in1=at, op=ALU.mult)
 
         def norm_quantise(u):
             ntw = work.tile([P, 2 * 512], U32, name="ntw", align_bytes=64)
             nts = work.tile([P, 2 * 512], U8, name="nts", align_bytes=64)
-            quantise(nc, st[("nt", u)][:].rearrange("p g c -> p (g c)"), ntw, nts, [4096])
+            lo = (u % 2) * 512
+            for g2 in range(2):
+                flat = st[("at", u // 2)][:, g2, lo : lo + 512, :].rearrange("p n t -> p (n t)")
+                quantise(nc, flat, ntw[:, g2 * 512 : (g2 + 1) * 512], nts[:, g2 * 512 : (g2 + 1) * 512], [2048])
             st[("ntw", u)] = ntw
             st[("nts", u)] = nts
 
         def agg_matmul(u, c):
             hw = st[("hw", u // 2)]
             hs = st[("hs", u // 2)]
-            acc = psum.tile([P, DOUT], F32, name="acc", tag="ap", bufs=4)
+            acc = psum.tile([P, DOUT], F32, name="acc", tag="ap", bufs=3)
             st[("acc", u, c)] = acc
             for lo, hi in ((0, 256), (256, 384)):
                 for g2 in range(2):
@@ -324,62 +303,121 @@ def tile_gcnconvmodule_t_kernel(tc, inputs, adj, W, b, out):
                 in_=ot[:, c0:c1, :],
             )
 
-        def graph(g, first=0):
-            return first <= g < B
+        LOOK = 3
+
+        def graph(g):
+            return 0 <= g < B
 
         def unit(u):
             return 0 <= u < UNITS
 
-        for k in range(-7, UNITS + 2):
-            if unit(k - 1):
-                norm_quantise(k - 1)
-            if unit(k):
-                norm_rows(k)
-                for qd in range(4):
-                    norm_transpose(k, 0, qd)
-                    norm_transpose(k, 1, qd)
-            if k == 2:
-                nc.vector.tensor_copy(out=bias[:], in_=b_bf[:])
-            if unit(k + 1):
-                release_gpsimd(k + 1)
-            if k % 2 == 0 and graph((k + 4) // 2):
-                diag_one((k + 4) // 2, 0)
-            if k % 2 == 1 and graph((k + 3) // 2):
-                diag_one((k + 3) // 2, 1)
-            if unit(k + 1):
-                norm_rows_gpsimd(k + 1)
-            if k % 2 == 1 and graph((k + 3) // 2):
-                for r in range(UNIT_GROUPS, GROUPS):
-                    count((k + 3) // 2, r)
-                dinv_rows((k + 3) // 2)
-            for c in range(4):
-                if unit(k - 2):
-                    agg_bias(k - 2, c)
-                    if k - 2 == UNITS - 1:
-                        finish(k - 2, c, c + 1)
-                if unit(k - 1):
-                    agg_matmul(k - 1, c)
-            if unit(k - 2) and k - 2 < UNITS - 1:
-                finish(k - 2, 0, 4)
+        def run(calls):
+            for call in calls:
+                call[0](*call[1:])
+
+        def stream(fills, reads, between):
+            for i in range(len(reads)):
+                run([reads[i]])
+                run(fills[i + LOOK : i + LOOK + 1])
+                run(between.get(i, []))
+
+        def mask_calls(g, h):
+            return [(mask_fill, g, h, i) for i in range(4)], [(mask, g, h, i) for i in range(4)]
+
+        diagonal(0, 0)
+        f00, r00 = mask_calls(0, 0)
+        f01, r01 = mask_calls(0, 1)
+        run(f00[0:LOOK])
+        stream(f00 + f01, r00 + r01, {0: [(diagonal, 0, 1)], 5: [(dinv_rows, 0, 0)], 7: [(dinv_rows, 0, 1)]})
+        w_quantise()
+        run([(x_transpose, 0, i) for i in range(4)])
+        load_x(2)
+        x_quantise(0)
+        diagonal(1, 0)
+        f10, r10 = mask_calls(1, 0)
+        run(f10[0:LOOK])
+        dinv_columns(0, 0)
+        dinv_columns(0, 1)
+        release_gpsimd(0)
+        run([(outer_row, 0, j) for j in range(UQ)])
+        diagonal(1, 1)
+        stream(f10, r10, {1: [(h_matmul, 0, i) for i in range(3)], 3: [(h_matmul, 0, i) for i in range(3, 6)]})
+        f11, r11 = mask_calls(1, 1)
+        run(f11[0:LOOK])
+        stream(f11, r11, {0: [(dinv_rows, 1, 0)]})
+        run([(x_transpose, 1, i) for i in range(4)])
+        for h in range(2):
+            load_adj(3, h)
+        load_x(3)
+        h_quantise(0)
+        x_quantise(1)
+        nc.vector.tensor_copy(out=bias[:], in_=b_bf[:])
+        diagonal(2, 0)
+
+        for k in range(UNITS + 1):
+            if k % 2 == 1 and (k + 7) // 2 < B:
+                g = (k + 7) // 2
+                load_x(g)
+                load_adj(g, 0)
+                load_adj(g, 1)
+            fills = []
+            reads = []
+            for i in range(4):
+                if graph((k + 4) // 2):
+                    fills.append((mask_fill, (k + 4) // 2, k % 2, i))
+                    reads.append((mask, (k + 4) // 2, k % 2, i))
+                if unit(k):
+                    fills.append((norm_fill, k, i))
+                    reads.append((norm, k, i))
+            between = {}
             if k % 2 == 0:
                 if graph((k + 2) // 2):
-                    dinv_repeat((k + 2) // 2)
-                    for g2 in range(2):
-                        for dblk in range(3):
-                            h_matmul((k + 2) // 2, g2, dblk)
-                    dinv_columns((k + 2) // 2)
-                if graph((k + 4) // 2):
-                    for r in range(UNIT_GROUPS):
-                        count((k + 4) // 2, r)
+                    g = (k + 2) // 2
+                    between = {i: [(h_matmul, g, i)] for i in range(6)}
+                    between[6] = [(dinv_columns, g, 0)]
+                    between[7] = [(dinv_columns, g, 1)]
+            elif graph((k + 5) // 2):
+                between = {2 * i: [(x_transpose, (k + 5) // 2, i)] for i in range(4)}
+            n = len(reads)
+            if n == 4:
+                between = {i: between.get(2 * i, []) + between.get(2 * i + 1, []) for i in range(4)}
+            if n > 0 and unit(k + 1):
+                row = [j for j in range(UQ) if on_scalar(j)]
+                for i, j in enumerate(row):
+                    between.setdefault(n // 2 - 2 + i * n // 4, []).append((outer_row, k + 1, j))
+            run(fills[0:LOOK])
+            if unit(k - 2):
+                finish(k - 2, 0, 4)
+            if k % 2 == 0 and graph((k + 2) // 2):
+                dinv_rows((k + 2) // 2, 1)
+            if k % 2 == 1 and graph((k + 3) // 2):
+                dinv_rows((k + 3) // 2, 0)
+            if unit(k - 1):
+                norm_quantise(k - 1)
+                for c in range(3):
+                    agg_matmul(k - 1, c)
+            if graph((k + 5) // 2):
+                diagonal((k + 5) // 2, (k + 1) % 2)
+            if k == 0:
+                run([(x_transpose, 2, i) for i in range(4)])
+                x_quantise(2)
+            elif k % 2 == 0 and graph((k + 4) // 2):
+                x_quantise((k + 4) // 2)
+            if k % 2 == 1 and graph((k + 1) // 2):
+                h_quantise((k + 1) // 2)
+            if unit(k + 1):
+                release_gpsimd(k + 1)
+                run([(outer_row, k + 1, j) for j in range(UQ) if not on_scalar(j)])
+            biases = [(agg_bias, k - 1, c) for c in range(4)] if unit(k - 1) else []
+            if biases:
+                biases.insert(1, (agg_matmul, k - 1, 3))
+            if n > 0:
+                between.setdefault(n // 2 - 1, []).extend(biases[0:2])
+                stream(fills, reads, between)
+                run(biases[2:])
             else:
-                if graph((k + 3) // 2):
-                    if k == -3:
-                        w_quantise()
-                    x_quantise((k + 3) // 2)
-                if graph((k + 5) // 2):
-                    for i in range(4):
-                        x_transpose((k + 5) // 2, i)
-                if graph((k + 1) // 2):
-                    h_quantise((k + 1) // 2)
-                if graph((k + 7) // 2, first=1):
-                    load((k + 7) // 2)
+                for c in range(4):
+                    agg_bias(k - 1, c)
+                    if c == 0:
+                        agg_matmul(k - 1, 3)
+                    finish(k - 1, c, c + 1)

@@ -13,6 +13,7 @@ U8 = mybir.dt.uint8
 FP8X4 = mybir.dt.float8_e4m3fn_x4
 ALU = mybir.AluOpType
 ACT = mybir.ActivationFunctionType
+AX = mybir.AxisListType
 
 P = 128
 B = 8
@@ -78,6 +79,16 @@ def tile_gcnconvmodule_t_kernel(tc, inputs, adj, W, b, out):
         make_identity(nc, ident_f[:])
         ones = const.tile([P, 1], BF16, name="ones")
         nc.vector.memset(ones[:], 1.0)
+        fold = const.tile([P, 32], F32, name="fold")
+        nc.vector.tensor_reduce(
+            out=fold[:], in_=ident_f[:].rearrange("p (j t) -> p j t", t=4), axis=AX.X, op=ALU.add
+        )
+        spread = const.tile([P, 4 * (P + 32)], BF16, name="spread")
+        nc.vector.memset(spread[:], 0.0)
+        nc.vector.tensor_copy(
+            out=spread[:].rearrange("p (i w) -> p i w", w=P + 32)[:, :, 0:32],
+            in_=fold[:].unsqueeze(1).to_broadcast([P, 4, 32]),
+        )
         mhalf = const.tile([P, UQ], F32, name="mhalf")
         nc.vector.memset(mhalf[:], -0.5)
 
@@ -197,19 +208,34 @@ def tile_gcnconvmodule_t_kernel(tc, inputs, adj, W, b, out):
                 op0=ALU.not_equal,
             )
 
-        def dinv_rows(g, h):
+        def dinv_part(g, h):
             at = st[("at", g)]
-            degp = psum.tile([P, UQ], F32, name="degp", tag="tp")
-            for j in range(UQ):
-                q = h * UQ + j
-                for i in range(8):
+            partp = psum.tile([P, 16], F32, name="partp", tag="tp")
+            for b32 in range(16):
+                n0 = h * 512 + b32 * 32
+                for g2 in range(2):
                     nc.tensor.matmul(
-                        out=degp[:, j : j + 1],
-                        lhsT=at[:, i // 4, q * P : (q + 1) * P, i % 4],
+                        out=partp[:, b32 : b32 + 1],
+                        lhsT=at[:, g2, n0 : n0 + 32, :].rearrange("p n t -> p (n t)"),
                         rhs=ones[:],
-                        start=(i == 0),
-                        stop=(i == 7),
+                        start=(g2 == 0),
+                        stop=(g2 == 1),
                     )
+            part = small.tile([P, 16], BF16, name="part")
+            nc.scalar.copy(out=part[:], in_=partp[:])
+            st[("part", g, h)] = part
+
+        def dinv_rows(g, h):
+            part = st[("part", g, h)][:].rearrange("p (q i) -> p q i", i=4)
+            degp = psum.tile([P, UQ], F32, name="degp", tag="tp")
+            for i in range(4):
+                nc.tensor.matmul(
+                    out=degp[:],
+                    lhsT=spread[:, i * P : (i + 1) * P],
+                    rhs=part[:, :, i],
+                    start=(i == 0),
+                    stop=(i == 3),
+                )
             deg = small.tile([P, UQ], F32, name="deg")
             nc.scalar.copy(out=deg[:], in_=degp[:])
             if h == 0:
@@ -328,23 +354,32 @@ def tile_gcnconvmodule_t_kernel(tc, inputs, adj, W, b, out):
         f00, r00 = mask_calls(0, 0)
         f01, r01 = mask_calls(0, 1)
         run(f00[0:LOOK])
-        stream(f00 + f01, r00 + r01, {0: [(diagonal, 0, 1)], 5: [(dinv_rows, 0, 0)], 7: [(dinv_rows, 0, 1)]})
-        w_quantise()
-        run([(x_transpose, 0, i) for i in range(4)])
+        stream(
+            f00 + f01,
+            r00 + r01,
+            {
+                0: [(diagonal, 0, 1)],
+                3: [(dinv_part, 0, 0)],
+                5: [(dinv_rows, 0, 0)],
+                6: [(x_transpose, 0, 0), (x_transpose, 0, 1)],
+                7: [(dinv_part, 0, 1), (x_transpose, 0, 2), (dinv_rows, 0, 1), (x_transpose, 0, 3)],
+            },
+        )
         load_x(2)
-        x_quantise(0)
+        w_quantise()
         diagonal(1, 0)
         f10, r10 = mask_calls(1, 0)
         run(f10[0:LOOK])
         dinv_columns(0, 0)
         dinv_columns(0, 1)
+        x_quantise(0)
         release_gpsimd(0)
         run([(outer_row, 0, j) for j in range(UQ)])
         diagonal(1, 1)
-        stream(f10, r10, {1: [(h_matmul, 0, i) for i in range(3)], 3: [(h_matmul, 0, i) for i in range(3, 6)]})
+        stream(f10, r10, {1: [(h_matmul, 0, i) for i in range(2)]})
         f11, r11 = mask_calls(1, 1)
         run(f11[0:LOOK])
-        stream(f11, r11, {0: [(dinv_rows, 1, 0)]})
+        stream(f11, r11, {0: [(h_matmul, 0, i) for i in range(2, 6)], 3: [(dinv_part, 1, 0), (dinv_rows, 1, 0)]})
         run([(x_transpose, 1, i) for i in range(4)])
         for h in range(2):
             load_adj(3, h)
@@ -373,29 +408,33 @@ def tile_gcnconvmodule_t_kernel(tc, inputs, adj, W, b, out):
             if k % 2 == 0:
                 if graph((k + 2) // 2):
                     g = (k + 2) // 2
-                    between = {i: [(h_matmul, g, i)] for i in range(6)}
+                    between[0] = [(h_matmul, g, 0), (h_matmul, g, 1)]
+                    for i in range(2, 6):
+                        between[i] = [(h_matmul, g, i)]
                     between[6] = [(dinv_columns, g, 0)]
                     between[7] = [(dinv_columns, g, 1)]
             elif graph((k + 5) // 2):
-                between = {2 * i: [(x_transpose, (k + 5) // 2, i)] for i in range(4)}
+                g = (k + 5) // 2
+                between = {0: [(x_transpose, g, 0), (x_transpose, g, 1)], 2: [(x_transpose, g, 2)], 4: [(x_transpose, g, 3)]}
             n = len(reads)
             if n == 4:
                 between = {i: between.get(2 * i, []) + between.get(2 * i + 1, []) for i in range(4)}
-            if n > 0 and unit(k + 1):
-                row = [j for j in range(UQ) if on_scalar(j)]
-                for i, j in enumerate(row):
-                    between.setdefault(n // 2 - 2 + i * n // 4, []).append((outer_row, k + 1, j))
             run(fills[0:LOOK])
             if unit(k - 2):
                 finish(k - 2, 0, 4)
-            if k % 2 == 0 and graph((k + 2) // 2):
-                dinv_rows((k + 2) // 2, 1)
-            if k % 2 == 1 and graph((k + 3) // 2):
-                dinv_rows((k + 3) // 2, 0)
+            if unit(k + 1):
+                outer_row(k + 1, 0)
+            dinv = ((k + 3) // 2, (k + 1) % 2)
+            if graph(dinv[0]):
+                dinv_part(*dinv)
+            if unit(k + 1):
+                outer_row(k + 1, 2)
             if unit(k - 1):
                 norm_quantise(k - 1)
                 for c in range(3):
                     agg_matmul(k - 1, c)
+            if graph(dinv[0]):
+                dinv_rows(*dinv)
             if graph((k + 5) // 2):
                 diagonal((k + 5) // 2, (k + 1) % 2)
             if k == 0:
@@ -407,7 +446,8 @@ def tile_gcnconvmodule_t_kernel(tc, inputs, adj, W, b, out):
                 h_quantise((k + 1) // 2)
             if unit(k + 1):
                 release_gpsimd(k + 1)
-                run([(outer_row, k + 1, j) for j in range(UQ) if not on_scalar(j)])
+                outer_row(k + 1, 1)
+                outer_row(k + 1, 3)
             biases = [(agg_bias, k - 1, c) for c in range(4)] if unit(k - 1) else []
             if biases:
                 biases.insert(1, (agg_matmul, k - 1, 3))

@@ -43,23 +43,24 @@ def tile_gcnconvmodule_t_kernel(tc, inputs, adj, W, b, out):
         adjp = ctx.enter_context(tc.tile_pool(name="adjp", bufs=3))
         work = ctx.enter_context(tc.tile_pool(name="work", bufs=2))
         small = ctx.enter_context(tc.tile_pool(name="small", bufs=3))
-        psum = ctx.enter_context(tc.psum_pool(name="psum", bufs=2))
+        psum = ctx.enter_context(tc.psum_pool(name="psum", bufs=3))
         ctx.enter_context(tc.manual_schedule())
 
         st = {}
 
         def adj_view(g):
-            return st[("ah", g)][:, 0 : Q * N].rearrange("p (q m) -> p q m", m=N)
+            return st[("ah", g)][:].rearrange("p (q m) -> p q m", m=N)
 
         def adj_words(g):
-            return st[("ah", g)][:].bitcast(F32)[:, 0 : Q * N // 2].rearrange("p (q w) -> p q w", w=N // 2)
+            return st[("ah", g)][:].bitcast(F32).rearrange("p (q w) -> p q w", w=N // 2)
 
-        def load_adj(g, half):
+        def load_adj(g, half, pieces=1):
             if half == 0:
-                st[("ah", g)] = adjp.tile([P, Q * (N + P)], BF16, name="ah")
+                st[("ah", g)] = adjp.tile([P, Q * N], BF16, name="ah")
             rows = adj[g].rearrange("(q p) m -> p q m", p=P)
-            lo = half * UQ
-            nc.sync.dma_start(out=adj_view(g)[:, lo : lo + UQ, :], in_=rows[:, lo : lo + UQ, :])
+            step = UQ // pieces
+            for lo in range(half * UQ, (half + 1) * UQ, step):
+                nc.sync.dma_start(out=adj_view(g)[:, lo : lo + step, :], in_=rows[:, lo : lo + step, :])
 
         def load_x(g):
             xt = work.tile([P, 8, DIN], BF16, name="xt")
@@ -69,8 +70,8 @@ def tile_gcnconvmodule_t_kernel(tc, inputs, adj, W, b, out):
                 in_=inputs[g].rearrange("(a p e) k -> p a (e k)", p=P, e=2),
             )
 
-        load_adj(0, 0)
-        load_adj(0, 1)
+        load_adj(0, 0, 2)
+        load_adj(0, 1, 2)
         load_x(0)
 
         ident_bf = const.tile([P, P], BF16, name="ident_bf")
@@ -165,16 +166,17 @@ def tile_gcnconvmodule_t_kernel(tc, inputs, adj, W, b, out):
             st[("hs", g)] = hs
 
         def diagonal(g, h):
-            ah32 = st[("ah", g)][:].bitcast(I32)
-            step = (N + P) // 2
-            base = h * UQ * step
-            diag = ah32[:, base : base + UQ * step].rearrange("p (i w) -> p i w", w=step)[:, :, 0 : P // 2]
-            nc.vector.tensor_tensor(
-                out=diag,
-                in0=diag,
-                in1=ident_bf[:].bitcast(I32).unsqueeze(1).to_broadcast([P, UQ, P // 2]),
-                op=ALU.bitwise_or,
-            )
+            for q in range(h * UQ, (h + 1) * UQ):
+                block = adj_view(g)[:, q, q * P : (q + 1) * P]
+                nc.gpsimd.affine_select(
+                    out=block,
+                    in_=block,
+                    pattern=[[-1, P]],
+                    compare_op=ALU.not_equal,
+                    fill=1.0,
+                    base=0,
+                    channel_multiplier=1,
+                )
 
         def pair_transpose(words0, words1, g2):
             vt = psum.tile([P, 2, 256], F32, name="vt", tag="vp", bufs=3)
@@ -271,7 +273,9 @@ def tile_gcnconvmodule_t_kernel(tc, inputs, adj, W, b, out):
             dt = small.tile([P, N], BF16, name="dt", bufs=2 * UQ)
             db = st[("db", g)]
             dn = st[("dn", g)][:, q : q + 1]
-            if on_scalar(j):
+            if u == 0 and not on_scalar(j):
+                nc.vector.tensor_scalar(out=dt[:], in0=db[:], scalar1=dn, scalar2=None, op0=ALU.mult)
+            elif on_scalar(j):
                 nc.scalar.activation(out=dt[:], in_=db[:], func=ACT.Copy, scale=dn)
             else:
                 nc.gpsimd.tensor_scalar(
@@ -298,37 +302,58 @@ def tile_gcnconvmodule_t_kernel(tc, inputs, adj, W, b, out):
             st[("ntw", u)] = ntw
             st[("nts", u)] = nts
 
-        def agg_matmul(u, c):
+        def agg_matmul(u, d):
             hw = st[("hw", u // 2)]
             hs = st[("hs", u // 2)]
-            acc = psum.tile([P, DOUT], F32, name="acc", tag="ap", bufs=3)
-            st[("acc", u, c)] = acc
-            for lo, hi in ((0, 256), (256, 384)):
+            acc = psum.tile([P, 4, P], F32, name="acc", tag="ap", bufs=2)
+            st[("acc", u, d)] = acc
+            for c in range(4):
                 for g2 in range(2):
+                    n0 = g2 * 512 + c * P
+                    d0 = g2 * DOUT + d * P
                     nc.tensor.matmul_mx(
-                        out=acc[:, lo:hi],
-                        lhsT=st[("ntw", u)][:, g2 * 512 + c * P : g2 * 512 + (c + 1) * P].bitcast(FP8X4),
-                        lhsT_scale=st[("nts", u)][:, g2 * 512 + c * P : g2 * 512 + (c + 1) * P],
-                        rhs=hw[:, g2 * DOUT + lo : g2 * DOUT + hi].bitcast(FP8X4),
-                        rhs_scale=hs[:, g2 * DOUT + lo : g2 * DOUT + hi],
+                        out=acc[:, c, :],
+                        lhsT=st[("ntw", u)][:, n0 : n0 + P].bitcast(FP8X4),
+                        lhsT_scale=st[("nts", u)][:, n0 : n0 + P],
+                        rhs=hw[:, d0 : d0 + P].bitcast(FP8X4),
+                        rhs_scale=hs[:, d0 : d0 + P],
                         start=(g2 == 0),
                         stop=(g2 == 1),
                     )
 
-        def agg_bias(u, c):
-            if c == 0:
+        def agg_bias(u, d):
+            if d == 0:
                 st[("ot", u)] = work.tile([P, 4, DOUT], F32, name="ot", bufs=3)
-            nc.vector.tensor_tensor(out=st[("ot", u)][:, c, :], in0=st[("acc", u, c)][:], in1=bias[:], op=ALU.add)
-
-        def finish(u, c0, c1):
-            ot = st[("ot", u)]
-            nc.scalar.activation(out=ot[:, c0:c1, :], in_=ot[:, c0:c1, :], func=ACT.Tanh)
-            row = (u % 2) * 512
-            nc.sync.dma_start(
-                out=out[u // 2, row + c0 * P : row + c1 * P, :].rearrange("(c p) d -> p c d", p=P),
-                in_=ot[:, c0:c1, :],
+            nc.vector.tensor_tensor(
+                out=st[("ot", u)][:, :, d * P : (d + 1) * P],
+                in0=st[("acc", u, d)][:],
+                in1=bias[:, d * P : (d + 1) * P].unsqueeze(1).to_broadcast([P, 4, P]),
+                op=ALU.add,
             )
 
+        def finish(u):
+            ot = st[("ot", u)]
+            nc.scalar.activation(out=ot[:], in_=ot[:], func=ACT.Tanh)
+            row = (u % 2) * 512
+            nc.sync.dma_start(out=out[u // 2, row : row + 512, :].rearrange("(c p) d -> p c d", p=P), in_=ot[:])
+
+        def last_block(u, d):
+            if d == 0:
+                st["ol"] = work.tile([P, 3, 4, P], F32, name="ol", tag="xg", align_bytes=64)
+            ot = st["ol"][:, d]
+            nc.vector.tensor_tensor(
+                out=ot,
+                in0=st[("acc", u, d)][:],
+                in1=bias[:, d * P : (d + 1) * P].unsqueeze(1).to_broadcast([P, 4, P]),
+                op=ALU.add,
+            )
+            nc.scalar.activation(out=ot, in_=ot, func=ACT.Tanh)
+            row = (u % 2) * 512
+            nc.sync.dma_start(
+                out=out[u // 2, row : row + 512, d * P : (d + 1) * P].rearrange("(c p) d -> p c d", p=P), in_=ot
+            )
+
+        BIAS_AT = 5
         LOOK = 3
 
         def graph(g):
@@ -350,6 +375,26 @@ def tile_gcnconvmodule_t_kernel(tc, inputs, adj, W, b, out):
         def mask_calls(g, h):
             return [(mask_fill, g, h, i) for i in range(4)], [(mask, g, h, i) for i in range(4)]
 
+        def plan(k):
+            fills = []
+            reads = []
+            g, h = (k + 4) // 2, k % 2
+            order = ((0, 0), (0, 1), (1, 0), (0, 2), (1, 1), (0, 3), (1, 2), (1, 3))
+            if k == 0:
+                f11, r11 = mask_calls(1, 1)
+                for i in range(4):
+                    fills += [(norm_fill, 0, i), f11[i]]
+                    reads += [(norm, 0, i), r11[i]]
+                order = order[0:2] + order[3:4] + order[5:6]
+            for kind, i in order:
+                if kind == 0 and graph(g):
+                    fills.append((mask_fill, g, h, i))
+                    reads.append((mask, g, h, i))
+                if kind == 1 and unit(k):
+                    fills.append((norm_fill, k, i))
+                    reads.append((norm, k, i))
+            return fills, reads
+
         diagonal(0, 0)
         f00, r00 = mask_calls(0, 0)
         f01, r01 = mask_calls(0, 1)
@@ -359,105 +404,112 @@ def tile_gcnconvmodule_t_kernel(tc, inputs, adj, W, b, out):
             r00 + r01,
             {
                 0: [(diagonal, 0, 1)],
-                3: [(dinv_part, 0, 0)],
-                5: [(dinv_rows, 0, 0)],
-                6: [(x_transpose, 0, 0), (x_transpose, 0, 1)],
-                7: [(dinv_part, 0, 1), (x_transpose, 0, 2), (dinv_rows, 0, 1), (x_transpose, 0, 3)],
+                4: [(dinv_part, 0, 0), (x_transpose, 0, 0), (x_transpose, 0, 1)],
+                5: [(dinv_rows, 0, 0), (x_transpose, 0, 2), (diagonal, 1, 0)],
+                7: [(dinv_part, 0, 1), (x_transpose, 0, 3), (dinv_rows, 0, 1)],
             },
         )
         load_x(2)
+        for h in range(2):
+            load_adj(3, h)
         w_quantise()
-        diagonal(1, 0)
         f10, r10 = mask_calls(1, 0)
         run(f10[0:LOOK])
         dinv_columns(0, 0)
         dinv_columns(0, 1)
-        x_quantise(0)
-        release_gpsimd(0)
-        run([(outer_row, 0, j) for j in range(UQ)])
         diagonal(1, 1)
-        stream(f10, r10, {1: [(h_matmul, 0, i) for i in range(2)]})
-        f11, r11 = mask_calls(1, 1)
-        run(f11[0:LOOK])
-        stream(f11, r11, {0: [(h_matmul, 0, i) for i in range(2, 6)], 3: [(dinv_part, 1, 0), (dinv_rows, 1, 0)]})
-        run([(x_transpose, 1, i) for i in range(4)])
-        for h in range(2):
-            load_adj(3, h)
-        load_x(3)
-        h_quantise(0)
-        x_quantise(1)
-        nc.vector.tensor_copy(out=bias[:], in_=b_bf[:])
-        diagonal(2, 0)
+        stream(f10, r10, {})
+        run([(outer_row, 0, j) for j in range(UQ)])
+        run(plan(0)[0][0:LOOK])
 
         for k in range(UNITS + 1):
-            if k % 2 == 1 and (k + 7) // 2 < B:
-                g = (k + 7) // 2
-                load_x(g)
-                load_adj(g, 0)
-                load_adj(g, 1)
-            fills = []
-            reads = []
-            for i in range(4):
-                if graph((k + 4) // 2):
-                    fills.append((mask_fill, (k + 4) // 2, k % 2, i))
-                    reads.append((mask, (k + 4) // 2, k % 2, i))
-                if unit(k):
-                    fills.append((norm_fill, k, i))
-                    reads.append((norm, k, i))
-            between = {}
-            if k % 2 == 0:
-                if graph((k + 2) // 2):
-                    g = (k + 2) // 2
-                    between[0] = [(h_matmul, g, 0), (h_matmul, g, 1)]
-                    for i in range(2, 6):
-                        between[i] = [(h_matmul, g, i)]
-                    between[6] = [(dinv_columns, g, 0)]
-                    between[7] = [(dinv_columns, g, 1)]
-            elif graph((k + 5) // 2):
-                g = (k + 5) // 2
-                between = {0: [(x_transpose, g, 0), (x_transpose, g, 1)], 2: [(x_transpose, g, 2)], 4: [(x_transpose, g, 3)]}
+            fills, reads = plan(k)
             n = len(reads)
-            if n == 4:
-                between = {i: between.get(2 * i, []) + between.get(2 * i + 1, []) for i in range(4)}
-            run(fills[0:LOOK])
-            if unit(k - 2):
-                finish(k - 2, 0, 4)
-            if unit(k + 1):
-                outer_row(k + 1, 0)
-            dinv = ((k + 3) // 2, (k + 1) % 2)
-            if graph(dinv[0]):
-                dinv_part(*dinv)
-            if unit(k + 1):
-                outer_row(k + 1, 2)
-            if unit(k - 1):
-                norm_quantise(k - 1)
-                for c in range(3):
-                    agg_matmul(k - 1, c)
-            if graph(dinv[0]):
-                dinv_rows(*dinv)
-            if graph((k + 5) // 2):
-                diagonal((k + 5) // 2, (k + 1) % 2)
+            even = k % 2 == 0
+
+            def load():
+                if even and (k + 6) // 2 < B:
+                    load_x((k + 6) // 2)
+                if even and (k + 8) // 2 < B:
+                    load_adj((k + 8) // 2, 0)
+                    load_adj((k + 8) // 2, 1)
+
+            if k > 0:
+                load()
+            between = {}
+
+            def after(i, *calls):
+                between[i * n // 8] = between.get(i * n // 8, []) + list(calls)
+
             if k == 0:
-                run([(x_transpose, 2, i) for i in range(4)])
-                x_quantise(2)
-            elif k % 2 == 0 and graph((k + 4) // 2):
-                x_quantise((k + 4) // 2)
-            if k % 2 == 1 and graph((k + 1) // 2):
-                h_quantise((k + 1) // 2)
-            if unit(k + 1):
+                between = {
+                    1: [(x_quantise, 0)],
+                    2: [(h_matmul, 0, 0), (h_matmul, 0, 1), (diagonal, 2, 0), (diagonal, 2, 1)],
+                    3: [(h_matmul, 0, 2), (h_matmul, 0, 3)],
+                    4: [(x_transpose, 1, 0), (dinv_part, 1, 0)],
+                    5: [(h_matmul, 0, 4), (h_matmul, 0, 5)],
+                    6: [(x_transpose, 1, 1), (dinv_rows, 1, 0)],
+                    7: [(x_transpose, 1, 2)],
+                    8: [(x_transpose, 1, 3), (dinv_part, 1, 1), (release_gpsimd, 1)]
+                    + [(outer_row, 1, j) for j in range(UQ)],
+                    9: [(h_quantise, 0)],
+                    10: [(dinv_rows, 1, 1)],
+                }
+            elif even and n > 0:
+                if graph((k + 2) // 2):
+                    after(2, (h_matmul, (k + 2) // 2, 0), (h_matmul, (k + 2) // 2, 1))
+                after(6, (h_quantise, k // 2))
+            if not even and graph((k + 3) // 2):
+                for i in range(4):
+                    after((2, 4, 6, 7)[i], (x_transpose, (k + 3) // 2, i))
+            if k == 1:
+                run([(dinv_columns, 1, 0), (dinv_columns, 1, 1)])
+                after(1, (h_matmul, 1, 2), (h_matmul, 1, 3))
+            if k > 0 and graph((k + 3) // 2):
+                after(1, (dinv_rows, (k + 3) // 2, (k + 1) % 2))
+            if even and k > 0 and graph((k + 2) // 2):
+                after(6, (dinv_columns, (k + 2) // 2, 0))
+                after(7, (dinv_columns, (k + 2) // 2, 1))
+            if k > 0 and unit(k + 1):
                 release_gpsimd(k + 1)
-                outer_row(k + 1, 1)
-                outer_row(k + 1, 3)
-            biases = [(agg_bias, k - 1, c) for c in range(4)] if unit(k - 1) else []
-            if biases:
-                biases.insert(1, (agg_matmul, k - 1, 3))
-            if n > 0:
-                between.setdefault(n // 2 - 1, []).extend(biases[0:2])
-                stream(fills, reads, between)
-                run(biases[2:])
-            else:
-                for c in range(4):
-                    agg_bias(k - 1, c)
-                    if c == 0:
-                        agg_matmul(k - 1, 3)
-                    finish(k - 1, c, c + 1)
+                run([(outer_row, k + 1, j) for j in range(UQ)])
+            if unit(k - 1) and n > 0:
+                between[0] = [(agg_bias, k - 1, 0)] + between.get(0, [])
+                between[1] = [(agg_bias, k - 1, 1), (agg_matmul, k - 1, 2)] + between.get(1, [])
+                last = BIAS_AT * n // 8
+                between[last] = between.get(last, []) + [(agg_bias, k - 1, 2)]
+            if k == 1:
+                diagonal(3, 0)
+            if k > 0 and graph((k + 6) // 2):
+                diagonal((k + 6) // 2, k % 2)
+            stream(fills, reads, between)
+            if unit(k - 1) and n > 0:
+                finish(k - 1)
+            if n == 0:
+                last_block(k - 1, 0)
+                agg_matmul(k - 1, 2)
+                last_block(k - 1, 1)
+                last_block(k - 1, 2)
+            if k == 0:
+                load()
+            if k == 0:
+                x_quantise(1)
+            if unit(k + 1):
+                run(plan(k + 1)[0][0:LOOK])
+            if unit(k):
+                norm_quantise(k)
+            if k == 0:
+                run([(h_matmul, 1, 0), (h_matmul, 1, 1)])
+            elif even and graph((k + 2) // 2):
+                run([(h_matmul, (k + 2) // 2, i) for i in (2, 3)])
+            elif not even and graph((k + 1) // 2):
+                run([(h_matmul, (k + 1) // 2, i) for i in (4, 5)])
+            if unit(k):
+                agg_matmul(k, 0)
+                agg_matmul(k, 1)
+            if graph((k + 4) // 2):
+                dinv_part((k + 4) // 2, k % 2)
+            if not even and graph((k + 3) // 2):
+                x_quantise((k + 3) // 2)
+            if k == 0:
+                nc.vector.tensor_copy(out=bias[:], in_=b_bf[:])

@@ -49,14 +49,14 @@ def tile_gcnconvmodule_t_kernel(tc, inputs, adj, W, b, out):
         st = {}
 
         def adj_view(g):
-            return st[("ah", g)][:].rearrange("p (q m) -> p q m", m=N)
+            return st[("ah", g)][:, 0 : Q * N].rearrange("p (q m) -> p q m", m=N)
 
         def adj_words(g):
-            return st[("ah", g)][:].bitcast(F32).rearrange("p (q w) -> p q w", w=N // 2)
+            return st[("ah", g)][:].bitcast(F32)[:, 0 : Q * N // 2].rearrange("p (q w) -> p q w", w=N // 2)
 
         def load_adj(g, half, pieces=1):
             if half == 0:
-                st[("ah", g)] = adjp.tile([P, Q * N], BF16, name="ah")
+                st[("ah", g)] = adjp.tile([P, Q * (N + P)], BF16, name="ah")
             rows = adj[g].rearrange("(q p) m -> p q m", p=P)
             step = UQ // pieces
             for lo in range(half * UQ, (half + 1) * UQ, step):
@@ -166,17 +166,16 @@ def tile_gcnconvmodule_t_kernel(tc, inputs, adj, W, b, out):
             st[("hs", g)] = hs
 
         def diagonal(g, h):
-            for q in range(h * UQ, (h + 1) * UQ):
-                block = adj_view(g)[:, q, q * P : (q + 1) * P]
-                nc.gpsimd.affine_select(
-                    out=block,
-                    in_=block,
-                    pattern=[[-1, P]],
-                    compare_op=ALU.not_equal,
-                    fill=1.0,
-                    base=0,
-                    channel_multiplier=1,
-                )
+            ah32 = st[("ah", g)][:].bitcast(I32)
+            step = (N + P) // 2
+            base = h * UQ * step
+            diag = ah32[:, base : base + UQ * step].rearrange("p (i w) -> p i w", w=step)[:, :, 0 : P // 2]
+            nc.vector.tensor_tensor(
+                out=diag,
+                in0=diag,
+                in1=ident_bf[:].bitcast(I32).unsqueeze(1).to_broadcast([P, UQ, P // 2]),
+                op=ALU.bitwise_or,
+            )
 
         def pair_transpose(words0, words1, g2):
             vt = psum.tile([P, 2, 256], F32, name="vt", tag="vp", bufs=3)
@@ -478,11 +477,11 @@ def tile_gcnconvmodule_t_kernel(tc, inputs, adj, W, b, out):
                 between[1] = [(agg_bias, k - 1, 1), (agg_matmul, k - 1, 2)] + between.get(1, [])
                 last = BIAS_AT * n // 8
                 between[last] = between.get(last, []) + [(agg_bias, k - 1, 2)]
+            stream(fills, reads, between)
             if k == 1:
                 diagonal(3, 0)
             if k > 0 and graph((k + 6) // 2):
                 diagonal((k + 6) // 2, k % 2)
-            stream(fills, reads, between)
             if unit(k - 1) and n > 0:
                 finish(k - 1)
             if n == 0:

@@ -23,6 +23,7 @@ DOUT = 384
 Q = N // P
 UQ = Q // 2
 UNITS = 2 * B
+THIN = 32
 
 
 def quantise(nc, flat, codes, scales, widths):
@@ -78,7 +79,7 @@ def tile_gcnconvmodule_t_kernel(tc, inputs, adj, W, b, out):
         make_identity(nc, ident_bf[:])
         ident_f = const.tile([P, P], F32, name="ident_f")
         make_identity(nc, ident_f[:])
-        ones = const.tile([P, 1], BF16, name="ones")
+        ones = const.tile([P, THIN], BF16, name="ones")
         nc.vector.memset(ones[:], 1.0)
         fold = const.tile([P, 32], F32, name="fold")
         nc.vector.tensor_reduce(
@@ -211,19 +212,19 @@ def tile_gcnconvmodule_t_kernel(tc, inputs, adj, W, b, out):
 
         def dinv_part(g, h):
             at = st[("at", g)]
-            partp = psum.tile([P, 16], F32, name="partp", tag="tp")
+            partp = psum.tile([P, 16, THIN], F32, name="partp", tag="tp")
             for b32 in range(16):
                 n0 = h * 512 + b32 * 32
                 for g2 in range(2):
                     nc.tensor.matmul(
-                        out=partp[:, b32 : b32 + 1],
+                        out=partp[:, b32, :],
                         lhsT=at[:, g2, n0 : n0 + 32, :].rearrange("p n t -> p (n t)"),
                         rhs=ones[:],
                         start=(g2 == 0),
                         stop=(g2 == 1),
                     )
             part = small.tile([P, 16], BF16, name="part")
-            nc.scalar.copy(out=part[:], in_=partp[:])
+            nc.scalar.copy(out=part[:], in_=partp[:, :, 0])
             st[("part", g, h)] = part
 
         def dinv_rows(g, h):
@@ -380,11 +381,7 @@ def tile_gcnconvmodule_t_kernel(tc, inputs, adj, W, b, out):
             g, h = (k + 4) // 2, k % 2
             order = ((0, 0), (0, 1), (1, 0), (0, 2), (1, 1), (0, 3), (1, 2), (1, 3))
             if k == 0:
-                f11, r11 = mask_calls(1, 1)
-                for i in range(4):
-                    fills += [(norm_fill, 0, i), f11[i]]
-                    reads += [(norm, 0, i), r11[i]]
-                order = order[0:2] + order[3:4] + order[5:6]
+                order = order[2:3] + order[4:5] + order[6:8] + order[0:2] + order[3:4] + order[5:6]
             for kind, i in order:
                 if kind == 0 and graph(g):
                     fills.append((mask_fill, g, h, i))
@@ -404,7 +401,7 @@ def tile_gcnconvmodule_t_kernel(tc, inputs, adj, W, b, out):
             {
                 0: [(diagonal, 0, 1)],
                 4: [(dinv_part, 0, 0), (x_transpose, 0, 0), (x_transpose, 0, 1)],
-                5: [(dinv_rows, 0, 0), (x_transpose, 0, 2), (diagonal, 1, 0)],
+                5: [(dinv_rows, 0, 0), (x_transpose, 0, 2)],
                 7: [(dinv_part, 0, 1), (x_transpose, 0, 3), (dinv_rows, 0, 1)],
             },
         )
@@ -412,14 +409,25 @@ def tile_gcnconvmodule_t_kernel(tc, inputs, adj, W, b, out):
         for h in range(2):
             load_adj(3, h)
         w_quantise()
+        diagonal(1, 0)
         f10, r10 = mask_calls(1, 0)
+        f11, r11 = mask_calls(1, 1)
         run(f10[0:LOOK])
         dinv_columns(0, 0)
         dinv_columns(0, 1)
-        diagonal(1, 1)
-        stream(f10, r10, {})
-        run([(outer_row, 0, j) for j in range(UQ)])
+        stream(
+            f10 + f11,
+            r10 + r11,
+            {
+                0: [(diagonal, 1, 1)],
+                3: [(outer_row, 0, j) for j in range(UQ)] + [(dinv_part, 1, 0)],
+                5: [(dinv_rows, 1, 0)],
+                7: [(x_quantise, 0), (diagonal, 2, 0)],
+            },
+        )
+        dinv_part(1, 1)
         run(plan(0)[0][0:LOOK])
+        run([(h_matmul, 0, i) for i in range(2)])
 
         for k in range(UNITS + 1):
             fills, reads = plan(k)
@@ -441,19 +449,13 @@ def tile_gcnconvmodule_t_kernel(tc, inputs, adj, W, b, out):
                 between[i * n // 8] = between.get(i * n // 8, []) + list(calls)
 
             if k == 0:
-                between = {
-                    1: [(x_quantise, 0)],
-                    2: [(h_matmul, 0, 0), (h_matmul, 0, 1), (diagonal, 2, 0), (diagonal, 2, 1)],
-                    3: [(h_matmul, 0, 2), (h_matmul, 0, 3)],
-                    4: [(x_transpose, 1, 0), (dinv_part, 1, 0)],
-                    5: [(h_matmul, 0, 4), (h_matmul, 0, 5)],
-                    6: [(x_transpose, 1, 1), (dinv_rows, 1, 0)],
-                    7: [(x_transpose, 1, 2)],
-                    8: [(x_transpose, 1, 3), (dinv_part, 1, 1), (release_gpsimd, 1)]
-                    + [(outer_row, 1, j) for j in range(UQ)],
-                    9: [(h_quantise, 0)],
-                    10: [(dinv_rows, 1, 1)],
-                }
+                after(0, (diagonal, 2, 1))
+                after(0, (h_matmul, 0, 2))
+                after(1, (h_matmul, 0, 3))
+                after(2, (h_matmul, 0, 4), (h_matmul, 0, 5))
+                for i in range(4):
+                    after(3 + i, (x_transpose, 1, i))
+                after(6, (h_quantise, 0))
             elif even and n > 0:
                 if graph((k + 2) // 2):
                     after(2, (h_matmul, (k + 2) // 2, 0), (h_matmul, (k + 2) // 2, 1))
@@ -462,26 +464,27 @@ def tile_gcnconvmodule_t_kernel(tc, inputs, adj, W, b, out):
                 for i in range(4):
                     after((2, 4, 6, 7)[i], (x_transpose, (k + 3) // 2, i))
             if k == 1:
-                run([(dinv_columns, 1, 0), (dinv_columns, 1, 1)])
                 after(1, (h_matmul, 1, 2), (h_matmul, 1, 3))
-            if k > 0 and graph((k + 3) // 2):
+            if graph((k + 3) // 2):
                 after(1, (dinv_rows, (k + 3) // 2, (k + 1) % 2))
-            if even and k > 0 and graph((k + 2) // 2):
+            if even and graph((k + 2) // 2):
                 after(6, (dinv_columns, (k + 2) // 2, 0))
                 after(7, (dinv_columns, (k + 2) // 2, 1))
-            if k > 0 and unit(k + 1):
-                release_gpsimd(k + 1)
-                run([(outer_row, k + 1, j) for j in range(UQ)])
+            outer = [(release_gpsimd, k + 1)] + [(outer_row, k + 1, j) for j in range(UQ)] if unit(k + 1) else []
+            if k == 0:
+                after(5, *outer)
+            else:
+                run(outer)
             if unit(k - 1) and n > 0:
                 between[0] = [(agg_bias, k - 1, 0)] + between.get(0, [])
                 between[1] = [(agg_bias, k - 1, 1), (agg_matmul, k - 1, 2)] + between.get(1, [])
                 last = BIAS_AT * n // 8
                 between[last] = between.get(last, []) + [(agg_bias, k - 1, 2)]
             stream(fills, reads, between)
-            if k == 1:
-                diagonal(3, 0)
-            if k > 0 and graph((k + 6) // 2):
+            if graph((k + 6) // 2):
                 diagonal((k + 6) // 2, k % 2)
+            if k == 0:
+                load()
             if unit(k - 1) and n > 0:
                 finish(k - 1)
             if n == 0:
@@ -489,8 +492,6 @@ def tile_gcnconvmodule_t_kernel(tc, inputs, adj, W, b, out):
                 agg_matmul(k - 1, 2)
                 last_block(k - 1, 1)
                 last_block(k - 1, 2)
-            if k == 0:
-                load()
             if k == 0:
                 x_quantise(1)
             if unit(k + 1):

@@ -23,6 +23,7 @@ DOUT = 384
 Q = N // P
 UQ = Q // 2
 UNITS = 2 * B
+WHO = "SGSG"
 THIN = 32
 
 
@@ -264,8 +265,8 @@ def tile_gcnconvmodule_t_kernel(tc, inputs, adj, W, b, out):
             st[("go", u)] = small.tile([P, 1], F32, name="go")
             nc.vector.memset(st[("go", u)][:], 0.0)
 
-        def on_scalar(j):
-            return j % 2 == 0
+        def by(u, j):
+            return "SVSV"[j] if u == 0 else WHO[j]
 
         def outer_row(u, j):
             g = u // 2
@@ -273,10 +274,10 @@ def tile_gcnconvmodule_t_kernel(tc, inputs, adj, W, b, out):
             dt = small.tile([P, N], BF16, name="dt", bufs=2 * UQ)
             db = st[("db", g)]
             dn = st[("dn", g)][:, q : q + 1]
-            if u == 0 and not on_scalar(j):
-                nc.vector.tensor_scalar(out=dt[:], in0=db[:], scalar1=dn, scalar2=None, op0=ALU.mult)
-            elif on_scalar(j):
+            if by(u, j) == "S":
                 nc.scalar.activation(out=dt[:], in_=db[:], func=ACT.Copy, scale=dn)
+            elif by(u, j) == "V":
+                nc.vector.tensor_scalar(out=dt[:], in0=db[:], scalar1=dn, scalar2=None, op0=ALU.mult)
             else:
                 nc.gpsimd.tensor_scalar(
                     out=dt[:], in0=db[:], scalar1=dn, scalar2=st[("go", u)][:, 0:1], op0=ALU.mult, op1=ALU.add
@@ -353,6 +354,13 @@ def tile_gcnconvmodule_t_kernel(tc, inputs, adj, W, b, out):
                 out=out[u // 2, row : row + 512, d * P : (d + 1) * P].rearrange("(c p) d -> p c d", p=P), in_=ot
             )
 
+        def warm(n):
+            wp = psum.tile([P, 512], F32, name="wp", tag="tp")
+            nc.tensor.matmul(out=wp[:, 0:n], lhsT=ident_bf[:], rhs=spread[:, 0:n], start=True, stop=True)
+
+        HJ, PART, ROWS, DB = 5, 1, 3, 6
+        WARM_E, WARM_O = (), ()
+        BIAS0, BIAS1, BIAS2 = 2, 4, 5
         BIAS_AT = 5
         LOOK = 3
 
@@ -395,38 +403,32 @@ def tile_gcnconvmodule_t_kernel(tc, inputs, adj, W, b, out):
         f00, r00 = mask_calls(0, 0)
         f01, r01 = mask_calls(0, 1)
         run(f00[0:LOOK])
-        stream(
-            f00 + f01,
-            r00 + r01,
-            {
-                0: [(diagonal, 0, 1)],
-                4: [(dinv_part, 0, 0), (x_transpose, 0, 0), (x_transpose, 0, 1)],
-                5: [(dinv_rows, 0, 0), (x_transpose, 0, 2)],
-                7: [(dinv_part, 0, 1), (x_transpose, 0, 3), (dinv_rows, 0, 1)],
-            },
-        )
-        load_x(2)
-        for h in range(2):
-            load_adj(3, h)
+        stream(f00 + f01, r00 + r01, {0: [(diagonal, 0, 1)], 4: [(dinv_part, 0, 0)], 7: [(dinv_rows, 0, 0)]})
         w_quantise()
         diagonal(1, 0)
         f10, r10 = mask_calls(1, 0)
         f11, r11 = mask_calls(1, 1)
         run(f10[0:LOOK])
-        dinv_columns(0, 0)
-        dinv_columns(0, 1)
+        dinv_part(0, 1)
+        run([(x_transpose, 0, i) for i in range(2)])
+        dinv_rows(0, 1)
         stream(
             f10 + f11,
             r10 + r11,
             {
-                0: [(diagonal, 1, 1)],
-                3: [(outer_row, 0, j) for j in range(UQ)] + [(dinv_part, 1, 0)],
-                5: [(dinv_rows, 1, 0)],
-                7: [(x_quantise, 0), (diagonal, 2, 0)],
+                0: [(diagonal, 1, 1), (x_transpose, 0, 2)],
+                1: [(x_transpose, 0, 3)],
+                2: [(dinv_columns, 0, 0), (dinv_columns, 0, 1)],
+                4: [(outer_row, 0, j) for j in range(UQ)] + [(dinv_part, 1, 0)],
+                6: [(dinv_rows, 1, 0)],
+                7: [(diagonal, 2, 0)],
             },
         )
-        dinv_part(1, 1)
+        load_x(2)
+        for h in range(2):
+            load_adj(3, h)
         run(plan(0)[0][0:LOOK])
+        x_quantise(0)
         run([(h_matmul, 0, i) for i in range(2)])
 
         for k in range(UNITS + 1):
@@ -458,7 +460,7 @@ def tile_gcnconvmodule_t_kernel(tc, inputs, adj, W, b, out):
                 after(6, (h_quantise, 0))
             elif even and n > 0:
                 if graph((k + 2) // 2):
-                    after(2, (h_matmul, (k + 2) // 2, 0), (h_matmul, (k + 2) // 2, 1))
+                    after(HJ, (h_matmul, (k + 2) // 2, 0), (h_matmul, (k + 2) // 2, 1))
                 after(6, (h_quantise, k // 2))
             if not even and graph((k + 3) // 2):
                 for i in range(4):
@@ -466,20 +468,23 @@ def tile_gcnconvmodule_t_kernel(tc, inputs, adj, W, b, out):
             if k == 1:
                 after(1, (h_matmul, 1, 2), (h_matmul, 1, 3))
             if graph((k + 3) // 2):
-                after(1, (dinv_rows, (k + 3) // 2, (k + 1) % 2))
+                after(PART, (dinv_part, (k + 3) // 2, (k + 1) % 2))
+                after(ROWS, (dinv_rows, (k + 3) // 2, (k + 1) % 2))
             if even and graph((k + 2) // 2):
-                after(6, (dinv_columns, (k + 2) // 2, 0))
-                after(7, (dinv_columns, (k + 2) // 2, 1))
+                after(DB, (dinv_columns, (k + 2) // 2, 0))
+                after(min(7, DB + 1), (dinv_columns, (k + 2) // 2, 1))
             outer = [(release_gpsimd, k + 1)] + [(outer_row, k + 1, j) for j in range(UQ)] if unit(k + 1) else []
             if k == 0:
-                after(5, *outer)
+                after(1, *[call for call in outer if call[0] is release_gpsimd or by(1, call[2]) != "S"])
+                after(6, *[call for call in outer if call[0] is not release_gpsimd and by(1, call[2]) == "S"])
             else:
                 run(outer)
+            for i in (WARM_E if even else WARM_O) if k > 0 and n > 0 else ():
+                after(i, (warm, 512))
             if unit(k - 1) and n > 0:
-                between[0] = [(agg_bias, k - 1, 0)] + between.get(0, [])
-                between[1] = [(agg_bias, k - 1, 1), (agg_matmul, k - 1, 2)] + between.get(1, [])
-                last = BIAS_AT * n // 8
-                between[last] = between.get(last, []) + [(agg_bias, k - 1, 2)]
+                for i, call in ((BIAS0, (agg_bias, 0)), (BIAS1, (agg_bias, 1)), (BIAS0, (agg_matmul, 2)), (BIAS2, (agg_bias, 2))):
+                    i = i * n // 8
+                    between[i] = between.get(i, []) + [(call[0], k - 1, call[1])]
             stream(fills, reads, between)
             if graph((k + 6) // 2):
                 diagonal((k + 6) // 2, k % 2)
@@ -507,8 +512,6 @@ def tile_gcnconvmodule_t_kernel(tc, inputs, adj, W, b, out):
             if unit(k):
                 agg_matmul(k, 0)
                 agg_matmul(k, 1)
-            if graph((k + 4) // 2):
-                dinv_part((k + 4) // 2, k % 2)
             if not even and graph((k + 3) // 2):
                 x_quantise((k + 3) // 2)
             if k == 0:

@@ -23,6 +23,7 @@ DOUT = 384
 Q = N // P
 UQ = Q // 2
 UNITS = 2 * B
+AGG = (((0, 1), 0, 256), ((2, 3), 0, 256), ((0, 1, 2, 3), 256, 384))
 WHO = "SGSG"
 THIN = 32
 
@@ -303,34 +304,39 @@ def tile_gcnconvmodule_t_kernel(tc, inputs, adj, W, b, out):
             st[("ntw", u)] = ntw
             st[("nts", u)] = nts
 
-        def agg_matmul(u, d):
+        def agg_matmul(u, i):
             hw = st[("hw", u // 2)]
             hs = st[("hs", u // 2)]
-            acc = psum.tile([P, 4, P], F32, name="acc", tag="ap", bufs=2)
-            st[("acc", u, d)] = acc
-            for c in range(4):
+            rows, lo, hi = AGG[i]
+            acc = psum.tile([P, len(rows), hi - lo], F32, name="acc", tag="ap", bufs=2)
+            st[("acc", u, i)] = acc
+            for j, c in enumerate(rows):
                 for g2 in range(2):
                     n0 = g2 * 512 + c * P
-                    d0 = g2 * DOUT + d * P
                     nc.tensor.matmul_mx(
-                        out=acc[:, c, :],
+                        out=acc[:, j, :],
                         lhsT=st[("ntw", u)][:, n0 : n0 + P].bitcast(FP8X4),
                         lhsT_scale=st[("nts", u)][:, n0 : n0 + P],
-                        rhs=hw[:, d0 : d0 + P].bitcast(FP8X4),
-                        rhs_scale=hs[:, d0 : d0 + P],
+                        rhs=hw[:, g2 * DOUT + lo : g2 * DOUT + hi].bitcast(FP8X4),
+                        rhs_scale=hs[:, g2 * DOUT + lo : g2 * DOUT + hi],
                         start=(g2 == 0),
                         stop=(g2 == 1),
                     )
 
-        def agg_bias(u, d):
-            if d == 0:
-                st[("ot", u)] = work.tile([P, 4, DOUT], F32, name="ot", bufs=3)
+        def add_bias(ot, u, i):
+            rows, lo, hi = AGG[i]
             nc.vector.tensor_tensor(
-                out=st[("ot", u)][:, :, d * P : (d + 1) * P],
-                in0=st[("acc", u, d)][:],
-                in1=bias[:, d * P : (d + 1) * P].unsqueeze(1).to_broadcast([P, 4, P]),
+                out=ot,
+                in0=st[("acc", u, i)][:],
+                in1=bias[:, lo:hi].unsqueeze(1).to_broadcast([P, len(rows), hi - lo]),
                 op=ALU.add,
             )
+
+        def agg_bias(u, i):
+            if i == 0:
+                st[("ot", u)] = work.tile([P, 4, DOUT], F32, name="ot", bufs=3)
+            rows, lo, hi = AGG[i]
+            add_bias(st[("ot", u)][:, rows[0] : rows[-1] + 1, lo:hi], u, i)
 
         def finish(u):
             ot = st[("ot", u)]
@@ -338,27 +344,24 @@ def tile_gcnconvmodule_t_kernel(tc, inputs, adj, W, b, out):
             row = (u % 2) * 512
             nc.sync.dma_start(out=out[u // 2, row : row + 512, :].rearrange("(c p) d -> p c d", p=P), in_=ot[:])
 
-        def last_block(u, d):
-            if d == 0:
-                st["ol"] = work.tile([P, 3, 4, P], F32, name="ol", tag="xg", align_bytes=64)
-            ot = st["ol"][:, d]
-            nc.vector.tensor_tensor(
-                out=ot,
-                in0=st[("acc", u, d)][:],
-                in1=bias[:, d * P : (d + 1) * P].unsqueeze(1).to_broadcast([P, 4, P]),
-                op=ALU.add,
-            )
+        def last_block(u, i):
+            if i == 0:
+                st["ol"] = work.tile([P, 3, 512], F32, name="ol", tag="xg", align_bytes=64)
+            rows, lo, hi = AGG[i]
+            ot = st["ol"][:, i].rearrange("p (c d) -> p c d", c=len(rows))
+            add_bias(ot, u, i)
             nc.scalar.activation(out=ot, in_=ot, func=ACT.Tanh)
-            row = (u % 2) * 512
+            row = (u % 2) * 512 + rows[0] * P
             nc.sync.dma_start(
-                out=out[u // 2, row : row + 512, d * P : (d + 1) * P].rearrange("(c p) d -> p c d", p=P), in_=ot
+                out=out[u // 2, row : row + len(rows) * P, lo:hi].rearrange("(c p) d -> p c d", p=P), in_=ot
             )
 
         def warm(n):
             wp = psum.tile([P, 512], F32, name="wp", tag="tp")
             nc.tensor.matmul(out=wp[:, 0:n], lhsT=ident_bf[:], rhs=spread[:, 0:n], start=True, stop=True)
 
-        HJ, PART, ROWS, DB = 5, 1, 3, 6
+        AGG2E, AGG2O = 2, 2
+        HJ, PART, ROWS, DB = 5, 1, 3, 7
         WARM_E, WARM_O = (), ()
         BIAS0, BIAS1, BIAS2 = 2, 4, 5
         BIAS_AT = 5
@@ -403,23 +406,23 @@ def tile_gcnconvmodule_t_kernel(tc, inputs, adj, W, b, out):
         f00, r00 = mask_calls(0, 0)
         f01, r01 = mask_calls(0, 1)
         run(f00[0:LOOK])
-        stream(f00 + f01, r00 + r01, {0: [(diagonal, 0, 1)], 4: [(dinv_part, 0, 0)], 7: [(dinv_rows, 0, 0)]})
+        stream(f00 + f01, r00 + r01, {0: [(diagonal, 0, 1)], 4: [(dinv_part, 0, 0)], 7: [(dinv_part, 0, 1), (dinv_rows, 0, 0), (dinv_rows, 0, 1)]})
         w_quantise()
         diagonal(1, 0)
         f10, r10 = mask_calls(1, 0)
         f11, r11 = mask_calls(1, 1)
         run(f10[0:LOOK])
-        dinv_part(0, 1)
+        dinv_columns(0, 0)
+        dinv_columns(0, 1)
         run([(x_transpose, 0, i) for i in range(2)])
-        dinv_rows(0, 1)
         stream(
             f10 + f11,
             r10 + r11,
             {
                 0: [(diagonal, 1, 1), (x_transpose, 0, 2)],
                 1: [(x_transpose, 0, 3)],
-                2: [(dinv_columns, 0, 0), (dinv_columns, 0, 1)],
-                4: [(outer_row, 0, j) for j in range(UQ)] + [(dinv_part, 1, 0)],
+                3: [(outer_row, 0, j) for j in range(UQ)],
+                4: [(dinv_part, 1, 0)],
                 6: [(dinv_rows, 1, 0)],
                 7: [(diagonal, 2, 0)],
             },
@@ -482,7 +485,7 @@ def tile_gcnconvmodule_t_kernel(tc, inputs, adj, W, b, out):
             for i in (WARM_E if even else WARM_O) if k > 0 and n > 0 else ():
                 after(i, (warm, 512))
             if unit(k - 1) and n > 0:
-                for i, call in ((BIAS0, (agg_bias, 0)), (BIAS1, (agg_bias, 1)), (BIAS0, (agg_matmul, 2)), (BIAS2, (agg_bias, 2))):
+                for i, call in ((BIAS0, (agg_bias, 0)), (BIAS1, (agg_bias, 1)), (AGG2E if even else AGG2O, (agg_matmul, 2)), (BIAS2, (agg_bias, 2))):
                     i = i * n // 8
                     between[i] = between.get(i, []) + [(call[0], k - 1, call[1])]
             stream(fills, reads, between)

@@ -168,15 +168,14 @@ def tile_gcnconvmodule_t_kernel(tc, inputs, adj, W, b, out):
             st[("hw", g)] = hw
             st[("hs", g)] = hs
 
-        def diagonal(g, h):
-            ah32 = st[("ah", g)][:].bitcast(I32)
+        def diagonal(g, lo, hi):
             step = (N + P) // 2
-            base = h * UQ * step
-            diag = ah32[:, base : base + UQ * step].rearrange("p (i w) -> p i w", w=step)[:, :, 0 : P // 2]
+            words = st[("ah", g)][:].bitcast(I32).rearrange("p (q w) -> p q w", w=step)
+            block = words[:, lo:hi, 0 : P // 2]
             nc.vector.tensor_tensor(
-                out=diag,
-                in0=diag,
-                in1=ident_bf[:].bitcast(I32).unsqueeze(1).to_broadcast([P, UQ, P // 2]),
+                out=block,
+                in0=block,
+                in1=ident_bf[:].bitcast(I32).unsqueeze(1).to_broadcast([P, hi - lo, P // 2]),
                 op=ALU.bitwise_or,
             )
 
@@ -212,10 +211,12 @@ def tile_gcnconvmodule_t_kernel(tc, inputs, adj, W, b, out):
                 op0=ALU.not_equal,
             )
 
-        def dinv_part(g, h):
+        def dinv_part(g, h, lo=0, hi=16):
             at = st[("at", g)]
-            partp = psum.tile([P, 16, THIN], F32, name="partp", tag="tp")
-            for b32 in range(16):
+            if lo == 0:
+                st["partp"] = psum.tile([P, 16, THIN], F32, name="partp", tag="tp")
+            partp = st["partp"]
+            for b32 in range(lo, hi):
                 n0 = h * 512 + b32 * 32
                 for g2 in range(2):
                     nc.tensor.matmul(
@@ -225,6 +226,8 @@ def tile_gcnconvmodule_t_kernel(tc, inputs, adj, W, b, out):
                         start=(g2 == 0),
                         stop=(g2 == 1),
                     )
+            if hi < 16:
+                return
             part = small.tile([P, 16], BF16, name="part")
             nc.scalar.copy(out=part[:], in_=partp[:, :, 0])
             st[("part", g, h)] = part
@@ -294,15 +297,15 @@ def tile_gcnconvmodule_t_kernel(tc, inputs, adj, W, b, out):
             at = at_view(u // 2, u % 2, i)
             nc.vector.tensor_tensor(out=at, in0=st[("nv", u, i)], in1=at, op=ALU.mult)
 
-        def norm_quantise(u):
-            ntw = work.tile([P, 2 * 512], U32, name="ntw", align_bytes=64)
-            nts = work.tile([P, 2 * 512], U8, name="nts", align_bytes=64)
-            lo = (u % 2) * 512
+        def norm_quantise(u, c0=0, c1=UQ):
+            if c0 == 0:
+                st[("ntw", u)] = work.tile([P, 2 * 512], U32, name="ntw", align_bytes=64)
+                st[("nts", u)] = work.tile([P, 2 * 512], U8, name="nts", align_bytes=64)
+            n0 = (u % 2) * 512
             for g2 in range(2):
-                flat = st[("at", u // 2)][:, g2, lo : lo + 512, :].rearrange("p n t -> p (n t)")
-                quantise(nc, flat, ntw[:, g2 * 512 : (g2 + 1) * 512], nts[:, g2 * 512 : (g2 + 1) * 512], [2048])
-            st[("ntw", u)] = ntw
-            st[("nts", u)] = nts
+                flat = st[("at", u // 2)][:, g2, n0 + c0 * P : n0 + c1 * P, :].rearrange("p n t -> p (n t)")
+                words = slice(g2 * 512 + c0 * P, g2 * 512 + c1 * P)
+                quantise(nc, flat, st[("ntw", u)][:, words], st[("nts", u)][:, words], [(c1 - c0) * P * 4])
 
         def agg_matmul(u, i):
             hw = st[("hw", u // 2)]
@@ -361,6 +364,8 @@ def tile_gcnconvmodule_t_kernel(tc, inputs, adj, W, b, out):
             nc.tensor.matmul(out=wp[:, 0:n], lhsT=ident_bf[:], rhs=spread[:, 0:n], start=True, stop=True)
 
         AGG2E, AGG2O = 2, 2
+        XT = (2, 4, 6, 7)
+        ODD = (5, 5, 7, 8)
         HJ, PART, ROWS, DB = 5, 1, 3, 7
         WARM_E, WARM_O = (), ()
         BIAS0, BIAS1, BIAS2 = 2, 4, 5
@@ -402,13 +407,24 @@ def tile_gcnconvmodule_t_kernel(tc, inputs, adj, W, b, out):
                     reads.append((norm, k, i))
             return fills, reads
 
-        diagonal(0, 0)
         f00, r00 = mask_calls(0, 0)
         f01, r01 = mask_calls(0, 1)
-        run(f00[0:LOOK])
-        stream(f00 + f01, r00 + r01, {0: [(diagonal, 0, 1)], 4: [(dinv_part, 0, 0)], 7: [(dinv_part, 0, 1), (dinv_rows, 0, 0), (dinv_rows, 0, 1)]})
+        diagonal(0, 0, 2)
+        run(f00[0:2])
+        diagonal(0, 2, 4)
+        run(f00[2:LOOK])
+        stream(
+            f00 + f01,
+            r00 + r01,
+            {
+                0: [(diagonal, 0, 4, 6)],
+                2: [(diagonal, 0, 6, 8)],
+                4: [(dinv_part, 0, 0)],
+                7: [(dinv_part, 0, 1), (dinv_rows, 0, 0), (dinv_rows, 0, 1)],
+            },
+        )
         w_quantise()
-        diagonal(1, 0)
+        diagonal(1, 0, 4)
         f10, r10 = mask_calls(1, 0)
         f11, r11 = mask_calls(1, 1)
         run(f10[0:LOOK])
@@ -419,12 +435,12 @@ def tile_gcnconvmodule_t_kernel(tc, inputs, adj, W, b, out):
             f10 + f11,
             r10 + r11,
             {
-                0: [(diagonal, 1, 1), (x_transpose, 0, 2)],
+                0: [(diagonal, 1, 4, 8), (x_transpose, 0, 2)],
                 1: [(x_transpose, 0, 3)],
                 3: [(outer_row, 0, j) for j in range(UQ)],
                 4: [(dinv_part, 1, 0)],
                 6: [(dinv_rows, 1, 0)],
-                7: [(diagonal, 2, 0)],
+                7: [(diagonal, 2, 0, 4)],
             },
         )
         load_x(2)
@@ -454,7 +470,7 @@ def tile_gcnconvmodule_t_kernel(tc, inputs, adj, W, b, out):
                 between[i * n // 8] = between.get(i * n // 8, []) + list(calls)
 
             if k == 0:
-                after(0, (diagonal, 2, 1))
+                after(0, (diagonal, 2, 4, 8))
                 after(0, (h_matmul, 0, 2))
                 after(1, (h_matmul, 0, 3))
                 after(2, (h_matmul, 0, 4), (h_matmul, 0, 5))
@@ -467,12 +483,17 @@ def tile_gcnconvmodule_t_kernel(tc, inputs, adj, W, b, out):
                 after(6, (h_quantise, k // 2))
             if not even and graph((k + 3) // 2):
                 for i in range(4):
-                    after((2, 4, 6, 7)[i], (x_transpose, (k + 3) // 2, i))
+                    after(XT[i], (x_transpose, (k + 3) // 2, i))
             if k == 1:
                 after(1, (h_matmul, 1, 2), (h_matmul, 1, 3))
             if graph((k + 3) // 2):
-                after(PART, (dinv_part, (k + 3) // 2, (k + 1) % 2))
-                after(ROWS, (dinv_rows, (k + 3) // 2, (k + 1) % 2))
+                if even:
+                    after(PART, (dinv_part, (k + 3) // 2, (k + 1) % 2))
+                    after(ROWS, (dinv_rows, (k + 3) // 2, (k + 1) % 2))
+                else:
+                    after(ODD[0], (dinv_part, (k + 3) // 2, 0, 0, ODD[3]))
+                    after(ODD[1], (dinv_part, (k + 3) // 2, 0, ODD[3], 16))
+                    after(ODD[2], (dinv_rows, (k + 3) // 2, 0))
             if even and graph((k + 2) // 2):
                 after(DB, (dinv_columns, (k + 2) // 2, 0))
                 after(min(7, DB + 1), (dinv_columns, (k + 2) // 2, 1))
@@ -488,15 +509,17 @@ def tile_gcnconvmodule_t_kernel(tc, inputs, adj, W, b, out):
                 for i, call in ((BIAS0, (agg_bias, 0)), (BIAS1, (agg_bias, 1)), (AGG2E if even else AGG2O, (agg_matmul, 2)), (BIAS2, (agg_bias, 2))):
                     i = i * n // 8
                     between[i] = between.get(i, []) + [(call[0], k - 1, call[1])]
+            if k == UNITS - 1:
+                between[1] = between[1] + [(norm_quantise, k, 0, 2)]
+                between[2] = between[2] + [(agg_matmul, k, 0)]
             stream(fills, reads, between)
             if graph((k + 6) // 2):
-                diagonal((k + 6) // 2, k % 2)
+                diagonal((k + 6) // 2, k % 2 * UQ, (k % 2 + 1) * UQ)
             if k == 0:
                 load()
             if unit(k - 1) and n > 0:
                 finish(k - 1)
             if n == 0:
-                last_block(k - 1, 0)
                 agg_matmul(k - 1, 2)
                 last_block(k - 1, 1)
                 last_block(k - 1, 2)
@@ -505,7 +528,9 @@ def tile_gcnconvmodule_t_kernel(tc, inputs, adj, W, b, out):
             if unit(k + 1):
                 run(plan(k + 1)[0][0:LOOK])
             if unit(k):
-                norm_quantise(k)
+                norm_quantise(k, 2 if k == UNITS - 1 else 0)
+                if k == UNITS - 1:
+                    last_block(k, 0)
             if k == 0:
                 run([(h_matmul, 1, 0), (h_matmul, 1, 1)])
             elif even and graph((k + 2) // 2):
@@ -513,7 +538,8 @@ def tile_gcnconvmodule_t_kernel(tc, inputs, adj, W, b, out):
             elif not even and graph((k + 1) // 2):
                 run([(h_matmul, (k + 1) // 2, i) for i in (4, 5)])
             if unit(k):
-                agg_matmul(k, 0)
+                if k < UNITS - 1:
+                    agg_matmul(k, 0)
                 agg_matmul(k, 1)
             if not even and graph((k + 3) // 2):
                 x_quantise((k + 3) // 2)

@@ -179,15 +179,18 @@ def tile_gcnconvmodule_t_kernel(tc, inputs, adj, W, b, out):
                 op=ALU.bitwise_or,
             )
 
-        def pair_transpose(words0, words1, g2):
-            vt = psum.tile([P, 2, 256], F32, name="vt", tag="vp", bufs=3)
+        def bf16_view(vt):
+            return vt[:].rearrange("p u n -> p (u n)").bitcast(BF16).rearrange("p (u n e) -> p n u e", u=2, e=2)
+
+        def pair_transpose(words0, words1, g2, tag, bufs):
+            vt = psum.tile([P, 2, 256], F32, name="vt", tag=tag, bufs=bufs)
             for u in range(2):
                 for j, words in enumerate((words0, words1)):
                     lo = g2 * 256 + u * P
                     nc.tensor.transpose(
                         out=vt[:, u, j * P : (j + 1) * P], in_=words[:, lo : lo + P], identity=ident_f[:]
                     )
-            return vt[:].rearrange("p u n -> p (u n)").bitcast(BF16).rearrange("p (u n e) -> p n u e", u=2, e=2)
+            return vt
 
         def at_view(g, h, i):
             pair, g2 = divmod(i, 2)
@@ -198,7 +201,7 @@ def tile_gcnconvmodule_t_kernel(tc, inputs, adj, W, b, out):
             pair, g2 = divmod(i, 2)
             words = adj_words(g)
             q = h * UQ + 2 * pair
-            st[("mv", g, h, i)] = pair_transpose(words[:, q, :], words[:, q + 1, :], g2)
+            st[("mv", g, h, i)] = bf16_view(pair_transpose(words[:, q, :], words[:, q + 1, :], g2, "vp", 3))
 
         def mask(g, h, i):
             if h == 0 and i == 0:
@@ -210,6 +213,20 @@ def tile_gcnconvmodule_t_kernel(tc, inputs, adj, W, b, out):
                 scalar2=None,
                 op0=ALU.not_equal,
             )
+
+        def mask_evacuate(g, h, i):
+            pair, g2 = divmod(i, 2)
+            words = adj_words(g)
+            q = h * UQ + 2 * pair
+            vt = pair_transpose(words[:, q, :], words[:, q + 1, :], g2, "tp", 3)
+            at = st[("at", g)][:].rearrange("p g n t -> p (g n t)").bitcast(F32).rearrange("p (g n u) -> p g n u", g=2, u=2)
+            n0 = h * 512 + pair * 256
+            nc.scalar.copy(out=at[:, g2, n0 : n0 + 256, :], in_=vt[:].rearrange("p u n -> p n u"))
+
+        def mask_late(g, h):
+            n0 = h * 512 + 256
+            at = st[("at", g)][:, 1, n0 : n0 + 256, :].rearrange("p n t -> p (n t)")
+            nc.vector.tensor_scalar(out=at, in0=at, scalar1=0.0, scalar2=None, op0=ALU.not_equal)
 
         def dinv_part(g, h, lo=0, hi=16):
             at = st[("at", g)]
@@ -291,7 +308,7 @@ def tile_gcnconvmodule_t_kernel(tc, inputs, adj, W, b, out):
         def norm_fill(u, i):
             pair, g2 = divmod(i, 2)
             words = [st[("dt", u, 2 * pair + j)][:].bitcast(F32) for j in range(2)]
-            st[("nv", u, i)] = pair_transpose(words[0], words[1], g2)
+            st[("nv", u, i)] = bf16_view(pair_transpose(words[0], words[1], g2, "vp", 3))
 
         def norm(u, i):
             at = at_view(u // 2, u % 2, i)
@@ -366,7 +383,8 @@ def tile_gcnconvmodule_t_kernel(tc, inputs, adj, W, b, out):
         AGG2E, AGG2O = 2, 2
         XT = (2, 4, 6, 7)
         ODD = (5, 5, 7, 8)
-        HJ, PART, ROWS, DB = 5, 1, 3, 7
+        SE0, SEP = 3, (0, 1)
+        HJ, PART, ROWS, DB = 5, 0, 3, 7
         WARM_E, WARM_O = (), ()
         BIAS0, BIAS1, BIAS2 = 2, 4, 5
         BIAS_AT = 5
@@ -399,7 +417,7 @@ def tile_gcnconvmodule_t_kernel(tc, inputs, adj, W, b, out):
             if k == 0:
                 order = order[2:3] + order[4:5] + order[6:8] + order[0:2] + order[3:4] + order[5:6]
             for kind, i in order:
-                if kind == 0 and graph(g):
+                if kind == 0 and graph(g) and (i < 3 or k == 0 or k % 2 not in SEP):
                     fills.append((mask_fill, g, h, i))
                     reads.append((mask, g, h, i))
                 if kind == 1 and unit(k):
@@ -505,14 +523,19 @@ def tile_gcnconvmodule_t_kernel(tc, inputs, adj, W, b, out):
                 run(outer)
             for i in (WARM_E if even else WARM_O) if k > 0 and n > 0 else ():
                 after(i, (warm, 512))
+            if k > 0 and graph((k + 4) // 2) and k % 2 in SEP:
+                after(SE0, (mask_evacuate, (k + 4) // 2, k % 2, 3))
             if unit(k - 1) and n > 0:
                 for i, call in ((BIAS0, (agg_bias, 0)), (BIAS1, (agg_bias, 1)), (AGG2E if even else AGG2O, (agg_matmul, 2)), (BIAS2, (agg_bias, 2))):
                     i = i * n // 8
                     between[i] = between.get(i, []) + [(call[0], k - 1, call[1])]
+            late = k > 0 and graph((k + 4) // 2) and k % 2 in SEP
             if k == UNITS - 1:
                 between[1] = between[1] + [(norm_quantise, k, 0, 2)]
                 between[2] = between[2] + [(agg_matmul, k, 0)]
             stream(fills, reads, between)
+            if late:
+                mask_late((k + 4) // 2, k % 2)
             if graph((k + 6) // 2):
                 diagonal((k + 6) // 2, k % 2 * UQ, (k % 2 + 1) * UQ)
             if k == 0:

from contextlib import ExitStack

import concourse.mybir as mybir
from concourse.masks import make_identity

FLOPS = 2 * 8 * 1024 * 512 * 384 + 2 * 8 * 1024 * 1024 * 384

BF16 = mybir.dt.bfloat16
F32 = mybir.dt.float32
I32 = mybir.dt.int32
U32 = mybir.dt.uint32
U8 = mybir.dt.uint8
FP8X4 = mybir.dt.float8_e4m3fn_x4
ALU = mybir.AluOpType
ACT = mybir.ActivationFunctionType
AX = mybir.AxisListType

P = 128
B = 8
N = 1024
DIN = 512
DOUT = 384
Q = N // P
UQ = Q // 2
UNITS = 2 * B
AGG = (((0, 1), 0, 256), ((2, 3), 0, 256), ((0, 1, 2, 3), 256, 384))
WHO = "SGSG"
THIN = 32


def quantise(nc, flat, codes, scales, widths):
    col = 0
    for width in widths:
        nc.vector.quantize_mx(
            out=codes[:, col // 4 : (col + width) // 4].bitcast(FP8X4),
            scales=scales[:, col // 4 : (col + width) // 4],
            in_=flat[:, col : col + width],
        )
        col += width


def tile_gcnconvmodule_t_kernel(tc, inputs, adj, W, b, out):
    nc = tc.nc
    with ExitStack() as ctx:
        const = ctx.enter_context(tc.tile_pool(name="const", bufs=1))
        adjp = ctx.enter_context(tc.tile_pool(name="adjp", bufs=3))
        work = ctx.enter_context(tc.tile_pool(name="work", bufs=2))
        small = ctx.enter_context(tc.tile_pool(name="small", bufs=3))
        psum = ctx.enter_context(tc.psum_pool(name="psum", bufs=3))
        ctx.enter_context(tc.manual_schedule())

        st = {}

        def adj_view(g):
            return st[("ah", g)][:, 0 : Q * N].rearrange("p (q m) -> p q m", m=N)

        def adj_words(g):
            return st[("ah", g)][:].bitcast(F32)[:, 0 : Q * N // 2].rearrange("p (q w) -> p q w", w=N // 2)

        def load_adj(g, half, pieces=1):
            if half == 0:
                st[("ah", g)] = adjp.tile([P, Q * (N + P)], BF16, name="ah")
            rows = adj[g].rearrange("(q p) m -> p q m", p=P)
            step = UQ // pieces
            for lo in range(half * UQ, (half + 1) * UQ, step):
                nc.sync.dma_start(out=adj_view(g)[:, lo : lo + step, :], in_=rows[:, lo : lo + step, :])

        def load_x(g):
            xt = work.tile([P, 8, DIN], BF16, name="xt")
            st[("xt", g)] = xt
            nc.sync.dma_start(
                out=xt[:].rearrange("p (a e) k -> p a (e k)", e=2),
                in_=inputs[g].rearrange("(a p e) k -> p a (e k)", p=P, e=2),
            )

        load_adj(0, 0, 2)
        load_adj(0, 1, 2)
        load_x(0)

        ident_bf = const.tile([P, P], BF16, name="ident_bf")
        make_identity(nc, ident_bf[:])
        ident_f = const.tile([P, P], F32, name="ident_f")
        make_identity(nc, ident_f[:])
        ones = const.tile([P, THIN], BF16, name="ones")
        nc.vector.memset(ones[:], 1.0)
        fold = const.tile([P, 32], F32, name="fold")
        nc.vector.tensor_reduce(
            out=fold[:], in_=ident_f[:].rearrange("p (j t) -> p j t", t=4), axis=AX.X, op=ALU.add
        )
        spread = const.tile([P, 4 * (P + 32)], BF16, name="spread")
        nc.vector.memset(spread[:], 0.0)
        nc.vector.tensor_copy(
            out=spread[:].rearrange("p (i w) -> p i w", w=P + 32)[:, :, 0:32],
            in_=fold[:].unsqueeze(1).to_broadcast([P, 4, 32]),
        )
        mhalf = const.tile([P, UQ], F32, name="mhalf")
        nc.vector.memset(mhalf[:], -0.5)

        w_raw = work.tile([P, 4, DOUT], BF16, name="w_raw", tag="ot", bufs=3)
        nc.sync.dma_start(
            out=w_raw[:].rearrange("p (u e) d -> p u (e d)", u=2),
            in_=W.rearrange("(u p e) d -> p u (e d)", u=2, e=2),
        )
        b_bf = const.tile([P, DOUT], BF16, name="b_bf")
        load_adj(1, 0)
        load_adj(1, 1)
        load_x(1)
        nc.sync.dma_start(out=b_bf[:], in_=b.partition_broadcast(P))
        load_adj(2, 0)
        load_adj(2, 1)
        bias = const.tile([P, DOUT], F32, name="bias")
        w_codes = const.tile([P, DOUT], U32, name="w_codes", align_bytes=64)
        w_scales = const.tile([P, DOUT], U8, name="w_scales", align_bytes=64)

        def w_quantise():
            w_grp = work.tile([P, DOUT, 4], BF16, name="w_grp", align_bytes=64, bufs=1)
            nc.vector.tensor_copy(out=w_grp[:], in_=w_raw[:].rearrange("p t d -> p d t"))
            quantise(nc, w_grp[:].rearrange("p d t -> p (d t)"), w_codes, w_scales, [1024, 512])

        def x_transpose(g, i):
            if i == 0:
                st[("xg", g)] = work.tile([P, N * 4], BF16, name="xg", align_bytes=64)
            xt32 = st[("xt", g)][:].bitcast(F32)
            xg32 = st[("xg", g)][:].bitcast(F32).rearrange("p (n u) -> p n u", u=2)
            xp = psum.tile([P, 2, 256], F32, name="xp", tag="tp")
            for u in range(2):
                for j in range(2):
                    nc.tensor.transpose(
                        out=xp[:, u, j * P : (j + 1) * P],
                        in_=xt32[:, 2 * i + j, u * P : (u + 1) * P],
                        identity=ident_f[:],
                    )
            nc.scalar.copy(out=xg32[:, i * 256 : (i + 1) * 256, :], in_=xp[:].rearrange("p u n -> p n u"))

        def x_quantise(g):
            xw = work.tile([P, N], U32, name="xw", align_bytes=64)
            xs = work.tile([P, N], U8, name="xs", align_bytes=64)
            quantise(nc, st[("xg", g)], xw, xs, [4096])
            st[("xw", g)] = xw
            st[("xs", g)] = xs

        def h_matmul(g, i):
            g2, dblk = divmod(i, 3)
            if i == 0:
                st[("hq", g)] = work.tile([P, 2, DOUT, 4], BF16, name="hq", align_bytes=64)
            xw = st[("xw", g)]
            xs = st[("xs", g)]
            hp = psum.tile([P, 4, P], F32, name="hp", tag="tp")
            for t in range(4):
                q = 4 * g2 + t
                nc.tensor.matmul_mx(
                    out=hp[:, t, :],
                    lhsT=xw[:, q * P : (q + 1) * P].bitcast(FP8X4),
                    lhsT_scale=xs[:, q * P : (q + 1) * P],
                    rhs=w_codes[:, dblk * P : (dblk + 1) * P].bitcast(FP8X4),
                    rhs_scale=w_scales[:, dblk * P : (dblk + 1) * P],
                    start=True,
                    stop=True,
                )
            nc.scalar.copy(
                out=st[("hq", g)][:, g2, dblk * P : (dblk + 1) * P, :], in_=hp[:].rearrange("p t d -> p d t")
            )

        def h_quantise(g):
            hw = small.tile([P, 2 * DOUT], U32, name="hw", align_bytes=64)
            hs = small.tile([P, 2 * DOUT], U8, name="hs", align_bytes=64)
            quantise(nc, st[("hq", g)][:].rearrange("p g d t -> p (g d t)"), hw, hs, [2048, 1024])
            st[("hw", g)] = hw
            st[("hs", g)] = hs

        def diagonal(g, lo, hi):
            step = (N + P) // 2
            words = st[("ah", g)][:].bitcast(I32).rearrange("p (q w) -> p q w", w=step)
            block = words[:, lo:hi, 0 : P // 2]
            nc.vector.tensor_tensor(
                out=block,
                in0=block,
                in1=ident_bf[:].bitcast(I32).unsqueeze(1).to_broadcast([P, hi - lo, P // 2]),
                op=ALU.bitwise_or,
            )

        def bf16_view(vt):
            return vt[:].rearrange("p u n -> p (u n)").bitcast(BF16).rearrange("p (u n e) -> p n u e", u=2, e=2)

        def pair_transpose(words0, words1, g2, tag, bufs):
            vt = psum.tile([P, 2, 256], F32, name="vt", tag=tag, bufs=bufs)
            for u in range(2):
                for j, words in enumerate((words0, words1)):
                    lo = g2 * 256 + u * P
                    nc.tensor.transpose(
                        out=vt[:, u, j * P : (j + 1) * P], in_=words[:, lo : lo + P], identity=ident_f[:]
                    )
            return vt

        def at_view(g, h, i):
            pair, g2 = divmod(i, 2)
            n0 = h * 512 + pair * 256
            return st[("at", g)][:, g2, n0 : n0 + 256, :].rearrange("p n (u e) -> p n u e", e=2)

        def mask_fill(g, h, i):
            pair, g2 = divmod(i, 2)
            words = adj_words(g)
            q = h * UQ + 2 * pair
            st[("mv", g, h, i)] = bf16_view(pair_transpose(words[:, q, :], words[:, q + 1, :], g2, "vp", 3))

        def mask(g, h, i):
            if h == 0 and i == 0:
                st[("at", g)] = work.tile([P, 2, N, 4], BF16, name="at", align_bytes=64, bufs=3)
            nc.vector.tensor_scalar(
                out=at_view(g, h, i),
                in0=st[("mv", g, h, i)],
                scalar1=0.0,
                scalar2=None,
                op0=ALU.not_equal,
            )

        def mask_evacuate(g, h, i):
            pair, g2 = divmod(i, 2)
            words = adj_words(g)
            q = h * UQ + 2 * pair
            vt = pair_transpose(words[:, q, :], words[:, q + 1, :], g2, "tp", 3)
            at = st[("at", g)][:].rearrange("p g n t -> p (g n t)").bitcast(F32).rearrange("p (g n u) -> p g n u", g=2, u=2)
            n0 = h * 512 + pair * 256
            nc.scalar.copy(out=at[:, g2, n0 : n0 + 256, :], in_=vt[:].rearrange("p u n -> p n u"))

        def mask_late(g, h):
            n0 = h * 512 + 256
            at = st[("at", g)][:, 1, n0 : n0 + 256, :].rearrange("p n t -> p (n t)")
            nc.vector.tensor_scalar(out=at, in0=at, scalar1=0.0, scalar2=None, op0=ALU.not_equal)

        def dinv_part(g, h, lo=0, hi=16):
            at = st[("at", g)]
            if lo == 0:
                st["partp"] = psum.tile([P, 16, THIN], F32, name="partp", tag="tp")
            partp = st["partp"]
            for b32 in range(lo, hi):
                n0 = h * 512 + b32 * 32
                for g2 in range(2):
                    nc.tensor.matmul(
                        out=partp[:, b32, :],
                        lhsT=at[:, g2, n0 : n0 + 32, :].rearrange("p n t -> p (n t)"),
                        rhs=ones[:],
                        start=(g2 == 0),
                        stop=(g2 == 1),
                    )
            if hi < 16:
                return
            part = small.tile([P, 16], BF16, name="part")
            nc.scalar.copy(out=part[:], in_=partp[:, :, 0])
            st[("part", g, h)] = part

        def dinv_rows(g, h):
            part = st[("part", g, h)][:].rearrange("p (q i) -> p q i", i=4)
            degp = psum.tile([P, UQ], F32, name="degp", tag="tp")
            for i in range(4):
                nc.tensor.matmul(
                    out=degp[:],
                    lhsT=spread[:, i * P : (i + 1) * P],
                    rhs=part[:, :, i],
                    start=(i == 0),
                    stop=(i == 3),
                )
            deg = small.tile([P, UQ], F32, name="deg")
            nc.scalar.copy(out=deg[:], in_=degp[:])
            if h == 0:
                st[("dn", g)] = small.tile([P, Q], F32, name="dn", bufs=4)
            nc.gpsimd.tensor_tensor(
                out=st[("dn", g)][:, h * UQ : (h + 1) * UQ], in0=deg[:], in1=mhalf[:], op=ALU.pow
            )

        def dinv_columns(g, h):
            if h == 0:
                st[("db", g)] = work.tile([P, N], F32, name="db")
            dn = st[("dn", g)]
            dbp = psum.tile([P, 512], F32, name="dbp", tag="tp")
            for i in range(4):
                q = 4 * h + i
                nc.tensor.transpose(
                    out=dbp[:, i * P : (i + 1) * P],
                    in_=dn[:, q : q + 1].to_broadcast([P, P]),
                    identity=ident_f[:],
                )
            nc.scalar.copy(out=st[("db", g)][:, h * 512 : (h + 1) * 512], in_=dbp[:])

        def release_gpsimd(u):
            st[("go", u)] = small.tile([P, 1], F32, name="go")
            nc.vector.memset(st[("go", u)][:], 0.0)

        def by(u, j):
            return "SVSV"[j] if u == 0 else WHO[j]

        def outer_row(u, j):
            g = u // 2
            q = (u % 2) * UQ + j
            dt = small.tile([P, N], BF16, name="dt", bufs=2 * UQ)
            db = st[("db", g)]
            dn = st[("dn", g)][:, q : q + 1]
            if by(u, j) == "S":
                nc.scalar.activation(out=dt[:], in_=db[:], func=ACT.Copy, scale=dn)
            elif by(u, j) == "V":
                nc.vector.tensor_scalar(out=dt[:], in0=db[:], scalar1=dn, scalar2=None, op0=ALU.mult)
            else:
                nc.gpsimd.tensor_scalar(
                    out=dt[:], in0=db[:], scalar1=dn, scalar2=st[("go", u)][:, 0:1], op0=ALU.mult, op1=ALU.add
                )
            st[("dt", u, j)] = dt

        def norm_fill(u, i):
            pair, g2 = divmod(i, 2)
            words = [st[("dt", u, 2 * pair + j)][:].bitcast(F32) for j in range(2)]
            st[("nv", u, i)] = bf16_view(pair_transpose(words[0], words[1], g2, "vp", 3))

        def norm(u, i):
            at = at_view(u // 2, u % 2, i)
            nc.vector.tensor_tensor(out=at, in0=st[("nv", u, i)], in1=at, op=ALU.mult)

        def norm_quantise(u, c0=0, c1=UQ):
            if c0 == 0:
                st[("ntw", u)] = work.tile([P, 2 * 512], U32, name="ntw", align_bytes=64)
                st[("nts", u)] = work.tile([P, 2 * 512], U8, name="nts", align_bytes=64)
            n0 = (u % 2) * 512
            for g2 in range(2):
                flat = st[("at", u // 2)][:, g2, n0 + c0 * P : n0 + c1 * P, :].rearrange("p n t -> p (n t)")
                words = slice(g2 * 512 + c0 * P, g2 * 512 + c1 * P)
                quantise(nc, flat, st[("ntw", u)][:, words], st[("nts", u)][:, words], [(c1 - c0) * P * 4])

        def agg_matmul(u, i):
            hw = st[("hw", u // 2)]
            hs = st[("hs", u // 2)]
            rows, lo, hi = AGG[i]
            acc = psum.tile([P, len(rows), hi - lo], F32, name="acc", tag="ap", bufs=2)
            st[("acc", u, i)] = acc
            for j, c in enumerate(rows):
                for g2 in range(2):
                    n0 = g2 * 512 + c * P
                    nc.tensor.matmul_mx(
                        out=acc[:, j, :],
                        lhsT=st[("ntw", u)][:, n0 : n0 + P].bitcast(FP8X4),
                        lhsT_scale=st[("nts", u)][:, n0 : n0 + P],
                        rhs=hw[:, g2 * DOUT + lo : g2 * DOUT + hi].bitcast(FP8X4),
                        rhs_scale=hs[:, g2 * DOUT + lo : g2 * DOUT + hi],
                        start=(g2 == 0),
                        stop=(g2 == 1),
                    )

        def add_bias(ot, u, i):
            rows, lo, hi = AGG[i]
            nc.vector.tensor_tensor(
                out=ot,
                in0=st[("acc", u, i)][:],
                in1=bias[:, lo:hi].unsqueeze(1).to_broadcast([P, len(rows), hi - lo]),
                op=ALU.add,
            )

        def agg_bias(u, i):
            if i == 0:
                st[("ot", u)] = work.tile([P, 4, DOUT], F32, name="ot", bufs=3)
            rows, lo, hi = AGG[i]
            add_bias(st[("ot", u)][:, rows[0] : rows[-1] + 1, lo:hi], u, i)

        def finish(u):
            ot = st[("ot", u)]
            nc.scalar.activation(out=ot[:], in_=ot[:], func=ACT.Tanh)
            row = (u % 2) * 512
            nc.sync.dma_start(out=out[u // 2, row : row + 512, :].rearrange("(c p) d -> p c d", p=P), in_=ot[:])

        def last_block(u, i):
            if i == 0:
                st["ol"] = work.tile([P, 3, 512], F32, name="ol", tag="xg", align_bytes=64)
            rows, lo, hi = AGG[i]
            ot = st["ol"][:, i].rearrange("p (c d) -> p c d", c=len(rows))
            add_bias(ot, u, i)
            nc.scalar.activation(out=ot, in_=ot, func=ACT.Tanh)
            row = (u % 2) * 512 + rows[0] * P
            nc.sync.dma_start(
                out=out[u // 2, row : row + len(rows) * P, lo:hi].rearrange("(c p) d -> p c d", p=P), in_=ot
            )

        def warm(n):
            wp = psum.tile([P, 512], F32, name="wp", tag="tp")
            nc.tensor.matmul(out=wp[:, 0:n], lhsT=ident_bf[:], rhs=spread[:, 0:n], start=True, stop=True)

        AGG2E, AGG2O = 2, 2
        XT = (2, 4, 6, 7)
        ODD = (5, 5, 7, 8)
        SE0, SEP = 3, (0, 1)
        HJ, PART, ROWS, DB = 5, 0, 3, 7
        WARM_E, WARM_O = (), ()
        BIAS0, BIAS1, BIAS2 = 2, 4, 5
        BIAS_AT = 5
        LOOK = 3

        def graph(g):
            return 0 <= g < B

        def unit(u):
            return 0 <= u < UNITS

        def run(calls):
            for call in calls:
                call[0](*call[1:])

        def stream(fills, reads, between):
            for i in range(len(reads)):
                run([reads[i]])
                run(fills[i + LOOK : i + LOOK + 1])
                run(between.get(i, []))

        def mask_calls(g, h):
            return [(mask_fill, g, h, i) for i in range(4)], [(mask, g, h, i) for i in range(4)]

        def plan(k):
            fills = []
            reads = []
            g, h = (k + 4) // 2, k % 2
            order = ((0, 0), (0, 1), (1, 0), (0, 2), (1, 1), (0, 3), (1, 2), (1, 3))
            if k == 0:
                order = order[2:3] + order[4:5] + order[6:8] + order[0:2] + order[3:4] + order[5:6]
            for kind, i in order:
                if kind == 0 and graph(g) and (i < 3 or k == 0 or k % 2 not in SEP):
                    fills.append((mask_fill, g, h, i))
                    reads.append((mask, g, h, i))
                if kind == 1 and unit(k):
                    fills.append((norm_fill, k, i))
                    reads.append((norm, k, i))
            return fills, reads

        f00, r00 = mask_calls(0, 0)
        f01, r01 = mask_calls(0, 1)
        diagonal(0, 0, 2)
        run(f00[0:2])
        diagonal(0, 2, 4)
        run(f00[2:LOOK])
        stream(
            f00 + f01,
            r00 + r01,
            {
                0: [(diagonal, 0, 4, 6)],
                2: [(diagonal, 0, 6, 8)],
                4: [(dinv_part, 0, 0)],
                7: [(dinv_part, 0, 1), (dinv_rows, 0, 0), (dinv_rows, 0, 1)],
            },
        )
        w_quantise()
        diagonal(1, 0, 4)
        f10, r10 = mask_calls(1, 0)
        f11, r11 = mask_calls(1, 1)
        run(f10[0:LOOK])
        dinv_columns(0, 0)
        dinv_columns(0, 1)
        run([(x_transpose, 0, i) for i in range(2)])
        stream(
            f10 + f11,
            r10 + r11,
            {
                0: [(diagonal, 1, 4, 8), (x_transpose, 0, 2)],
                1: [(x_transpose, 0, 3)],
                3: [(outer_row, 0, j) for j in range(UQ)],
                4: [(dinv_part, 1, 0)],
                6: [(dinv_rows, 1, 0)],
                7: [(diagonal, 2, 0, 4)],
            },
        )
        load_x(2)
        for h in range(2):
            load_adj(3, h)
        run(plan(0)[0][0:LOOK])
        x_quantise(0)
        run([(h_matmul, 0, i) for i in range(2)])

        for k in range(UNITS + 1):
            fills, reads = plan(k)
            n = len(reads)
            even = k % 2 == 0

            def load():
                if even and (k + 6) // 2 < B:
                    load_x((k + 6) // 2)
                if even and (k + 8) // 2 < B:
                    load_adj((k + 8) // 2, 0)
                    load_adj((k + 8) // 2, 1)

            if k > 0:
                load()
            between = {}

            def after(i, *calls):
                between[i * n // 8] = between.get(i * n // 8, []) + list(calls)

            if k == 0:
                after(0, (diagonal, 2, 4, 8))
                after(0, (h_matmul, 0, 2))
                after(1, (h_matmul, 0, 3))
                after(2, (h_matmul, 0, 4), (h_matmul, 0, 5))
                for i in range(4):
                    after(3 + i, (x_transpose, 1, i))
                after(6, (h_quantise, 0))
            elif even and n > 0:
                if graph((k + 2) // 2):
                    after(HJ, (h_matmul, (k + 2) // 2, 0), (h_matmul, (k + 2) // 2, 1))
                after(6, (h_quantise, k // 2))
            if not even and graph((k + 3) // 2):
                for i in range(4):
                    after(XT[i], (x_transpose, (k + 3) // 2, i))
            if k == 1:
                after(1, (h_matmul, 1, 2), (h_matmul, 1, 3))
            if graph((k + 3) // 2):
                if even:
                    after(PART, (dinv_part, (k + 3) // 2, (k + 1) % 2))
                    after(ROWS, (dinv_rows, (k + 3) // 2, (k + 1) % 2))
                else:
                    after(ODD[0], (dinv_part, (k + 3) // 2, 0, 0, ODD[3]))
                    after(ODD[1], (dinv_part, (k + 3) // 2, 0, ODD[3], 16))
                    after(ODD[2], (dinv_rows, (k + 3) // 2, 0))
            if even and graph((k + 2) // 2):
                after(DB, (dinv_columns, (k + 2) // 2, 0))
                after(min(7, DB + 1), (dinv_columns, (k + 2) // 2, 1))
            outer = [(release_gpsimd, k + 1)] + [(outer_row, k + 1, j) for j in range(UQ)] if unit(k + 1) else []
            if k == 0:
                after(1, *[call for call in outer if call[0] is release_gpsimd or by(1, call[2]) != "S"])
                after(6, *[call for call in outer if call[0] is not release_gpsimd and by(1, call[2]) == "S"])
            else:
                run(outer)
            for i in (WARM_E if even else WARM_O) if k > 0 and n > 0 else ():
                after(i, (warm, 512))
            if k > 0 and graph((k + 4) // 2) and k % 2 in SEP:
                after(SE0, (mask_evacuate, (k + 4) // 2, k % 2, 3))
            if unit(k - 1) and n > 0:
                for i, call in ((BIAS0, (agg_bias, 0)), (BIAS1, (agg_bias, 1)), (AGG2E if even else AGG2O, (agg_matmul, 2)), (BIAS2, (agg_bias, 2))):
                    i = i * n // 8
                    between[i] = between.get(i, []) + [(call[0], k - 1, call[1])]
            late = k > 0 and graph((k + 4) // 2) and k % 2 in SEP
            if k == UNITS - 1:
                between[1] = between[1] + [(norm_quantise, k, 0, 2)]
                between[2] = between[2] + [(agg_matmul, k, 0)]
            stream(fills, reads, between)
            if late:
                mask_late((k + 4) // 2, k % 2)
            if graph((k + 6) // 2):
                diagonal((k + 6) // 2, k % 2 * UQ, (k % 2 + 1) * UQ)
            if k == 0:
                load()
            if unit(k - 1) and n > 0:
                finish(k - 1)
            if n == 0:
                agg_matmul(k - 1, 2)
                last_block(k - 1, 1)
                last_block(k - 1, 2)
            if k == 0:
                x_quantise(1)
            if unit(k + 1):
                run(plan(k + 1)[0][0:LOOK])
            if unit(k):
                norm_quantise(k, 2 if k == UNITS - 1 else 0)
                if k == UNITS - 1:
                    last_block(k, 0)
            if k == 0:
                run([(h_matmul, 1, 0), (h_matmul, 1, 1)])
            elif even and graph((k + 2) // 2):
                run([(h_matmul, (k + 2) // 2, i) for i in (2, 3)])
            elif not even and graph((k + 1) // 2):
                run([(h_matmul, (k + 1) // 2, i) for i in (4, 5)])
            if unit(k):
                if k < UNITS - 1:
                    agg_matmul(k, 0)
                agg_matmul(k, 1)
            if not even and graph((k + 3) // 2):
                x_quantise((k + 3) // 2)
            if k == 0:
                nc.vector.tensor_copy(out=bias[:], in_=b_bf[:])
